import numpy as np
import ml_dtypes


def mxq(x, axis, fmt="e4m3"):
    dtype, down = {"e4m3": (ml_dtypes.float8_e4m3fn, 7), "e5m2": (ml_dtypes.float8_e5m2, 14)}[fmt]
    v = np.moveaxis(np.asarray(x, np.float32).astype(ml_dtypes.bfloat16).astype(np.float64), axis, -1)
    blocks = v.reshape(v.shape[:-1] + (-1, 32))
    amax = np.abs(blocks).max(-1, keepdims=True)
    byte = np.maximum(np.where(amax > 0, np.frexp(amax)[1] - 1 + 127, 0) - down, 1)
    scale = np.exp2(byte - 127.0)
    codes = (blocks / scale).astype(np.float32).astype(dtype).astype(np.float64)
    return np.moveaxis((codes * scale).reshape(v.shape), -1, axis)


WIDE = False


def mx_kscale(k):
    if not WIDE:
        return np.ones(k)
    levels = np.array([10, -10, 5, -5, 0])
    if k % 512:
        return np.exp2(np.random.permutation(np.resize(levels, k // 32))).repeat(32)
    a = np.empty((k // 512, 16))
    for p in range(k // 512):
        a[p, :8] = np.random.permutation(np.resize(levels, 8))
        for g in range(8):
            far = levels[np.abs(levels - a[p, g]) >= 10]
            a[p, g + 8] = far[np.random.randint(len(far))]
    return np.exp2(a.ravel()).repeat(32)


BF16 = ml_dtypes.bfloat16


def bf(x):
    return np.asarray(x, np.float32).astype(BF16)


def f64(x):
    return np.asarray(x).astype(np.float64)


N, L, WD, C, O = 128, 64, 512, 512, 512
EPS = 1e-8
CONV_CLAMP = 256.0
ACT_GAIN = np.sqrt(2.0)
LRELU_SLOPE = 0.2
STYLE_WSCALE = 1.0 / np.sqrt(WD)
X_AMP = CONV_CLAMP / 2.0
W_AMP = np.sqrt(EPS)


def draw0():
    s, t = mx_kscale(WD), mx_kscale(C)
    return {"x": bf(np.random.standard_normal((N, L, C)) * X_AMP),
            "w": bf(np.random.standard_normal((N, WD)) * s),
            "weight": bf(np.random.standard_normal((O, C)) * W_AMP / np.sqrt(C) / t[None, :]),
            "style_w": bf(np.random.standard_normal((C, WD)) * t[:, None] / s[None, :]),
            "style_b": bf((1.0 + 0.1 * np.random.standard_normal(C)) * t),
            "bias": bf(np.random.standard_normal(O) * 0.2 * X_AMP)}


def core(x, w, weight, style_w, style_b, bias):
    wt = f64(weight)
    style = (mxq(f64(w), 1, "e4m3") @ mxq(f64(style_w), 1, "e4m3").T) * STYLE_WSCALE + f64(style_b)
    d = mxq(np.square(style), 1, "e4m3") @ mxq(np.square(wt), 1, "e4m3").T
    decoef = 1.0 / np.sqrt(d + EPS)
    x_mod = f64(x) * style[:, None, :]
    y = mxq(x_mod, 2, "e4m3") @ mxq(wt, 1, "e4m3").T
    y = y * decoef[:, None, :]
    y = y + f64(bias)
    y = np.where(y >= 0, y, LRELU_SLOPE * y) * ACT_GAIN
    return np.clip(y, -CONV_CLAMP, CONV_CLAMP)


def e4m3fn_bytes(y):
    return np.clip(np.asarray(y, np.float64), -448.0, 448.0).astype(np.float32).astype(ml_dtypes.float8_e4m3fn).view(np.uint8)


def e4m3fn_values(b):
    return np.asarray(b, np.uint8).view(ml_dtypes.float8_e4m3fn).astype(np.float64)


def setup_inputs():
    d = draw0()
    x0 = np.asarray(d['w']).astype(np.float64)
    s = (np.max(np.abs(x0), axis=(0,), keepdims=True) / 448.0).astype(np.float32)
    out = {}
    for k, v in d.items():
        if k == 'w':
            out['w_bytes'] = e4m3fn_bytes(x0 / s.astype(np.float64))
            out['w_scale'] = s
        else:
            out[k] = v
    return out


def reference(x, w_bytes, w_scale, weight, style_w, style_b, bias):
    return core(x, e4m3fn_values(w_bytes) * w_scale.astype(np.float64), weight, style_w, style_b, bias)

@@ -1,0 +1,386 @@
+import math
+from contextlib import ExitStack
+
+import concourse.mybir as mybir
+from concourse.masks import make_identity
+
+SAMPLES, POINTS, LATENT, C, O = 128, 64, 512, 512, 512
+EPS = 1e-8
+CLAMP = 256.0
+SLOPE = 0.2
+GAIN = math.sqrt(2.0)
+FLOPS = 2 * SAMPLES * POINTS * C * O + 2 * SAMPLES * LATENT * C + 2 * SAMPLES * C * O
+
+F32 = mybir.dt.float32
+BF16 = mybir.dt.bfloat16
+U32 = mybir.dt.uint32
+U8 = mybir.dt.uint8
+FP8 = mybir.dt.float8_e4m3fn
+X4 = mybir.dt.float8_e4m3fn_x4
+ALU = mybir.AluOpType
+ACT = mybir.ActivationFunctionType
+
+P = 128
+PACK = 4
+GROUP_SAMPLES = 4
+TOKENS = GROUP_SAMPLES * POINTS
+J = TOKENS // P
+ROWS = POINTS // J
+GROUPS = SAMPLES // GROUP_SAMPLES
+HALF = SAMPLES // 2
+PRELOADED = 8
+X_TILES = PRELOADED + 2
+
+SUMMED = {(u, 1) for u in range(0, GROUPS - 2, 2)} | {(GROUPS - 3, 1)}
+VECTOR_RELU = {(GROUPS - 3, 0)}
+
+IDENTITY_PRODUCT = (0, PACK - 1)
+IDENTITY_PRODUCT_GROUPS = GROUPS - 2
+
+STEPS = (
+    ("load", PRELOADED),
+    ("back 0", -2),
+    ("modulate 0", 3),
+    ("demodulate 0", 0),
+    ("quantise", 2),
+    ("product 1", 0),
+    ("relu 0", -2),
+    ("demodulate 1", 0),
+    ("clip 0", 0),
+    ("finish 0", -2),
+    ("product 0", 1),
+    ("clip 1", 0),
+    ("back 1", -2),
+    ("steep", 0),
+    ("relu 1", -2),
+    ("modulate 1", 3),
+    ("turn", 4),
+    ("finish 1", -2),
+    ("store", -2),
+)
+FIRST_TURN = -4
+EARLY = {("turn", 0), ("turn", 1), ("modulate 0", 0), ("modulate 0", 1)} | {("load", u) for u in range(PRELOADED)}
+SECOND_HALF = {
+    (-2, "quantise"): "style",
+    (-2, "steep"): "square",
+    (-1, "product 1"): "quantise",
+    (0, "back 1"): "product",
+    (2, "clip 0"): "root",
+    (3, "steep"): "reciprocal",
+}
+
+
+def tile_modulatemlp_pa_kernel(tc, x, w_bytes, w_scale, weight, style_w, style_b, bias, out):
+    nc = tc.nc
+    x_view = x.rearrange("n l c -> (n l) c").rearrange("(g r j) c -> g r (j c)", r=P, j=J)
+    out_view = out.rearrange("n l o -> (n l) o").rearrange("(g r j) o -> g r (j o)", r=P, j=J)
+
+    with ExitStack() as ctx:
+        ctx.enter_context(tc.manual_schedule())
+        keep = ctx.enter_context(tc.tile_pool(name="keep", bufs=1))
+        x_pool = ctx.enter_context(tc.tile_pool(name="x_pool", bufs=X_TILES))
+        work = ctx.enter_context(tc.tile_pool(name="work", bufs=4))
+        xt_ps = ctx.enter_context(tc.psum_pool(name="xt_ps", bufs=2))
+        y_ps = ctx.enter_context(tc.psum_pool(name="y_ps", bufs=3))
+        z_ps = ctx.enter_context(tc.psum_pool(name="z_ps", bufs=3))
+
+        style_w_sb = keep.tile([P, PACK, LATENT], BF16)
+        weight_sb = keep.tile([P, PACK, C], BF16)
+        w_codes = keep.tile([P, LATENT], U8)
+        w_scale_sb = keep.tile([P, PACK], F32)
+        style_b_sb = keep.tile([P, PACK], BF16)
+        bias_sb = keep.tile([P, PACK], BF16)
+        style_w_view = style_w.rearrange("(m t) l -> m t l", t=PACK)
+        nc.sync.dma_start(out=w_codes[:], in_=w_bytes)
+        nc.sync.dma_start(out=style_w_sb[:, 0:2, :], in_=style_w_view[:, 0:2, :])
+        nc.sync.dma_start(out=style_w_sb[:, 2:4, :], in_=style_w_view[:, 2:4, :])
+        nc.scalar.dma_start(out=w_scale_sb[:], in_=w_scale.rearrange("o (p t) -> p (o t)", t=PACK))
+        nc.scalar.dma_start(out=style_b_sb[:], in_=style_b.rearrange("(p t) -> p t", t=PACK))
+        nc.scalar.dma_start(out=bias_sb[:], in_=bias.rearrange("(p t) -> p t", t=PACK))
+        nc.sync.dma_start(out=weight_sb[:], in_=weight.rearrange("(m k) c -> m k c", k=PACK))
+
+        x_tiles = {}
+
+        def load(u):
+            x_sb = x_pool.tile([P, J, C], BF16, name="x_sb")
+            nc.sync.dma_start(out=x_sb[:].rearrange("p j c -> p (j c)"), in_=x_view[u])
+            x_tiles[u] = x_sb
+
+        for u in range(PRELOADED):
+            load(u)
+
+        ident = keep.tile([P, P], F32)
+        make_identity(nc, ident[:])
+        ones = keep.tile([P, 1], F32)
+        nc.vector.memset(ones[:], 1.0)
+        table_out = keep.tile([P, 1], F32)
+        nc.scalar.activation(out=table_out[:], in_=ones[:], func=ACT.Sqrt)
+        zero = keep.tile([P, 512], BF16)
+        nc.vector.memset(zero[:], 0.0)
+        half_eps = keep.tile([P, 1], F32)
+        nc.vector.tensor_scalar(out=half_eps[:], in0=ones[:], scalar1=0.5 * EPS, scalar2=None, op0=ALU.mult)
+
+        style_w_q = keep.tile([P, C], U32, align_bytes=64)
+        style_w_s = keep.tile([P, C], U8, align_bytes=64)
+        w_q = keep.tile([P, SAMPLES], U32, align_bytes=64)
+        w_s = keep.tile([P, SAMPLES], U8, align_bytes=64)
+        weight_q = keep.tile([P, O], U32, align_bytes=64)
+        weight_s = keep.tile([P, O], U8, align_bytes=64)
+        weight2_q = keep.tile([P, O], U32, align_bytes=64)
+        weight2_s = keep.tile([P, O], U8, align_bytes=64)
+        style2_q = keep.tile([P, SAMPLES], U32, align_bytes=64)
+        style2_s = keep.tile([P, SAMPLES], U8, align_bytes=64)
+        style_w_t = keep.tile([P, PACK, P, PACK], BF16, align_bytes=64)
+        w_t = keep.tile([P, SAMPLES, PACK], BF16, align_bytes=64)
+        weight_t = keep.tile([P, PACK, P, PACK], BF16, align_bytes=64)
+        weight2_t = keep.tile([P, O * PACK], BF16, align_bytes=64)
+        style2_t = keep.tile([P, SAMPLES * PACK], BF16, align_bytes=64)
+        weight_flat = weight_t[:].rearrange("p k m c -> p (k m c)")
+        w_bf = keep.tile([P, LATENT], BF16)
+        style = keep.tile([P, SAMPLES, PACK], F32)
+        root = keep.tile([P, PACK, SAMPLES], F32)
+        decoef = keep.tile([P, PACK, SAMPLES], F32)
+        bias_gain = keep.tile([P, PACK], F32)
+
+        def transpose_words(dst, row):
+            words = row.bitcast(F32)
+            for h in range(2):
+                nc.tensor.transpose(dst[:, h, :], words[:, h::2], ident[:])
+
+        def halves(big, h):
+            part = big[:, 2 * h : 2 * h + 2].rearrange("p t m k -> p t (m k)").bitcast(F32)
+            return part.rearrange("p t (m u) -> p t m u", u=2)
+
+        def warm(count):
+            unused = xt_ps.tile([P, J, 2, P], F32, name="xt")
+            for r in range(count):
+                nc.tensor.matmul(out=unused[:].rearrange("p j u r -> p (j u r)"), lhsT=zero[:, :P], rhs=zero[:],
+                                 start=True, stop=True)
+
+        def warm_mx(count):
+            unused = y_ps.tile([P, 2, TOKENS], F32, name="yt")
+            for r in range(count):
+                nc.tensor.matmul_mx(out=unused[:].rearrange("p j u -> p (j u)"), lhsT=style_w_q[:, :P].bitcast(X4),
+                                    lhsT_scale=style_w_s[:, :P], rhs=style_w_q[:].bitcast(X4),
+                                    rhs_scale=style_w_s[:], start=True, stop=True)
+
+        def turn_rows(pool, name, rows, h):
+            turned = pool.tile([P, 2, 2, P], F32, name=name)
+            for k in range(2):
+                transpose_words(turned[:, k], rows[:, 2 * h + k, :])
+            return turned
+
+        def quantise_style_w(h):
+            cols = slice(2 * P * h, 2 * P * (h + 1))
+            nc.vector.quantize_mx(out=style_w_q[:, cols].bitcast(X4), scales=style_w_s[:, cols],
+                                  in_=style_w_t[:, 2 * h : 2 * h + 2].rearrange("p t m k -> p (t m k)"))
+
+        def square_on_scalar(h):
+            cols = slice(h * 2 * P * PACK, (h + 1) * 2 * P * PACK)
+            nc.scalar.activation(out=weight2_t[:, cols], in_=weight_flat[:, cols], func=ACT.Square)
+
+        def square_on_vector(h):
+            cols = slice(h * 2 * P * PACK, (h + 1) * 2 * P * PACK)
+            nc.vector.tensor_tensor(out=weight2_t[:, cols], in0=weight_flat[:, cols], in1=weight_flat[:, cols], op=ALU.mult)
+
+        style_ps = {}
+        d_ps = {}
+
+        def style_product(t):
+            cols = slice(t * P, (t + 1) * P)
+            nc.tensor.matmul_mx(out=style_ps[0][:, t, :], lhsT=style_w_q[:, cols].bitcast(X4), lhsT_scale=style_w_s[:, cols],
+                                rhs=w_q[:].bitcast(X4), rhs_scale=w_s[:], start=True, stop=True)
+
+        def make_style(h):
+            ns = slice(h * HALF, (h + 1) * HALF)
+            nc.vector.scalar_tensor_tensor(
+                out=style[:, ns, :], in0=style_ps[0][:, :, ns].rearrange("p t n -> p n t"), scalar=1.0 / math.sqrt(LATENT),
+                in1=style_b_sb[:].unsqueeze(1).to_broadcast([P, HALF, PACK]), op0=ALU.mult, op1=ALU.add)
+
+        def square_style(h):
+            cols = slice(h * HALF * PACK, (h + 1) * HALF * PACK)
+            nc.scalar.activation(out=style2_t[:, cols], in_=style[:].rearrange("p n t -> p (n t)")[:, cols], func=ACT.Square)
+
+        def quantise_style2(h):
+            ns = slice(h * HALF, (h + 1) * HALF)
+            nc.vector.quantize_mx(out=style2_q[:, ns].bitcast(X4), scales=style2_s[:, ns],
+                                  in_=style2_t[:, h * HALF * PACK : (h + 1) * HALF * PACK])
+
+        def d_product(h):
+            ns = slice(h * HALF, (h + 1) * HALF)
+            d_ps[h] = z_ps.tile([P, PACK, HALF], F32, name="zt")
+            for k in range(PACK):
+                cols = slice(k * P, (k + 1) * P)
+                nc.tensor.matmul_mx(out=d_ps[h][:, k, :], lhsT=weight2_q[:, cols].bitcast(X4), lhsT_scale=weight2_s[:, cols],
+                                    rhs=style2_q[:, ns].bitcast(X4), rhs_scale=style2_s[:, ns], start=True, stop=True)
+
+        def take_root(h):
+            ns = slice(h * HALF, (h + 1) * HALF)
+            nc.scalar.activation(out=root[:, :, ns], in_=d_ps[h][:], func=ACT.Sqrt, scale=0.5, bias=half_eps[:])
+
+        def take_reciprocal(h):
+            ns = slice(h * HALF, (h + 1) * HALF)
+            nc.vector.reciprocal(out=decoef[:, :, ns], in_=root[:, :, ns])
+
+        turned_x, modulated, quantised, products, z, clipped, steep, turned_z, relu, finished = ({} for d in range(10))
+
+        def turn(u):
+            xt = xt_ps.tile([P, J, 2, P], F32, name="xt")
+            x_sb = x_tiles.pop(u)
+            for j in range(J):
+                transpose_words(xt[:, j], x_sb[:, j, :])
+            turned_x[u] = xt
+
+        def modulate(u, j):
+            if j == 0:
+                modulated[u] = work.tile([P, J, P, PACK], BF16, name="xm", align_bytes=64)
+            of_group = style[:, u * GROUP_SAMPLES : (u + 1) * GROUP_SAMPLES, :].rearrange("p n (u e) -> p n u e", e=2)
+            nc.vector.tensor_tensor(
+                out=modulated[u][:, j].rearrange("p (n l) (u e) -> p n l u e", n=GROUP_SAMPLES, e=2),
+                in0=turned_x[u][:, j].bitcast(BF16).rearrange("p u (n l e) -> p n l u e", n=GROUP_SAMPLES, e=2),
+                in1=of_group.unsqueeze(2).to_broadcast([P, GROUP_SAMPLES, ROWS, 2, 2]),
+                op=ALU.mult)
+
+        def quantise(u):
+            codes = work.tile([P, TOKENS], U32, name="xq", align_bytes=64)
+            scales = work.tile([P, TOKENS], U8, name="xs", align_bytes=64)
+            nc.vector.quantize_mx(out=codes[:].bitcast(X4), scales=scales[:],
+                                  in_=modulated.pop(u)[:].rearrange("p j r t -> p (j r t)"))
+            quantised[u] = (codes, scales)
+
+        def product(u, h):
+            codes, scales = quantised[u]
+            yt = y_ps.tile([P, 2, TOKENS], F32, name="yt")
+            for part in range(2):
+                cols = slice((2 * h + part) * P, (2 * h + part + 1) * P)
+                nc.tensor.matmul_mx(out=yt[:, part, :], lhsT=weight_q[:, cols].bitcast(X4), lhsT_scale=weight_s[:, cols],
+                                    rhs=codes[:].bitcast(X4), rhs_scale=scales[:], start=True, stop=True)
+            products[u, h] = yt
+
+        def demodulate(u, h):
+            if h == 0:
+                z[u] = work.tile([P, PACK, TOKENS], F32, name="zr")
+            yt = products.pop((u, h))
+            for part in range(2):
+                k = 2 * h + part
+                for n in range(GROUP_SAMPLES):
+                    sample = u * GROUP_SAMPLES + n
+                    nc.scalar.activation(
+                        out=z[u][:, k, :].rearrange("p (j n l) -> p n j l", j=J, n=GROUP_SAMPLES)[:, n],
+                        in_=yt[:, part, :].rearrange("p (j n l) -> p n j l", j=J, n=GROUP_SAMPLES)[:, n],
+                        func=ACT.Identity, scale=decoef[:, k, sample : sample + 1], bias=bias_gain[:, k : k + 1])
+
+        def clip(u, h):
+            if h == 0:
+                clipped[u] = work.tile([P, PACK, TOKENS], F32, name="zc")
+            ks = slice(2 * h, 2 * h + 2)
+            cols = slice(0, sum((u, j) not in SUMMED for j in range(J)) * P)
+            nc.gpsimd.tensor_scalar(out=clipped[u][:, ks, cols], in0=z[u][:, ks, cols], scalar1=CLAMP,
+                                    scalar2=-CLAMP / SLOPE, op0=ALU.min, op1=ALU.max)
+
+        def make_steep(u):
+            for j in range(J):
+                if (u, j) in SUMMED:
+                    negative = work.tile([P, PACK, P], F32, name="nq")
+                    nc.gpsimd.tensor_scalar(out=negative[:], in0=z[u][:, :, j * P : (j + 1) * P], scalar1=0.0,
+                                            scalar2=-CLAMP / SLOPE, op0=ALU.min, op1=ALU.max)
+                    steep[u, j] = work.tile([P, PACK, P], F32, name="q")
+                    nc.gpsimd.tensor_scalar(out=steep[u, j][:], in0=negative[:], scalar1=-(1.0 - SLOPE), scalar2=1.0,
+                                            op0=ALU.mult, op1=ALU.mult)
+
+        def turn_back(u, j):
+            zt = z_ps.tile([P, PACK, P], F32, name="zt")
+            summed = (u, j) in SUMMED
+            source = z[u] if summed else clipped[u]
+            for k in range(PACK):
+                as_product = (j, k) == IDENTITY_PRODUCT and u < IDENTITY_PRODUCT_GROUPS
+                nc.tensor.matmul(out=zt[:, k, :], lhsT=source[:, k, j * P : (j + 1) * P], rhs=ident[:],
+                                 is_transpose=not as_product, start=True, stop=not summed)
+                if summed:
+                    nc.tensor.matmul(out=zt[:, k, :], lhsT=steep[u, j][:, k, :], rhs=ident[:],
+                                     is_transpose=True, start=False, stop=True)
+            turned_z[u, j] = zt
+
+        def make_relu(u, j):
+            if (u, j) in SUMMED:
+                return
+            relu[u, j] = work.tile([P, P, PACK], F32, name="qn")
+            in_order = turned_z[u, j][:].rearrange("p k m -> p m k")
+            if (u, j) in VECTOR_RELU:
+                nc.vector.tensor_scalar(out=relu[u, j][:], in0=in_order, scalar1=0.0, scalar2=-(1.0 - SLOPE),
+                                        op0=ALU.min, op1=ALU.mult)
+            else:
+                nc.scalar.activation(out=relu[u, j][:], in_=in_order, func=ACT.Relu, scale=-(1.0 - SLOPE))
+
+        def finish(u, j):
+            if j == 0:
+                finished[u] = work.tile([P, J, O], F32, name="ot")
+            row = finished[u][:, j, :].rearrange("p (m k) -> p m k", k=PACK)
+            in_order = turned_z[u, j][:].rearrange("p k m -> p m k")
+            if (u, j) in SUMMED:
+                nc.vector.tensor_scalar(out=row, in0=in_order, scalar1=CLAMP, scalar2=-CLAMP, op0=ALU.min, op1=ALU.max)
+            else:
+                nc.vector.tensor_tensor(out=row, in0=in_order, in1=relu[u, j][:], op=ALU.add)
+
+        def store(u):
+            if u < GROUPS - 1:
+                nc.sync.dma_start(out=out_view[u], in_=finished[u][:].rearrange("p j o -> p (j o)"))
+            else:
+                for j in range(J):
+                    nc.sync.dma_start(out=out_view[u].rearrange("p (j o) -> p j o", j=J)[:, j, :], in_=finished[u][:, j, :])
+
+        warm(6)
+        nc.vector.tensor_copy(out=w_bf[:], in_=w_codes[:].bitcast(FP8))
+        style_w_ps = [turn_rows(y_ps, "yt", style_w_sb, 0)]
+        w_ps = y_ps.tile([P, 2, P], F32, name="yt")
+        transpose_words(w_ps[:], w_bf[:])
+        nc.vector.tensor_tensor(
+            out=w_t[:].rearrange("p n (u e) -> p n u e", e=2),
+            in0=w_ps[:].bitcast(BF16).rearrange("p u (n e) -> p n u e", e=2),
+            in1=w_scale_sb[:].rearrange("p (u e) -> p u e", e=2).unsqueeze(1).to_broadcast([P, SAMPLES, 2, 2]),
+            op=ALU.mult)
+        style_w_ps.append(turn_rows(y_ps, "yt", style_w_sb, 1))
+        for h in range(2):
+            nc.scalar.copy(out=halves(style_w_t, h), in_=style_w_ps[h][:].rearrange("p t u m -> p t m u"))
+        nc.vector.quantize_mx(out=w_q[:].bitcast(X4), scales=w_s[:], in_=w_t[:].rearrange("p n k -> p (n k)"))
+        for h in range(2):
+            quantise_style_w(h)
+        weight_ps = [turn_rows(z_ps, "zt", weight_sb, h) for h in range(2)]
+        style_ps[0] = z_ps.tile([P, PACK, P], F32, name="zt")
+        for t in range(PACK):
+            style_product(t)
+        nc.vector.tensor_copy(out=halves(weight_t, 1), in_=weight_ps[1][:].rearrange("p t u m -> p t m u"))
+        turn(0)
+        nc.vector.tensor_scalar(out=bias_gain[:], in0=bias_sb[:], scalar1=GAIN, scalar2=None, op0=ALU.mult)
+        square_on_vector(1)
+        turn(1)
+        make_style(0)
+        nc.scalar.copy(out=halves(weight_t, 0), in_=weight_ps[0][:].rearrange("p t u m -> p t m u"))
+        square_on_scalar(0)
+        warm_mx(1)
+        square_style(0)
+        nc.vector.quantize_mx(out=weight2_q[:].bitcast(X4), scales=weight2_s[:], in_=weight2_t[:])
+        quantise_style2(0)
+        d_product(0)
+        modulate(0, 0)
+        nc.vector.quantize_mx(out=weight_q[:].bitcast(X4), scales=weight_s[:], in_=weight_flat)
+        modulate(1, 0)
+        take_root(0)
+        take_reciprocal(0)
+        warm_mx(5)
+
+        steps = {"load": load, "turn": turn, "quantise": quantise, "steep": make_steep, "store": store}
+        for name, step in (("modulate", modulate), ("product", product), ("demodulate", demodulate), ("clip", clip),
+                           ("back", turn_back), ("relu", make_relu), ("finish", finish)):
+            for part in range(2):
+                steps["%s %d" % (name, part)] = lambda u, step=step, part=part: step(u, part)
+        second_half = {"style": make_style, "square": square_style, "quantise": quantise_style2, "product": d_product,
+                       "root": take_root, "reciprocal": take_reciprocal}
+
+        for i in range(FIRST_TURN, GROUPS + 2):
+            for name, ahead in STEPS:
+                if (i, name) in SECOND_HALF:
+                    second_half[SECOND_HALF[i, name]](1)
+                u = i + ahead
+                if 0 <= u < GROUPS and (name, u) not in EARLY:
+                    steps[name](u)

@@ -113,10 +113,6 @@ def tile_modulatemlp_pa_kernel(tc, x, w_bytes, w_scale, weight, style_w, style_b
         make_identity(nc, ident[:])
         ones = keep.tile([P, 1], F32)
         nc.vector.memset(ones[:], 1.0)
-        table_out = keep.tile([P, 1], F32)
-        nc.scalar.activation(out=table_out[:], in_=ones[:], func=ACT.Sqrt)
-        zero = keep.tile([P, 512], BF16)
-        nc.vector.memset(zero[:], 0.0)
         half_eps = keep.tile([P, 1], F32)
         nc.vector.tensor_scalar(out=half_eps[:], in0=ones[:], scalar1=0.5 * EPS, scalar2=None, op0=ALU.mult)
 
@@ -150,19 +146,6 @@ def tile_modulatemlp_pa_kernel(tc, x, w_bytes, w_scale, weight, style_w, style_b
         def halves(big, h):
             part = big[:, 2 * h : 2 * h + 2].rearrange("p t m k -> p t (m k)").bitcast(F32)
             return part.rearrange("p t (m u) -> p t m u", u=2)
-
-        def warm(count):
-            unused = xt_ps.tile([P, J, 2, P], F32, name="xt")
-            for r in range(count):
-                nc.tensor.matmul(out=unused[:].rearrange("p j u r -> p (j u r)"), lhsT=zero[:, :P], rhs=zero[:],
-                                 start=True, stop=True)
-
-        def warm_mx(count):
-            unused = y_ps.tile([P, 2, TOKENS], F32, name="yt")
-            for r in range(count):
-                nc.tensor.matmul_mx(out=unused[:].rearrange("p j u -> p (j u)"), lhsT=style_w_q[:, :P].bitcast(X4),
-                                    lhsT_scale=style_w_s[:, :P], rhs=style_w_q[:].bitcast(X4),
-                                    rhs_scale=style_w_s[:], start=True, stop=True)
 
         def turn_rows(pool, name, rows, h):
             turned = pool.tile([P, 2, 2, P], F32, name=name)
@@ -329,7 +312,6 @@ def tile_modulatemlp_pa_kernel(tc, x, w_bytes, w_scale, weight, style_w, style_b
                 for j in range(J):
                     nc.sync.dma_start(out=out_view[u].rearrange("p (j o) -> p j o", j=J)[:, j, :], in_=finished[u][:, j, :])
 
-        warm(6)
         nc.vector.tensor_copy(out=w_bf[:], in_=w_codes[:].bitcast(FP8))
         style_w_ps = [turn_rows(y_ps, "yt", style_w_sb, 0)]
         w_ps = y_ps.tile([P, 2, P], F32, name="yt")
@@ -357,7 +339,6 @@ def tile_modulatemlp_pa_kernel(tc, x, w_bytes, w_scale, weight, style_w, style_b
         make_style(0)
         nc.scalar.copy(out=halves(weight_t, 0), in_=weight_ps[0][:].rearrange("p t u m -> p t m u"))
         square_on_scalar(0)
-        warm_mx(1)
         square_style(0)
         nc.vector.quantize_mx(out=weight2_q[:].bitcast(X4), scales=weight2_s[:], in_=weight2_t[:])
         quantise_style2(0)
@@ -367,7 +348,6 @@ def tile_modulatemlp_pa_kernel(tc, x, w_bytes, w_scale, weight, style_w, style_b
         modulate(1, 0)
         take_root(0)
         take_reciprocal(0)
-        warm_mx(5)
 
         steps = {"load": load, "turn": turn, "quantise": quantise, "steep": make_steep, "store": store}
         for name, step in (("modulate", modulate), ("product", product), ("demodulate", demodulate), ("clip", clip),

@@ -21,90 +21,56 @@ ALU = mybir.AluOpType
 ACT = mybir.ActivationFunctionType
 
 P = 128
+BANK = 512
 PACK = 4
 GROUP_SAMPLES = 4
 TOKENS = GROUP_SAMPLES * POINTS
 J = TOKENS // P
-ROWS = POINTS // J
 GROUPS = SAMPLES // GROUP_SAMPLES
 HALF = SAMPLES // 2
+PLAIN = 6 * P
+VECTOR_ALONE = {(u, 1) for u in range(GROUPS - 4, GROUPS - 2)}
 PRELOADED = 8
-X_TILES = PRELOADED + 2
-
-SUMMED = {(u, 1) for u in range(0, GROUPS - 2, 2)} | {(GROUPS - 3, 1)}
-VECTOR_RELU = {(GROUPS - 3, 0)}
-
-IDENTITY_PRODUCT = (0, PACK - 1)
-IDENTITY_PRODUCT_GROUPS = GROUPS - 2
-
-STEPS = (
-    ("load", PRELOADED),
-    ("back 0", -2),
-    ("modulate 0", 3),
-    ("demodulate 0", 0),
-    ("quantise", 2),
-    ("product 1", 0),
-    ("relu 0", -2),
-    ("demodulate 1", 0),
-    ("clip 0", 0),
-    ("finish 0", -2),
-    ("product 0", 1),
-    ("clip 1", 0),
-    ("back 1", -2),
-    ("steep", 0),
-    ("relu 1", -2),
-    ("modulate 1", 3),
-    ("turn", 4),
-    ("finish 1", -2),
-    ("store", -2),
-)
-FIRST_TURN = -4
-EARLY = {("turn", 0), ("turn", 1), ("modulate 0", 0), ("modulate 0", 1)} | {("load", u) for u in range(PRELOADED)}
-SECOND_HALF = {
-    (-2, "quantise"): "style",
-    (-2, "steep"): "square",
-    (-1, "product 1"): "quantise",
-    (0, "back 1"): "product",
-    (2, "clip 0"): "root",
-    (3, "steep"): "reciprocal",
-}
 
 
 def tile_modulatemlp_pa_kernel(tc, x, w_bytes, w_scale, weight, style_w, style_b, bias, out):
     nc = tc.nc
-    x_view = x.rearrange("n l c -> (n l) c").rearrange("(g r j) c -> g r (j c)", r=P, j=J)
-    out_view = out.rearrange("n l o -> (n l) o").rearrange("(g r j) o -> g r (j o)", r=P, j=J)
+    x_view = x.rearrange("n l c -> (n l) c").rearrange("(g j r) c -> g r j c", r=P, j=J)
+    out_view = out.rearrange("n l o -> (n l) o").rearrange("(g j r) o -> g r j o", r=P, j=J)
 
     with ExitStack() as ctx:
         ctx.enter_context(tc.manual_schedule())
         keep = ctx.enter_context(tc.tile_pool(name="keep", bufs=1))
-        x_pool = ctx.enter_context(tc.tile_pool(name="x_pool", bufs=X_TILES))
-        work = ctx.enter_context(tc.tile_pool(name="work", bufs=4))
-        xt_ps = ctx.enter_context(tc.psum_pool(name="xt_ps", bufs=2))
-        y_ps = ctx.enter_context(tc.psum_pool(name="y_ps", bufs=3))
-        z_ps = ctx.enter_context(tc.psum_pool(name="z_ps", bufs=3))
+        psum = ctx.enter_context(tc.psum_pool(name="psum", bufs=1))
 
-        style_w_sb = keep.tile([P, PACK, LATENT], BF16)
-        weight_sb = keep.tile([P, PACK, C], BF16)
+        def ring(name, count, shape, dtype):
+            return [keep.tile(shape, dtype, name="%s%d" % (name, r), align_bytes=64) for r in range(count)]
+
+        x_banks = [psum.tile([P, BANK], F32, name="x_bank%d" % r) for r in range(2)]
+        y_banks = [psum.tile([P, BANK], F32, name="y_bank%d" % r) for r in range(3)]
+        z_banks = [psum.tile([P, BANK], F32, name="z_bank%d" % r) for r in range(3)]
+
+        style_w_sb = ring("style_w_sb", 2, [P, 2, LATENT], BF16)
+        weight_sb = ring("weight_sb", 2, [P, 2, C], BF16)
         w_codes = keep.tile([P, LATENT], U8)
         w_scale_sb = keep.tile([P, PACK], F32)
         style_b_sb = keep.tile([P, PACK], BF16)
-        bias_sb = keep.tile([P, PACK], BF16)
-        style_w_view = style_w.rearrange("(m t) l -> m t l", t=PACK)
+        bias_sb = keep.tile([PACK, P], BF16)
+        style_w_view = style_w.rearrange("(m h e) l -> h m e l", h=2, e=2)
+        weight_view = weight.rearrange("(h e m) c -> h m e c", h=2, e=2)
         nc.sync.dma_start(out=w_codes[:], in_=w_bytes)
-        nc.sync.dma_start(out=style_w_sb[:, 0:2, :], in_=style_w_view[:, 0:2, :])
-        nc.sync.dma_start(out=style_w_sb[:, 2:4, :], in_=style_w_view[:, 2:4, :])
+        for h in range(2):
+            nc.sync.dma_start(out=style_w_sb[h][:], in_=style_w_view[h])
         nc.scalar.dma_start(out=w_scale_sb[:], in_=w_scale.rearrange("o (p t) -> p (o t)", t=PACK))
         nc.scalar.dma_start(out=style_b_sb[:], in_=style_b.rearrange("(p t) -> p t", t=PACK))
-        nc.scalar.dma_start(out=bias_sb[:], in_=bias.rearrange("(p t) -> p t", t=PACK))
-        nc.sync.dma_start(out=weight_sb[:], in_=weight.rearrange("(m k) c -> m k c", k=PACK))
+        nc.scalar.dma_start(out=bias_sb[:], in_=bias.rearrange("(k m) -> k m", k=PACK))
+        for h in range(2):
+            nc.sync.dma_start(out=weight_sb[h][:], in_=weight_view[h])
 
-        x_tiles = {}
+        x_sb = ring("x_sb", GROUPS, [P, J, C], BF16)
 
         def load(u):
-            x_sb = x_pool.tile([P, J, C], BF16, name="x_sb")
-            nc.sync.dma_start(out=x_sb[:].rearrange("p j c -> p (j c)"), in_=x_view[u])
-            x_tiles[u] = x_sb
+            nc.sync.dma_start(out=x_sb[u][:], in_=x_view[u])
 
         for u in range(PRELOADED):
             load(u)
@@ -114,7 +80,11 @@ def tile_modulatemlp_pa_kernel(tc, x, w_bytes, w_scale, weight, style_w, style_b
         ones = keep.tile([P, 1], F32)
         nc.vector.memset(ones[:], 1.0)
         half_eps = keep.tile([P, 1], F32)
-        nc.vector.tensor_scalar(out=half_eps[:], in0=ones[:], scalar1=0.5 * EPS, scalar2=None, op0=ALU.mult)
+        nc.scalar.activation(out=half_eps[:], in_=ones[:], func=ACT.Abs_reciprocal_sqrt, scale=(0.5 * EPS) ** -2)
+        bias_rows = keep.tile([P, P], F32)
+        nc.vector.memset(bias_rows[:], 0.0)
+        steep_ident = keep.tile([P, P], F32)
+        nc.vector.tensor_scalar(out=steep_ident[:], in0=ident[:], scalar1=-(1.0 - SLOPE), scalar2=None, op0=ALU.mult)
 
         style_w_q = keep.tile([P, C], U32, align_bytes=64)
         style_w_s = keep.tile([P, C], U8, align_bytes=64)
@@ -126,241 +96,261 @@ def tile_modulatemlp_pa_kernel(tc, x, w_bytes, w_scale, weight, style_w, style_b
         weight2_s = keep.tile([P, O], U8, align_bytes=64)
         style2_q = keep.tile([P, SAMPLES], U32, align_bytes=64)
         style2_s = keep.tile([P, SAMPLES], U8, align_bytes=64)
-        style_w_t = keep.tile([P, PACK, P, PACK], BF16, align_bytes=64)
+        style_w_t = ring("style_w_t", 2, [P, 2 * P * PACK], BF16)
+        weight_t = ring("weight_t", 2, [P, 2 * P * PACK], BF16)
+        weight2_t = ring("weight2_t", 2, [P, 2 * P * PACK], BF16)
         w_t = keep.tile([P, SAMPLES, PACK], BF16, align_bytes=64)
-        weight_t = keep.tile([P, PACK, P, PACK], BF16, align_bytes=64)
-        weight2_t = keep.tile([P, O * PACK], BF16, align_bytes=64)
-        style2_t = keep.tile([P, SAMPLES * PACK], BF16, align_bytes=64)
-        weight_flat = weight_t[:].rearrange("p k m c -> p (k m c)")
+        style2_t = ring("style2_t", 2, [P, HALF * PACK], BF16)
         w_bf = keep.tile([P, LATENT], BF16)
-        style = keep.tile([P, SAMPLES, PACK], F32)
-        root = keep.tile([P, PACK, SAMPLES], F32)
-        decoef = keep.tile([P, PACK, SAMPLES], F32)
+        style = ring("style", 2, [P, HALF, PACK], F32)
+        decoef = ring("decoef", 2, [P, PACK, HALF], F32)
         bias_gain = keep.tile([P, PACK], F32)
 
-        def transpose_words(dst, row):
-            words = row.bitcast(F32)
-            for h in range(2):
-                nc.tensor.transpose(dst[:, h, :], words[:, h::2], ident[:])
+        modulated = ring("modulated", 2, [P, TOKENS, PACK], BF16)
+        codes = ring("codes", 4, [P, TOKENS], U32)
+        scales = ring("scales", 4, [P, TOKENS], U8)
+        z = ring("z", 3, [P, J, PACK, P], F32)
+        clipped = ring("clipped", 3, [P, J * O], F32)
+        negative = ring("negative", 3, [P, 2, P], F32)
+        relu = ring("relu", 3, [P, O], F32)
+        finished = ring("finished", 4, [P, J, O], F32)
 
-        def halves(big, h):
-            part = big[:, 2 * h : 2 * h + 2].rearrange("p t m k -> p t (m k)").bitcast(F32)
-            return part.rearrange("p t (m u) -> p t m u", u=2)
+        def at(tiles, index):
+            return tiles[index % len(tiles)]
 
-        def turn_rows(pool, name, rows, h):
-            turned = pool.tile([P, 2, 2, P], F32, name=name)
-            for k in range(2):
-                transpose_words(turned[:, k], rows[:, 2 * h + k, :])
-            return turned
+        def turn_rows(bank, rows):
+            parts = bank[:].rearrange("p (u j r) -> p u j r", u=2, j=2)
+            for j in range(2):
+                words = rows[:, j, :].bitcast(F32)
+                for u in range(2):
+                    nc.tensor.transpose(parts[:, u, j, :], words[:, u::2], ident[:])
 
-        def quantise_style_w(h):
+        def side_by_side(bank):
+            return bank[:].bitcast(BF16).rearrange("p (u r e) -> p r u e", u=2, e=2)
+
+        def copy_words(engine_copy, dst, bank):
+            engine_copy(out=dst[:].bitcast(F32).rearrange("p (r u) -> p r u", u=2),
+                        in_=bank[:].rearrange("p (u r) -> p r u", u=2))
+
+        def quantise_half(q, s, h, source):
             cols = slice(2 * P * h, 2 * P * (h + 1))
-            nc.vector.quantize_mx(out=style_w_q[:, cols].bitcast(X4), scales=style_w_s[:, cols],
-                                  in_=style_w_t[:, 2 * h : 2 * h + 2].rearrange("p t m k -> p (t m k)"))
+            nc.vector.quantize_mx(out=q[:, cols].bitcast(X4), scales=s[:, cols], in_=source[:])
 
-        def square_on_scalar(h):
-            cols = slice(h * 2 * P * PACK, (h + 1) * 2 * P * PACK)
-            nc.scalar.activation(out=weight2_t[:, cols], in_=weight_flat[:, cols], func=ACT.Square)
-
-        def square_on_vector(h):
-            cols = slice(h * 2 * P * PACK, (h + 1) * 2 * P * PACK)
-            nc.vector.tensor_tensor(out=weight2_t[:, cols], in0=weight_flat[:, cols], in1=weight_flat[:, cols], op=ALU.mult)
-
-        style_ps = {}
-        d_ps = {}
-
-        def style_product(t):
-            cols = slice(t * P, (t + 1) * P)
-            nc.tensor.matmul_mx(out=style_ps[0][:, t, :], lhsT=style_w_q[:, cols].bitcast(X4), lhsT_scale=style_w_s[:, cols],
-                                rhs=w_q[:].bitcast(X4), rhs_scale=w_s[:], start=True, stop=True)
+        style_bank = z_banks[2]
+        d_bank = y_banks[2]
 
         def make_style(h):
-            ns = slice(h * HALF, (h + 1) * HALF)
+            sums = style_bank[:].rearrange("p (t n) -> p n t", t=PACK)[:, h * HALF : (h + 1) * HALF, :]
             nc.vector.scalar_tensor_tensor(
-                out=style[:, ns, :], in0=style_ps[0][:, :, ns].rearrange("p t n -> p n t"), scalar=1.0 / math.sqrt(LATENT),
+                out=style[h][:], in0=sums, scalar=1.0 / math.sqrt(LATENT),
                 in1=style_b_sb[:].unsqueeze(1).to_broadcast([P, HALF, PACK]), op0=ALU.mult, op1=ALU.add)
 
         def square_style(h):
-            cols = slice(h * HALF * PACK, (h + 1) * HALF * PACK)
-            nc.scalar.activation(out=style2_t[:, cols], in_=style[:].rearrange("p n t -> p (n t)")[:, cols], func=ACT.Square)
+            flat = style[h][:].rearrange("p n t -> p (n t)")
+            if h == 0:
+                nc.vector.tensor_tensor(out=style2_t[h][:], in0=flat, in1=flat, op=ALU.mult)
+            else:
+                nc.scalar.activation(out=style2_t[h][:], in_=flat, func=ACT.Square)
 
         def quantise_style2(h):
             ns = slice(h * HALF, (h + 1) * HALF)
-            nc.vector.quantize_mx(out=style2_q[:, ns].bitcast(X4), scales=style2_s[:, ns],
-                                  in_=style2_t[:, h * HALF * PACK : (h + 1) * HALF * PACK])
+            nc.vector.quantize_mx(out=style2_q[:, ns].bitcast(X4), scales=style2_s[:, ns], in_=style2_t[h][:])
 
-        def d_product(h):
+        def d_product(h, bank):
             ns = slice(h * HALF, (h + 1) * HALF)
-            d_ps[h] = z_ps.tile([P, PACK, HALF], F32, name="zt")
             for k in range(PACK):
                 cols = slice(k * P, (k + 1) * P)
-                nc.tensor.matmul_mx(out=d_ps[h][:, k, :], lhsT=weight2_q[:, cols].bitcast(X4), lhsT_scale=weight2_s[:, cols],
-                                    rhs=style2_q[:, ns].bitcast(X4), rhs_scale=style2_s[:, ns], start=True, stop=True)
+                nc.tensor.matmul_mx(out=bank[:, k * HALF : (k + 1) * HALF], lhsT=weight2_q[:, cols].bitcast(X4),
+                                    lhsT_scale=weight2_s[:, cols], rhs=style2_q[:, ns].bitcast(X4),
+                                    rhs_scale=style2_s[:, ns], start=True, stop=True)
 
-        def take_root(h):
-            ns = slice(h * HALF, (h + 1) * HALF)
-            nc.scalar.activation(out=root[:, :, ns], in_=d_ps[h][:], func=ACT.Sqrt, scale=0.5, bias=half_eps[:])
-
-        def take_reciprocal(h):
-            ns = slice(h * HALF, (h + 1) * HALF)
-            nc.vector.reciprocal(out=decoef[:, :, ns], in_=root[:, :, ns])
-
-        turned_x, modulated, quantised, products, z, clipped, steep, turned_z, relu, finished = ({} for d in range(10))
+        def take_root(h, bank):
+            nc.scalar.activation(out=decoef[h][:].rearrange("p k n -> p (k n)"), in_=bank[:, : PACK * HALF],
+                                 func=ACT.Abs_reciprocal_sqrt, scale=0.5, bias=half_eps[:])
 
         def turn(u):
-            xt = xt_ps.tile([P, J, 2, P], F32, name="xt")
-            x_sb = x_tiles.pop(u)
-            for j in range(J):
-                transpose_words(xt[:, j], x_sb[:, j, :])
-            turned_x[u] = xt
+            turn_rows(at(x_banks, u), x_sb[u])
 
-        def modulate(u, j):
-            if j == 0:
-                modulated[u] = work.tile([P, J, P, PACK], BF16, name="xm", align_bytes=64)
-            of_group = style[:, u * GROUP_SAMPLES : (u + 1) * GROUP_SAMPLES, :].rearrange("p n (u e) -> p n u e", e=2)
+        def modulate(u):
+            first = u * GROUP_SAMPLES % HALF
+            of_group = style[u * GROUP_SAMPLES // HALF][:, first : first + GROUP_SAMPLES, :]
             nc.vector.tensor_tensor(
-                out=modulated[u][:, j].rearrange("p (n l) (u e) -> p n l u e", n=GROUP_SAMPLES, e=2),
-                in0=turned_x[u][:, j].bitcast(BF16).rearrange("p u (n l e) -> p n l u e", n=GROUP_SAMPLES, e=2),
-                in1=of_group.unsqueeze(2).to_broadcast([P, GROUP_SAMPLES, ROWS, 2, 2]),
+                out=at(modulated, u)[:].rearrange("p (n l) (u e) -> p n l u e", n=GROUP_SAMPLES, e=2),
+                in0=side_by_side(at(x_banks, u)).rearrange("p (n l) u e -> p n l u e", n=GROUP_SAMPLES),
+                in1=of_group.rearrange("p n (u e) -> p n u e", e=2).unsqueeze(2).to_broadcast([P, GROUP_SAMPLES, POINTS, 2, 2]),
                 op=ALU.mult)
 
         def quantise(u):
-            codes = work.tile([P, TOKENS], U32, name="xq", align_bytes=64)
-            scales = work.tile([P, TOKENS], U8, name="xs", align_bytes=64)
-            nc.vector.quantize_mx(out=codes[:].bitcast(X4), scales=scales[:],
-                                  in_=modulated.pop(u)[:].rearrange("p j r t -> p (j r t)"))
-            quantised[u] = (codes, scales)
+            nc.vector.quantize_mx(out=at(codes, u)[:].bitcast(X4), scales=at(scales, u)[:],
+                                  in_=at(modulated, u)[:].rearrange("p r t -> p (r t)"))
 
-        def product(u, h):
-            codes, scales = quantised[u]
-            yt = y_ps.tile([P, 2, TOKENS], F32, name="yt")
-            for part in range(2):
-                cols = slice((2 * h + part) * P, (2 * h + part + 1) * P)
-                nc.tensor.matmul_mx(out=yt[:, part, :], lhsT=weight_q[:, cols].bitcast(X4), lhsT_scale=weight_s[:, cols],
-                                    rhs=codes[:].bitcast(X4), rhs_scale=scales[:], start=True, stop=True)
-            products[u, h] = yt
+        def product(q):
+            u, h = divmod(q, 2)
+            for e in range(2):
+                cols = slice((2 * h + e) * P, (2 * h + e + 1) * P)
+                nc.tensor.matmul_mx(out=at(y_banks, q)[:, e * TOKENS : (e + 1) * TOKENS], lhsT=weight_q[:, cols].bitcast(X4),
+                                    lhsT_scale=weight_s[:, cols], rhs=at(codes, u)[:].bitcast(X4),
+                                    rhs_scale=at(scales, u)[:], start=True, stop=True)
 
-        def demodulate(u, h):
-            if h == 0:
-                z[u] = work.tile([P, PACK, TOKENS], F32, name="zr")
-            yt = products.pop((u, h))
-            for part in range(2):
-                k = 2 * h + part
-                for n in range(GROUP_SAMPLES):
-                    sample = u * GROUP_SAMPLES + n
+        def demodulate(q, samples):
+            u, h = divmod(q, 2)
+            for e in range(2):
+                k = 2 * h + e
+                for n in samples:
+                    half, sample = divmod(u * GROUP_SAMPLES + n, HALF)
+                    j, r = divmod(n * POINTS, P)
+                    first = e * TOKENS + n * POINTS
                     nc.scalar.activation(
-                        out=z[u][:, k, :].rearrange("p (j n l) -> p n j l", j=J, n=GROUP_SAMPLES)[:, n],
-                        in_=yt[:, part, :].rearrange("p (j n l) -> p n j l", j=J, n=GROUP_SAMPLES)[:, n],
-                        func=ACT.Identity, scale=decoef[:, k, sample : sample + 1], bias=bias_gain[:, k : k + 1])
+                        out=at(z, u)[:, j, k, r : r + POINTS], in_=at(y_banks, q)[:, first : first + POINTS],
+                        func=ACT.Identity, scale=decoef[half][:, k, sample : sample + 1], bias=bias_gain[:, k : k + 1])
 
-        def clip(u, h):
-            if h == 0:
-                clipped[u] = work.tile([P, PACK, TOKENS], F32, name="zc")
-            ks = slice(2 * h, 2 * h + 2)
-            cols = slice(0, sum((u, j) not in SUMMED for j in range(J)) * P)
-            nc.gpsimd.tensor_scalar(out=clipped[u][:, ks, cols], in0=z[u][:, ks, cols], scalar1=CLAMP,
+        def clip(engine, u, cols):
+            engine.tensor_scalar(out=at(clipped, u)[:, cols], in0=at(z, u)[:].rearrange("p j k r -> p (j k r)")[:, cols],
+                                 scalar1=CLAMP, scalar2=-CLAMP / SLOPE, op0=ALU.min, op1=ALU.max)
+
+        def take_negative(u):
+            nc.gpsimd.tensor_scalar(out=at(negative, u)[:], in0=at(z, u)[:, 1, 2:, :], scalar1=0.0,
                                     scalar2=-CLAMP / SLOPE, op0=ALU.min, op1=ALU.max)
 
-        def make_steep(u):
-            for j in range(J):
-                if (u, j) in SUMMED:
-                    negative = work.tile([P, PACK, P], F32, name="nq")
-                    nc.gpsimd.tensor_scalar(out=negative[:], in0=z[u][:, :, j * P : (j + 1) * P], scalar1=0.0,
-                                            scalar2=-CLAMP / SLOPE, op0=ALU.min, op1=ALU.max)
-                    steep[u, j] = work.tile([P, PACK, P], F32, name="q")
-                    nc.gpsimd.tensor_scalar(out=steep[u, j][:], in0=negative[:], scalar1=-(1.0 - SLOPE), scalar2=1.0,
-                                            op0=ALU.mult, op1=ALU.mult)
+        def block(u, j, k):
+            return at(z_banks, J * u + j)[:, k * P : (k + 1) * P]
 
-        def turn_back(u, j):
-            zt = z_ps.tile([P, PACK, P], F32, name="zt")
-            summed = (u, j) in SUMMED
-            source = z[u] if summed else clipped[u]
-            for k in range(PACK):
-                as_product = (j, k) == IDENTITY_PRODUCT and u < IDENTITY_PRODUCT_GROUPS
-                nc.tensor.matmul(out=zt[:, k, :], lhsT=source[:, k, j * P : (j + 1) * P], rhs=ident[:],
-                                 is_transpose=not as_product, start=True, stop=not summed)
-                if summed:
-                    nc.tensor.matmul(out=zt[:, k, :], lhsT=steep[u, j][:, k, :], rhs=ident[:],
-                                     is_transpose=True, start=False, stop=True)
-            turned_z[u, j] = zt
+        def turn_plain(u, j, count):
+            for k in range(count):
+                first = (j * PACK + k) * P
+                nc.tensor.transpose(block(u, j, k), at(clipped, u)[:, first : first + P], ident[:])
 
-        def make_relu(u, j):
-            if (u, j) in SUMMED:
-                return
-            relu[u, j] = work.tile([P, P, PACK], F32, name="qn")
-            in_order = turned_z[u, j][:].rearrange("p k m -> p m k")
-            if (u, j) in VECTOR_RELU:
-                nc.vector.tensor_scalar(out=relu[u, j][:], in0=in_order, scalar1=0.0, scalar2=-(1.0 - SLOPE),
-                                        op0=ALU.min, op1=ALU.mult)
+        def turn_summed(u, e, start):
+            nc.tensor.matmul(out=block(u, 1, 2 + e), lhsT=at(z, u)[:, 1, 2 + e, :], rhs=ident[:], is_transpose=True,
+                             start=start, stop=not start)
+
+        def add_steep(u, e, start):
+            nc.tensor.matmul(out=block(u, 1, 2 + e), lhsT=at(negative, u)[:, e, :], rhs=steep_ident[:],
+                             start=start, stop=not start)
+
+        def finish_plain(u, j, width):
+            turned = at(z_banks, J * u + j)[:, :width]
+            steep = at(relu, J * u + j)[:, :width]
+            if (u, j) not in VECTOR_ALONE:
+                nc.scalar.activation(out=steep, in_=turned, func=ACT.Relu, scale=-(1.0 - SLOPE))
             else:
-                nc.scalar.activation(out=relu[u, j][:], in_=in_order, func=ACT.Relu, scale=-(1.0 - SLOPE))
+                nc.vector.tensor_scalar(out=steep, in0=turned, scalar1=0.0, scalar2=-(1.0 - SLOPE), op0=ALU.min, op1=ALU.mult)
+            nc.vector.tensor_tensor(out=at(finished, u)[:, j, :width], in0=turned, in1=steep, op=ALU.add)
 
-        def finish(u, j):
-            if j == 0:
-                finished[u] = work.tile([P, J, O], F32, name="ot")
-            row = finished[u][:, j, :].rearrange("p (m k) -> p m k", k=PACK)
-            in_order = turned_z[u, j][:].rearrange("p k m -> p m k")
-            if (u, j) in SUMMED:
-                nc.vector.tensor_scalar(out=row, in0=in_order, scalar1=CLAMP, scalar2=-CLAMP, op0=ALU.min, op1=ALU.max)
-            else:
-                nc.vector.tensor_tensor(out=row, in0=in_order, in1=relu[u, j][:], op=ALU.add)
+        def finish_summed(u):
+            nc.vector.tensor_scalar(out=at(finished, u)[:, 1, 2 * P :], in0=at(z_banks, J * u + 1)[:, 2 * P :],
+                                    scalar1=CLAMP, scalar2=-CLAMP, op0=ALU.min, op1=ALU.max)
 
-        def store(u):
-            if u < GROUPS - 1:
-                nc.sync.dma_start(out=out_view[u], in_=finished[u][:].rearrange("p j o -> p (j o)"))
-            else:
-                for j in range(J):
-                    nc.sync.dma_start(out=out_view[u].rearrange("p (j o) -> p j o", j=J)[:, j, :], in_=finished[u][:, j, :])
+        def store(u, tiles):
+            nc.sync.dma_start(out=out_view[u][:, tiles], in_=at(finished, u)[:, tiles])
 
         nc.vector.tensor_copy(out=w_bf[:], in_=w_codes[:].bitcast(FP8))
-        style_w_ps = [turn_rows(y_ps, "yt", style_w_sb, 0)]
-        w_ps = y_ps.tile([P, 2, P], F32, name="yt")
-        transpose_words(w_ps[:], w_bf[:])
+        w_bank = y_banks[2]
+        w_words = w_bf[:].bitcast(F32)
+        for u in range(2):
+            nc.tensor.transpose(w_bank[:, u * P : (u + 1) * P], w_words[:, u::2], ident[:])
+        for h in range(2):
+            turn_rows(y_banks[h], style_w_sb[h])
         nc.vector.tensor_tensor(
             out=w_t[:].rearrange("p n (u e) -> p n u e", e=2),
-            in0=w_ps[:].bitcast(BF16).rearrange("p u (n e) -> p n u e", e=2),
+            in0=w_bank[:, : 2 * P].bitcast(BF16).rearrange("p (u n e) -> p n u e", u=2, e=2),
             in1=w_scale_sb[:].rearrange("p (u e) -> p u e", e=2).unsqueeze(1).to_broadcast([P, SAMPLES, 2, 2]),
             op=ALU.mult)
-        style_w_ps.append(turn_rows(y_ps, "yt", style_w_sb, 1))
-        for h in range(2):
-            nc.scalar.copy(out=halves(style_w_t, h), in_=style_w_ps[h][:].rearrange("p t u m -> p t m u"))
+        copy_words(nc.scalar.copy, style_w_t[0], y_banks[0])
+        nc.vector.tensor_scalar(out=bias_rows[:PACK, :], in0=bias_sb[:], scalar1=GAIN, scalar2=None, op0=ALU.mult)
         nc.vector.quantize_mx(out=w_q[:].bitcast(X4), scales=w_s[:], in_=w_t[:].rearrange("p n k -> p (n k)"))
+        copy_words(nc.scalar.copy, style_w_t[1], y_banks[1])
         for h in range(2):
-            quantise_style_w(h)
-        weight_ps = [turn_rows(z_ps, "zt", weight_sb, h) for h in range(2)]
-        style_ps[0] = z_ps.tile([P, PACK, P], F32, name="zt")
+            quantise_half(style_w_q, style_w_s, h, style_w_t[h])
+        for h in range(2):
+            turn_rows(z_banks[h], weight_sb[h])
+        nc.tensor.transpose(w_bank[:, :P], bias_rows[:], ident[:])
         for t in range(PACK):
-            style_product(t)
-        nc.vector.tensor_copy(out=halves(weight_t, 1), in_=weight_ps[1][:].rearrange("p t u m -> p t m u"))
+            cols = slice(t * P, (t + 1) * P)
+            nc.tensor.matmul_mx(out=style_bank[:, cols], lhsT=style_w_q[:, cols].bitcast(X4), lhsT_scale=style_w_s[:, cols],
+                                rhs=w_q[:].bitcast(X4), rhs_scale=w_s[:], start=True, stop=True)
         turn(0)
-        nc.vector.tensor_scalar(out=bias_gain[:], in0=bias_sb[:], scalar1=GAIN, scalar2=None, op0=ALU.mult)
-        square_on_vector(1)
         turn(1)
+        for h in range(2):
+            nc.scalar.activation(out=weight2_t[h][:].rearrange("p (r u e) -> p r u e", u=2, e=2),
+                                 in_=side_by_side(z_banks[h]), func=ACT.Square)
+        nc.vector.tensor_copy(out=bias_gain[:], in_=w_bank[:, :PACK])
         make_style(0)
-        nc.scalar.copy(out=halves(weight_t, 0), in_=weight_ps[0][:].rearrange("p t u m -> p t m u"))
-        square_on_scalar(0)
+        quantise_half(weight2_q, weight2_s, 0, weight2_t[0])
         square_style(0)
-        nc.vector.quantize_mx(out=weight2_q[:].bitcast(X4), scales=weight2_s[:], in_=weight2_t[:])
+        for h in range(2):
+            copy_words(nc.scalar.copy, weight_t[h], z_banks[h])
+        modulate(0)
         quantise_style2(0)
-        d_product(0)
-        modulate(0, 0)
-        nc.vector.quantize_mx(out=weight_q[:].bitcast(X4), scales=weight_s[:], in_=weight_flat)
-        modulate(1, 0)
-        take_root(0)
-        take_reciprocal(0)
+        quantise_half(weight2_q, weight2_s, 1, weight2_t[1])
+        d_product(0, d_bank)
+        take_root(0, d_bank)
+        quantise(0)
+        for h in range(2):
+            quantise_half(weight_q, weight_s, h, weight_t[h])
+            product(h)
+        turn(2)
+        modulate(1)
+        make_style(1)
+        quantise(1)
+        product(2)
+        turn(3)
+        square_style(1)
+        modulate(2)
+        quantise_style2(1)
+        d_product(1, z_banks[1])
+        quantise(2)
+        modulate(3)
 
-        steps = {"load": load, "turn": turn, "quantise": quantise, "steep": make_steep, "store": store}
-        for name, step in (("modulate", modulate), ("product", product), ("demodulate", demodulate), ("clip", clip),
-                           ("back", turn_back), ("relu", make_relu), ("finish", finish)):
-            for part in range(2):
-                steps["%s %d" % (name, part)] = lambda u, step=step, part=part: step(u, part)
-        second_half = {"style": make_style, "square": square_style, "quantise": quantise_style2, "product": d_product,
-                       "root": take_root, "reciprocal": take_reciprocal}
+        last = GROUPS - 1
+        for i in range(last + 1):
+            g = i - 1
+            if g >= 1:
+                turn_summed(g - 1, 1, start=False)
+            if i < last:
+                demodulate(2 * i, range(GROUP_SAMPLES))
+                demodulate(2 * i + 1, range(GROUP_SAMPLES))
+                clip(nc.gpsimd, i, slice(0, PLAIN))
+                take_negative(i)
+            else:
+                for j in range(J):
+                    for h in range(2):
+                        demodulate(2 * i + h, range(2 * j, 2 * j + 2))
+                    clip(nc.gpsimd, i, slice(j * O, (j + 1) * O))
+            if i == 0:
+                product(3)
+                take_root(1, z_banks[1])
+            if i + 4 <= last:
+                turn(i + 4)
+            if g >= 0:
+                turn_plain(g, 0, PACK)
+            if g >= 1:
+                finish_plain(g - 1, 1, 2 * P)
+                finish_summed(g - 1)
+                store(g - 1, slice(0, J))
+            if i + PRELOADED <= last:
+                load(i + PRELOADED)
+            if g >= 0:
+                turn_plain(g, 1, 2)
+                turn_summed(g, 0, start=True)
+                finish_plain(g, 0, O)
+                add_steep(g, 0, start=False)
+            for q in (2 * i + 3, 2 * i + 4):
+                if 3 < q < 2 * GROUPS:
+                    product(q)
+            if g >= 0:
+                add_steep(g, 1, start=True)
+            if i + 3 <= last:
+                quantise(i + 3)
+            if i + 4 <= last:
+                modulate(i + 4)
 
-        for i in range(FIRST_TURN, GROUPS + 2):
-            for name, ahead in STEPS:
-                if (i, name) in SECOND_HALF:
-                    second_half[SECOND_HALF[i, name]](1)
-                u = i + ahead
-                if 0 <= u < GROUPS and (name, u) not in EARLY:
-                    steps[name](u)
+        turn_summed(last - 1, 1, start=False)
+        turn_plain(last, 0, PACK)
+        finish_plain(last - 1, 1, 2 * P)
+        finish_summed(last - 1)
+        store(last - 1, slice(0, J))
+        turn_plain(last, 1, PACK)
+        for j in range(J):
+            finish_plain(last, j, O)
+            store(last, slice(j, j + 1))

@@ -29,7 +29,8 @@ J = TOKENS // P
 GROUPS = SAMPLES // GROUP_SAMPLES
 HALF = SAMPLES // 2
 PLAIN = 6 * P
-VECTOR_ALONE = {(u, 1) for u in range(GROUPS - 4, GROUPS - 2)}
+AHEAD = 3
+LAG = 2
 PRELOADED = 8
 
 
@@ -106,17 +107,23 @@ def tile_modulatemlp_pa_kernel(tc, x, w_bytes, w_scale, weight, style_w, style_b
         decoef = ring("decoef", 2, [P, PACK, HALF], F32)
         bias_gain = keep.tile([P, PACK], F32)
 
-        modulated = ring("modulated", 2, [P, TOKENS, PACK], BF16)
+        shared = ring("shared", 5, [P, J * O], F32)
         codes = ring("codes", 4, [P, TOKENS], U32)
         scales = ring("scales", 4, [P, TOKENS], U8)
-        z = ring("z", 3, [P, J, PACK, P], F32)
-        clipped = ring("clipped", 3, [P, J * O], F32)
-        negative = ring("negative", 3, [P, 2, P], F32)
+        z = ring("z", 4, [P, J, PACK, P], F32)
+        negative = ring("negative", 4, [P, 2, P], F32)
+        steeper = ring("steeper", 4, [P, P], F32)
         relu = ring("relu", 3, [P, O], F32)
         finished = ring("finished", 4, [P, J, O], F32)
 
         def at(tiles, index):
             return tiles[index % len(tiles)]
+
+        def modulated(u):
+            return at(shared, u)[:, : TOKENS * PACK // 2].bitcast(BF16)
+
+        def clipped(u):
+            return at(shared, u + AHEAD)
 
         def turn_rows(bank, rows):
             parts = bank[:].rearrange("p (u j r) -> p u j r", u=2, j=2)
@@ -175,14 +182,14 @@ def tile_modulatemlp_pa_kernel(tc, x, w_bytes, w_scale, weight, style_w, style_b
             first = u * GROUP_SAMPLES % HALF
             of_group = style[u * GROUP_SAMPLES // HALF][:, first : first + GROUP_SAMPLES, :]
             nc.vector.tensor_tensor(
-                out=at(modulated, u)[:].rearrange("p (n l) (u e) -> p n l u e", n=GROUP_SAMPLES, e=2),
+                out=modulated(u).rearrange("p (n l u e) -> p n l u e", n=GROUP_SAMPLES, u=2, e=2),
                 in0=side_by_side(at(x_banks, u)).rearrange("p (n l) u e -> p n l u e", n=GROUP_SAMPLES),
                 in1=of_group.rearrange("p n (u e) -> p n u e", e=2).unsqueeze(2).to_broadcast([P, GROUP_SAMPLES, POINTS, 2, 2]),
                 op=ALU.mult)
 
         def quantise(u):
             nc.vector.quantize_mx(out=at(codes, u)[:].bitcast(X4), scales=at(scales, u)[:],
-                                  in_=at(modulated, u)[:].rearrange("p r t -> p (r t)"))
+                                  in_=modulated(u))
 
         def product(q):
             u, h = divmod(q, 2)
@@ -205,12 +212,14 @@ def tile_modulatemlp_pa_kernel(tc, x, w_bytes, w_scale, weight, style_w, style_b
                         func=ACT.Identity, scale=decoef[half][:, k, sample : sample + 1], bias=bias_gain[:, k : k + 1])
 
         def clip(engine, u, cols):
-            engine.tensor_scalar(out=at(clipped, u)[:, cols], in0=at(z, u)[:].rearrange("p j k r -> p (j k r)")[:, cols],
+            engine.tensor_scalar(out=clipped(u)[:, cols], in0=at(z, u)[:].rearrange("p j k r -> p (j k r)")[:, cols],
                                  scalar1=CLAMP, scalar2=-CLAMP / SLOPE, op0=ALU.min, op1=ALU.max)
 
         def take_negative(u):
             nc.gpsimd.tensor_scalar(out=at(negative, u)[:], in0=at(z, u)[:, 1, 2:, :], scalar1=0.0,
                                     scalar2=-CLAMP / SLOPE, op0=ALU.min, op1=ALU.max)
+            nc.gpsimd.tensor_scalar(out=at(steeper, u)[:], in0=at(negative, u)[:, 1, :], scalar1=-(1.0 - SLOPE),
+                                    scalar2=1.0, op0=ALU.mult, op1=ALU.mult)
 
         def block(u, j, k):
             return at(z_banks, J * u + j)[:, k * P : (k + 1) * P]
@@ -218,7 +227,7 @@ def tile_modulatemlp_pa_kernel(tc, x, w_bytes, w_scale, weight, style_w, style_b
         def turn_plain(u, j, count):
             for k in range(count):
                 first = (j * PACK + k) * P
-                nc.tensor.transpose(block(u, j, k), at(clipped, u)[:, first : first + P], ident[:])
+                nc.tensor.transpose(block(u, j, k), clipped(u)[:, first : first + P], ident[:])
 
         def turn_summed(u, e, start):
             nc.tensor.matmul(out=block(u, 1, 2 + e), lhsT=at(z, u)[:, 1, 2 + e, :], rhs=ident[:], is_transpose=True,
@@ -231,10 +240,7 @@ def tile_modulatemlp_pa_kernel(tc, x, w_bytes, w_scale, weight, style_w, style_b
         def finish_plain(u, j, width):
             turned = at(z_banks, J * u + j)[:, :width]
             steep = at(relu, J * u + j)[:, :width]
-            if (u, j) not in VECTOR_ALONE:
-                nc.scalar.activation(out=steep, in_=turned, func=ACT.Relu, scale=-(1.0 - SLOPE))
-            else:
-                nc.vector.tensor_scalar(out=steep, in0=turned, scalar1=0.0, scalar2=-(1.0 - SLOPE), op0=ALU.min, op1=ALU.mult)
+            nc.scalar.activation(out=steep, in_=turned, func=ACT.Relu, scale=-(1.0 - SLOPE))
             nc.vector.tensor_tensor(out=at(finished, u)[:, j, :width], in0=turned, in1=steep, op=ALU.add)
 
         def finish_summed(u):
@@ -303,54 +309,64 @@ def tile_modulatemlp_pa_kernel(tc, x, w_bytes, w_scale, weight, style_w, style_b
         modulate(3)
 
         last = GROUPS - 1
-        for i in range(last + 1):
-            g = i - 1
+
+        def turn_second_tile(u):
+            if u < last:
+                turn_summed(u, 0, start=False)
+                turn_plain(u, 1, 2)
+                turn_summed(u, 1, start=True)
+                nc.tensor.matmul(out=block(u, 1, 3), lhsT=at(steeper, u)[:], rhs=ident[:], is_transpose=True,
+                                 start=False, stop=True)
+            else:
+                turn_plain(u, 1, PACK)
+
+        def finish_second_tile(u):
+            if u < last:
+                finish_plain(u, 1, 2 * P)
+                finish_summed(u)
+                store(u, slice(0, J))
+            else:
+                finish_plain(u, 1, O)
+                store(u, slice(1, 2))
+
+        for i in range(GROUPS + LAG + 1):
+            g = i - LAG
             if g >= 1:
-                turn_summed(g - 1, 1, start=False)
+                turn_second_tile(g - 1)
             if i < last:
                 demodulate(2 * i, range(GROUP_SAMPLES))
                 demodulate(2 * i + 1, range(GROUP_SAMPLES))
-                clip(nc.gpsimd, i, slice(0, PLAIN))
-                take_negative(i)
-            else:
+            elif i == last:
                 for j in range(J):
                     for h in range(2):
                         demodulate(2 * i + h, range(2 * j, 2 * j + 2))
-                    clip(nc.gpsimd, i, slice(j * O, (j + 1) * O))
             if i == 0:
                 product(3)
                 take_root(1, z_banks[1])
             if i + 4 <= last:
                 turn(i + 4)
-            if g >= 0:
+            if 0 <= g <= last:
                 turn_plain(g, 0, PACK)
             if g >= 1:
-                finish_plain(g - 1, 1, 2 * P)
-                finish_summed(g - 1)
-                store(g - 1, slice(0, J))
+                finish_second_tile(g - 1)
             if i + PRELOADED <= last:
                 load(i + PRELOADED)
-            if g >= 0:
-                turn_plain(g, 1, 2)
-                turn_summed(g, 0, start=True)
+            if 0 <= g <= last:
                 finish_plain(g, 0, O)
-                add_steep(g, 0, start=False)
+            if g == last:
+                store(g, slice(0, 1))
             for q in (2 * i + 3, 2 * i + 4):
                 if 3 < q < 2 * GROUPS:
                     product(q)
-            if g >= 0:
-                add_steep(g, 1, start=True)
-            if i + 3 <= last:
-                quantise(i + 3)
+            if 0 <= g < last:
+                add_steep(g, 0, start=True)
+            if i + AHEAD <= last:
+                quantise(i + AHEAD)
+            if i < last:
+                clip(nc.gpsimd, i, slice(0, PLAIN))
+                take_negative(i)
+            elif i == last:
+                for j in range(J):
+                    clip(nc.gpsimd, i, slice(j * O, (j + 1) * O))
             if i + 4 <= last:
                 modulate(i + 4)
-
-        turn_summed(last - 1, 1, start=False)
-        turn_plain(last, 0, PACK)
-        finish_plain(last - 1, 1, 2 * P)
-        finish_summed(last - 1)
-        store(last - 1, slice(0, J))
-        turn_plain(last, 1, PACK)
-        for j in range(J):
-            finish_plain(last, j, O)
-            store(last, slice(j, j + 1))

@@ -28,9 +28,13 @@ TOKENS = GROUP_SAMPLES * POINTS
 J = TOKENS // P
 GROUPS = SAMPLES // GROUP_SAMPLES
 HALF = SAMPLES // 2
-PLAIN = 6 * P
+PLAIN = ((0, 0), (0, 1), (0, 2), (0, 3), (1, 3))
+BY_PRODUCT = ((1, 0),)
+BY_TURN = ((1, 1), (1, 2))
+BLOCKS = PLAIN + BY_PRODUCT + BY_TURN
+ON_VECTOR = 0
 AHEAD = 3
-LAG = 2
+LAG = 1
 PRELOADED = 8
 
 
@@ -110,9 +114,9 @@ def tile_modulatemlp_pa_kernel(tc, x, w_bytes, w_scale, weight, style_w, style_b
         shared = ring("shared", 5, [P, J * O], F32)
         codes = ring("codes", 4, [P, TOKENS], U32)
         scales = ring("scales", 4, [P, TOKENS], U8)
-        z = ring("z", 4, [P, J, PACK, P], F32)
-        negative = ring("negative", 4, [P, 2, P], F32)
-        steeper = ring("steeper", 4, [P, P], F32)
+        z = ring("z", 4, [P, J * O], F32)
+        negative = ring("negative", 4, [P, O], F32)
+        steeper = ring("steeper", 4, [P, O], F32)
         relu = ring("relu", 3, [P, O], F32)
         finished = ring("finished", 4, [P, J, O], F32)
 
@@ -123,7 +127,7 @@ def tile_modulatemlp_pa_kernel(tc, x, w_bytes, w_scale, weight, style_w, style_b
             return at(shared, u)[:, : TOKENS * PACK // 2].bitcast(BF16)
 
         def clipped(u):
-            return at(shared, u + AHEAD)
+            return at(shared, u + AHEAD - 1)
 
         def turn_rows(bank, rows):
             parts = bank[:].rearrange("p (u j r) -> p u j r", u=2, j=2)
@@ -154,10 +158,7 @@ def tile_modulatemlp_pa_kernel(tc, x, w_bytes, w_scale, weight, style_w, style_b
 
         def square_style(h):
             flat = style[h][:].rearrange("p n t -> p (n t)")
-            if h == 0:
-                nc.vector.tensor_tensor(out=style2_t[h][:], in0=flat, in1=flat, op=ALU.mult)
-            else:
-                nc.scalar.activation(out=style2_t[h][:], in_=flat, func=ACT.Square)
+            nc.vector.tensor_tensor(out=style2_t[h][:], in0=flat, in1=flat, op=ALU.mult)
 
         def quantise_style2(h):
             ns = slice(h * HALF, (h + 1) * HALF)
@@ -199,53 +200,74 @@ def tile_modulatemlp_pa_kernel(tc, x, w_bytes, w_scale, weight, style_w, style_b
                                     lhsT_scale=weight_s[:, cols], rhs=at(codes, u)[:].bitcast(X4),
                                     rhs_scale=at(scales, u)[:], start=True, stop=True)
 
-        def demodulate(q, samples):
-            u, h = divmod(q, 2)
-            for e in range(2):
-                k = 2 * h + e
-                for n in samples:
-                    half, sample = divmod(u * GROUP_SAMPLES + n, HALF)
-                    j, r = divmod(n * POINTS, P)
-                    first = e * TOKENS + n * POINTS
-                    nc.scalar.activation(
-                        out=at(z, u)[:, j, k, r : r + POINTS], in_=at(y_banks, q)[:, first : first + POINTS],
-                        func=ACT.Identity, scale=decoef[half][:, k, sample : sample + 1], bias=bias_gain[:, k : k + 1])
+        last = GROUPS - 1
 
-        def clip(engine, u, cols):
-            engine.tensor_scalar(out=clipped(u)[:, cols], in0=at(z, u)[:].rearrange("p j k r -> p (j k r)")[:, cols],
-                                 scalar1=CLAMP, scalar2=-CLAMP / SLOPE, op0=ALU.min, op1=ALU.max)
+        def place(u, j, k, first=0):
+            number = BLOCKS.index((j, k)) if u < last else j * PACK + k
+            return slice((number - first) * P, (number - first + 1) * P)
+
+        def demodulate(engine, q, parts):
+            u, h = divmod(q, 2)
+            for e, n in parts:
+                k = 2 * h + e
+                half, sample = divmod(u * GROUP_SAMPLES + n, HALF)
+                j, r = divmod(n * POINTS, P)
+                first = e * TOKENS + n * POINTS
+                dst = at(z, u)[:, place(u, j, k)][:, r : r + POINTS]
+                src = at(y_banks, q)[:, first : first + POINTS]
+                factor = decoef[half][:, k, sample : sample + 1]
+                if engine is nc.scalar:
+                    nc.scalar.activation(out=dst, in_=src, func=ACT.Identity, scale=factor, bias=bias_gain[:, k : k + 1])
+                else:
+                    nc.vector.tensor_scalar(out=dst, in0=src, scalar1=factor, scalar2=bias_gain[:, k : k + 1],
+                                            op0=ALU.mult, op1=ALU.add)
+
+        def clip(u, cols):
+            nc.gpsimd.tensor_scalar(out=clipped(u)[:, cols], in0=at(z, u)[:, cols],
+                                    scalar1=CLAMP, scalar2=-CLAMP / SLOPE, op0=ALU.min, op1=ALU.max)
 
         def take_negative(u):
-            nc.gpsimd.tensor_scalar(out=at(negative, u)[:], in0=at(z, u)[:, 1, 2:, :], scalar1=0.0,
+            summed = (len(BLOCKS) - len(PLAIN)) * P
+            nc.gpsimd.tensor_scalar(out=at(negative, u)[:, :summed], in0=at(z, u)[:, len(PLAIN) * P :], scalar1=0.0,
                                     scalar2=-CLAMP / SLOPE, op0=ALU.min, op1=ALU.max)
-            nc.gpsimd.tensor_scalar(out=at(steeper, u)[:], in0=at(negative, u)[:, 1, :], scalar1=-(1.0 - SLOPE),
-                                    scalar2=1.0, op0=ALU.mult, op1=ALU.mult)
+            if BY_TURN:
+                nc.gpsimd.tensor_scalar(out=at(steeper, u)[:, : len(BY_TURN) * P],
+                                        in0=at(negative, u)[:, len(BY_PRODUCT) * P : summed],
+                                        scalar1=-(1.0 - SLOPE), scalar2=1.0, op0=ALU.mult, op1=ALU.mult)
 
         def block(u, j, k):
             return at(z_banks, J * u + j)[:, k * P : (k + 1) * P]
 
-        def turn_plain(u, j, count):
-            for k in range(count):
-                first = (j * PACK + k) * P
-                nc.tensor.transpose(block(u, j, k), clipped(u)[:, first : first + P], ident[:])
+        def turn_block(u, j, k, source, start, stop):
+            nc.tensor.matmul(out=block(u, j, k), lhsT=source, rhs=ident[:], is_transpose=True, start=start, stop=stop)
 
-        def turn_summed(u, e, start):
-            nc.tensor.matmul(out=block(u, 1, 2 + e), lhsT=at(z, u)[:, 1, 2 + e, :], rhs=ident[:], is_transpose=True,
+        def add_steep(u, j, k, start):
+            nc.tensor.matmul(out=block(u, j, k), lhsT=at(negative, u)[:, place(u, j, k, len(PLAIN))], rhs=steep_ident[:],
                              start=start, stop=not start)
 
-        def add_steep(u, e, start):
-            nc.tensor.matmul(out=block(u, 1, 2 + e), lhsT=at(negative, u)[:, e, :], rhs=steep_ident[:],
-                             start=start, stop=not start)
+        def turn_back(u, j):
+            for k in range(PACK):
+                if u == last or (j, k) in PLAIN:
+                    turn_block(u, j, k, clipped(u)[:, place(u, j, k)], True, True)
+                elif (j, k) in BY_TURN:
+                    turn_block(u, j, k, at(z, u)[:, place(u, j, k)], True, False)
+                    turn_block(u, j, k, at(steeper, u)[:, place(u, j, k, len(PLAIN) + len(BY_PRODUCT))], False, True)
+                else:
+                    turn_block(u, j, k, at(z, u)[:, place(u, j, k)], j == 0, j == 1)
 
-        def finish_plain(u, j, width):
-            turned = at(z_banks, J * u + j)[:, :width]
-            steep = at(relu, J * u + j)[:, :width]
-            nc.scalar.activation(out=steep, in_=turned, func=ACT.Relu, scale=-(1.0 - SLOPE))
-            nc.vector.tensor_tensor(out=at(finished, u)[:, j, :width], in0=turned, in1=steep, op=ALU.add)
-
-        def finish_summed(u):
-            nc.vector.tensor_scalar(out=at(finished, u)[:, 1, 2 * P :], in0=at(z_banks, J * u + 1)[:, 2 * P :],
-                                    scalar1=CLAMP, scalar2=-CLAMP, op0=ALU.min, op1=ALU.max)
+        def finish(u, j):
+            bank = at(z_banks, J * u + j)
+            plain = [k for k in range(PACK) if u == last or (j, k) in PLAIN]
+            summed = [k for k in range(PACK) if k not in plain]
+            if plain:
+                cols = slice(plain[0] * P, (plain[-1] + 1) * P)
+                steep = at(relu, J * u + j)[:, cols]
+                nc.scalar.activation(out=steep, in_=bank[:, cols], func=ACT.Relu, scale=-(1.0 - SLOPE))
+                nc.vector.tensor_tensor(out=at(finished, u)[:, j, cols], in0=bank[:, cols], in1=steep, op=ALU.add)
+            if summed:
+                cols = slice(summed[0] * P, (summed[-1] + 1) * P)
+                nc.vector.tensor_scalar(out=at(finished, u)[:, j, cols], in0=bank[:, cols],
+                                        scalar1=CLAMP, scalar2=-CLAMP, op0=ALU.min, op1=ALU.max)
 
         def store(u, tiles):
             nc.sync.dma_start(out=out_view[u][:, tiles], in_=at(finished, u)[:, tiles])
@@ -304,69 +326,64 @@ def tile_modulatemlp_pa_kernel(tc, x, w_bytes, w_scale, weight, style_w, style_b
         square_style(1)
         modulate(2)
         quantise_style2(1)
-        d_product(1, z_banks[1])
         quantise(2)
         modulate(3)
 
-        last = GROUPS - 1
+        parts = [(e, n) for e in range(2) for n in range(GROUP_SAMPLES)]
+        by_tile = [(e, n) for n in range(GROUP_SAMPLES) for e in range(2)]
 
-        def turn_second_tile(u):
-            if u < last:
-                turn_summed(u, 0, start=False)
-                turn_plain(u, 1, 2)
-                turn_summed(u, 1, start=True)
-                nc.tensor.matmul(out=block(u, 1, 3), lhsT=at(steeper, u)[:], rhs=ident[:], is_transpose=True,
-                                 start=False, stop=True)
-            else:
-                turn_plain(u, 1, PACK)
+        def on_vector(u):
+            return len(parts) if u == last - 1 else ON_VECTOR if u > 1 else 0
 
-        def finish_second_tile(u):
-            if u < last:
-                finish_plain(u, 1, 2 * P)
-                finish_summed(u)
-                store(u, slice(0, J))
-            else:
-                finish_plain(u, 1, O)
-                store(u, slice(1, 2))
+        def clip_group(i):
+            if i < last:
+                clip(i, slice(0, len(PLAIN) * P))
+                take_negative(i)
+            elif i == last:
+                for j in range(J):
+                    clip(i, slice(j * O, (j + 1) * O))
 
         for i in range(GROUPS + LAG + 1):
             g = i - LAG
             if g >= 1:
-                turn_second_tile(g - 1)
+                turn_back(g - 1, 1)
             if i < last:
-                demodulate(2 * i, range(GROUP_SAMPLES))
-                demodulate(2 * i + 1, range(GROUP_SAMPLES))
+                demodulate(nc.scalar, 2 * i, parts[on_vector(i) :])
+                demodulate(nc.scalar, 2 * i + 1, parts)
             elif i == last:
-                for j in range(J):
-                    for h in range(2):
-                        demodulate(2 * i + h, range(2 * j, 2 * j + 2))
+                demodulate(nc.scalar, 2 * i + 1, by_tile)
+            clip_group(i)
             if i == 0:
                 product(3)
-                take_root(1, z_banks[1])
             if i + 4 <= last:
                 turn(i + 4)
+            if i == 0:
+                d_product(1, z_banks[1])
+            if i == 1:
+                take_root(1, z_banks[1])
             if 0 <= g <= last:
-                turn_plain(g, 0, PACK)
+                turn_back(g, 0)
             if g >= 1:
-                finish_second_tile(g - 1)
+                finish(g - 1, 1)
+                store(g - 1, slice(0, J) if g - 1 < last else slice(1, 2))
             if i + PRELOADED <= last:
                 load(i + PRELOADED)
+            if 0 <= g < last and (0, PACK - 1) in BY_PRODUCT:
+                add_steep(g, 0, PACK - 1, start=False)
             if 0 <= g <= last:
-                finish_plain(g, 0, O)
+                finish(g, 0)
             if g == last:
                 store(g, slice(0, 1))
             for q in (2 * i + 3, 2 * i + 4):
                 if 3 < q < 2 * GROUPS:
                     product(q)
             if 0 <= g < last:
-                add_steep(g, 0, start=True)
+                add_steep(g, 1, 0, start=True)
             if i + AHEAD <= last:
                 quantise(i + AHEAD)
-            if i < last:
-                clip(nc.gpsimd, i, slice(0, PLAIN))
-                take_negative(i)
-            elif i == last:
-                for j in range(J):
-                    clip(nc.gpsimd, i, slice(j * O, (j + 1) * O))
             if i + 4 <= last:
                 modulate(i + 4)
+            if i + 2 < last:
+                demodulate(nc.vector, 2 * i + 4, parts[: on_vector(i + 2)])
+            elif i + 2 == last:
+                demodulate(nc.vector, 2 * last, by_tile)

@@ -28,13 +28,14 @@ TOKENS = GROUP_SAMPLES * POINTS
 J = TOKENS // P
 GROUPS = SAMPLES // GROUP_SAMPLES
 HALF = SAMPLES // 2
-PLAIN = ((0, 0), (0, 1), (0, 2), (0, 3), (1, 3))
-BY_PRODUCT = ((1, 0),)
-BY_TURN = ((1, 1), (1, 2))
+PLAIN = ((0, 0), (0, 1), (0, 2), (0, 3), (1, 0), (1, 1))
+BY_PRODUCT = ((1, 2), (1, 3))
+BY_TURN = ()
 BLOCKS = PLAIN + BY_PRODUCT + BY_TURN
 ON_VECTOR = 0
 AHEAD = 3
 LAG = 1
+RAMP = 2
 PRELOADED = 8
 
 
@@ -148,7 +149,6 @@ def tile_modulatemlp_pa_kernel(tc, x, w_bytes, w_scale, weight, style_w, style_b
             nc.vector.quantize_mx(out=q[:, cols].bitcast(X4), scales=s[:, cols], in_=source[:])
 
         style_bank = z_banks[2]
-        d_bank = y_banks[2]
 
         def make_style(h):
             sums = style_bank[:].rearrange("p (t n) -> p n t", t=PACK)[:, h * HALF : (h + 1) * HALF, :]
@@ -164,41 +164,43 @@ def tile_modulatemlp_pa_kernel(tc, x, w_bytes, w_scale, weight, style_w, style_b
             ns = slice(h * HALF, (h + 1) * HALF)
             nc.vector.quantize_mx(out=style2_q[:, ns].bitcast(X4), scales=style2_s[:, ns], in_=style2_t[h][:])
 
-        def d_product(h, bank):
-            ns = slice(h * HALF, (h + 1) * HALF)
-            for k in range(PACK):
+        def d_product(half, bank, blocks):
+            ns = slice(half * HALF, (half + 1) * HALF)
+            for k in blocks:
                 cols = slice(k * P, (k + 1) * P)
                 nc.tensor.matmul_mx(out=bank[:, k * HALF : (k + 1) * HALF], lhsT=weight2_q[:, cols].bitcast(X4),
                                     lhsT_scale=weight2_s[:, cols], rhs=style2_q[:, ns].bitcast(X4),
                                     rhs_scale=style2_s[:, ns], start=True, stop=True)
 
-        def take_root(h, bank):
-            nc.scalar.activation(out=decoef[h][:].rearrange("p k n -> p (k n)"), in_=bank[:, : PACK * HALF],
+        def take_root(half, bank, blocks):
+            cols = slice(blocks.start * HALF, blocks.stop * HALF)
+            nc.scalar.activation(out=decoef[half][:].rearrange("p k n -> p (k n)")[:, cols], in_=bank[:, cols],
                                  func=ACT.Abs_reciprocal_sqrt, scale=0.5, bias=half_eps[:])
 
         def turn(u):
             turn_rows(at(x_banks, u), x_sb[u])
 
-        def modulate(u):
-            first = u * GROUP_SAMPLES % HALF
-            of_group = style[u * GROUP_SAMPLES // HALF][:, first : first + GROUP_SAMPLES, :]
+        def modulate(u, first=0, count=GROUP_SAMPLES):
+            half, sample = divmod(u * GROUP_SAMPLES + first, HALF)
+            factors = style[half][:, sample : sample + count, :].rearrange("p n (u e) -> p n u e", e=2)
+            ns = slice(first, first + count)
             nc.vector.tensor_tensor(
-                out=modulated(u).rearrange("p (n l u e) -> p n l u e", n=GROUP_SAMPLES, u=2, e=2),
-                in0=side_by_side(at(x_banks, u)).rearrange("p (n l) u e -> p n l u e", n=GROUP_SAMPLES),
-                in1=of_group.rearrange("p n (u e) -> p n u e", e=2).unsqueeze(2).to_broadcast([P, GROUP_SAMPLES, POINTS, 2, 2]),
-                op=ALU.mult)
+                out=modulated(u).rearrange("p (n l u e) -> p n l u e", n=GROUP_SAMPLES, u=2, e=2)[:, ns],
+                in0=side_by_side(at(x_banks, u)).rearrange("p (n l) u e -> p n l u e", n=GROUP_SAMPLES)[:, ns],
+                in1=factors.unsqueeze(2).to_broadcast([P, count, POINTS, 2, 2]), op=ALU.mult)
 
-        def quantise(u):
-            nc.vector.quantize_mx(out=at(codes, u)[:].bitcast(X4), scales=at(scales, u)[:],
-                                  in_=modulated(u))
+        def quantise(u, tokens=slice(0, TOKENS)):
+            nc.vector.quantize_mx(out=at(codes, u)[:, tokens].bitcast(X4), scales=at(scales, u)[:, tokens],
+                                  in_=modulated(u)[:, tokens.start * PACK : tokens.stop * PACK])
 
-        def product(q):
+        def product(q, tokens=slice(0, TOKENS), bank=None):
             u, h = divmod(q, 2)
+            bank = at(y_banks, q + 1) if bank is None else bank
             for e in range(2):
                 cols = slice((2 * h + e) * P, (2 * h + e + 1) * P)
-                nc.tensor.matmul_mx(out=at(y_banks, q)[:, e * TOKENS : (e + 1) * TOKENS], lhsT=weight_q[:, cols].bitcast(X4),
-                                    lhsT_scale=weight_s[:, cols], rhs=at(codes, u)[:].bitcast(X4),
-                                    rhs_scale=at(scales, u)[:], start=True, stop=True)
+                nc.tensor.matmul_mx(out=bank[:, e * TOKENS : (e + 1) * TOKENS][:, tokens], lhsT=weight_q[:, cols].bitcast(X4),
+                                    lhsT_scale=weight_s[:, cols], rhs=at(codes, u)[:, tokens].bitcast(X4),
+                                    rhs_scale=at(scales, u)[:, tokens], start=True, stop=True)
 
         last = GROUPS - 1
 
@@ -206,15 +208,16 @@ def tile_modulatemlp_pa_kernel(tc, x, w_bytes, w_scale, weight, style_w, style_b
             number = BLOCKS.index((j, k)) if u < last else j * PACK + k
             return slice((number - first) * P, (number - first + 1) * P)
 
-        def demodulate(engine, q, parts):
+        def demodulate(engine, q, parts, bank=None):
             u, h = divmod(q, 2)
+            bank = at(y_banks, q + 1) if bank is None else bank
             for e, n in parts:
                 k = 2 * h + e
                 half, sample = divmod(u * GROUP_SAMPLES + n, HALF)
                 j, r = divmod(n * POINTS, P)
                 first = e * TOKENS + n * POINTS
                 dst = at(z, u)[:, place(u, j, k)][:, r : r + POINTS]
-                src = at(y_banks, q)[:, first : first + POINTS]
+                src = bank[:, first : first + POINTS]
                 factor = decoef[half][:, k, sample : sample + 1]
                 if engine is nc.scalar:
                     nc.scalar.activation(out=dst, in_=src, func=ACT.Identity, scale=factor, bias=bias_gain[:, k : k + 1])
@@ -235,8 +238,11 @@ def tile_modulatemlp_pa_kernel(tc, x, w_bytes, w_scale, weight, style_w, style_b
                                         in0=at(negative, u)[:, len(BY_PRODUCT) * P : summed],
                                         scalar1=-(1.0 - SLOPE), scalar2=1.0, op0=ALU.mult, op1=ALU.mult)
 
+        def z_bank(u, j):
+            return at(z_banks, J * u + j) if u < last else x_banks[j]
+
         def block(u, j, k):
-            return at(z_banks, J * u + j)[:, k * P : (k + 1) * P]
+            return z_bank(u, j)[:, k * P : (k + 1) * P]
 
         def turn_block(u, j, k, source, start, stop):
             nc.tensor.matmul(out=block(u, j, k), lhsT=source, rhs=ident[:], is_transpose=True, start=start, stop=stop)
@@ -245,18 +251,15 @@ def tile_modulatemlp_pa_kernel(tc, x, w_bytes, w_scale, weight, style_w, style_b
             nc.tensor.matmul(out=block(u, j, k), lhsT=at(negative, u)[:, place(u, j, k, len(PLAIN))], rhs=steep_ident[:],
                              start=start, stop=not start)
 
-        def turn_back(u, j):
-            for k in range(PACK):
+        def turn_back(u, j, blocks):
+            for k in blocks:
                 if u == last or (j, k) in PLAIN:
                     turn_block(u, j, k, clipped(u)[:, place(u, j, k)], True, True)
-                elif (j, k) in BY_TURN:
-                    turn_block(u, j, k, at(z, u)[:, place(u, j, k)], True, False)
-                    turn_block(u, j, k, at(steeper, u)[:, place(u, j, k, len(PLAIN) + len(BY_PRODUCT))], False, True)
                 else:
-                    turn_block(u, j, k, at(z, u)[:, place(u, j, k)], j == 0, j == 1)
+                    turn_block(u, j, k, at(z, u)[:, place(u, j, k)], k == 2, k == 3)
 
         def finish(u, j):
-            bank = at(z_banks, J * u + j)
+            bank = z_bank(u, j)
             plain = [k for k in range(PACK) if u == last or (j, k) in PLAIN]
             summed = [k for k in range(PACK) if k not in plain]
             if plain:
@@ -271,6 +274,9 @@ def tile_modulatemlp_pa_kernel(tc, x, w_bytes, w_scale, weight, style_w, style_b
 
         def store(u, tiles):
             nc.sync.dma_start(out=out_view[u][:, tiles], in_=at(finished, u)[:, tiles])
+
+        parts = [(e, n) for e in range(2) for n in range(GROUP_SAMPLES)]
+        by_tile = [(e, n) for n in range(GROUP_SAMPLES) for e in range(2)]
 
         nc.vector.tensor_copy(out=w_bf[:], in_=w_codes[:].bitcast(FP8))
         w_bank = y_banks[2]
@@ -300,23 +306,30 @@ def tile_modulatemlp_pa_kernel(tc, x, w_bytes, w_scale, weight, style_w, style_b
         turn(0)
         turn(1)
         for h in range(2):
-            nc.scalar.activation(out=weight2_t[h][:].rearrange("p (r u e) -> p r u e", u=2, e=2),
-                                 in_=side_by_side(z_banks[h]), func=ACT.Square)
+            copy_words(nc.scalar.copy, weight_t[h], z_banks[h])
+        nc.scalar.activation(out=weight2_t[1][:], in_=weight_t[1][:], func=ACT.Square)
         nc.vector.tensor_copy(out=bias_gain[:], in_=w_bank[:, :PACK])
+        nc.vector.tensor_tensor(out=weight2_t[0][:], in0=weight_t[0][:], in1=weight_t[0][:], op=ALU.mult)
+        quantise_half(weight_q, weight_s, 0, weight_t[0])
         make_style(0)
         quantise_half(weight2_q, weight2_s, 0, weight2_t[0])
         square_style(0)
-        for h in range(2):
-            copy_words(nc.scalar.copy, weight_t[h], z_banks[h])
-        modulate(0)
+        modulate(0, 0, 2)
         quantise_style2(0)
+        quantise(0, slice(0, P))
+        d_product(0, z_banks[0], range(0, 2))
+        product(0, slice(0, P), y_banks[0])
+        take_root(0, z_banks[0], range(0, 2))
+        demodulate(nc.scalar, 0, by_tile[:PACK], y_banks[0])
+        modulate(0, 2, 2)
         quantise_half(weight2_q, weight2_s, 1, weight2_t[1])
-        d_product(0, d_bank)
-        take_root(0, d_bank)
-        quantise(0)
-        for h in range(2):
-            quantise_half(weight_q, weight_s, h, weight_t[h])
-            product(h)
+        quantise(0, slice(P, TOKENS))
+        quantise_half(weight_q, weight_s, 1, weight_t[1])
+        product(0, slice(P, TOKENS))
+        d_product(0, z_banks[1], range(2, PACK))
+        product(1)
+        demodulate(nc.scalar, 0, by_tile[PACK:])
+        take_root(0, z_banks[1], range(2, PACK))
         turn(2)
         modulate(1)
         make_style(1)
@@ -329,11 +342,14 @@ def tile_modulatemlp_pa_kernel(tc, x, w_bytes, w_scale, weight, style_w, style_b
         quantise(2)
         modulate(3)
 
-        parts = [(e, n) for e in range(2) for n in range(GROUP_SAMPLES)]
-        by_tile = [(e, n) for n in range(GROUP_SAMPLES) for e in range(2)]
-
         def on_vector(u):
-            return len(parts) if u == last - 1 else ON_VECTOR if u > 1 else 0
+            return len(parts) if u in (0, last - 1) else ON_VECTOR if u > 3 else 0
+
+        def prepare(i):
+            if i + AHEAD <= last:
+                quantise(i + AHEAD)
+            if i + AHEAD + 1 <= last:
+                modulate(i + AHEAD + 1)
 
         def clip_group(i):
             if i < last:
@@ -346,43 +362,45 @@ def tile_modulatemlp_pa_kernel(tc, x, w_bytes, w_scale, weight, style_w, style_b
         for i in range(GROUPS + LAG + 1):
             g = i - LAG
             if g >= 1:
-                turn_back(g - 1, 1)
+                turn_back(g - 1, 1, range(3, PACK))
             if i < last:
                 demodulate(nc.scalar, 2 * i, parts[on_vector(i) :])
                 demodulate(nc.scalar, 2 * i + 1, parts)
+                if i == 1:
+                    take_root(1, z_banks[2], range(PACK))
             elif i == last:
                 demodulate(nc.scalar, 2 * i + 1, by_tile)
             clip_group(i)
-            if i == 0:
-                product(3)
+            if i < RAMP:
+                product(2 * i + 3)
             if i + 4 <= last:
                 turn(i + 4)
-            if i == 0:
-                d_product(1, z_banks[1])
-            if i == 1:
-                take_root(1, z_banks[1])
             if 0 <= g <= last:
-                turn_back(g, 0)
+                turn_back(g, 0, range(PACK))
             if g >= 1:
                 finish(g - 1, 1)
-                store(g - 1, slice(0, J) if g - 1 < last else slice(1, 2))
+                store(g - 1, slice(0, J) if g - 1 < last - 1 else slice(1, 2))
             if i + PRELOADED <= last:
                 load(i + PRELOADED)
-            if 0 <= g < last and (0, PACK - 1) in BY_PRODUCT:
-                add_steep(g, 0, PACK - 1, start=False)
+            if 0 <= g <= last:
+                turn_back(g, 1, range(3))
+            if 0 <= g < last:
+                add_steep(g, 1, 2, start=False)
+            if i < RAMP:
+                prepare(i)
             if 0 <= g <= last:
                 finish(g, 0)
-            if g == last:
+            if last - 1 <= g <= last:
                 store(g, slice(0, 1))
             for q in (2 * i + 3, 2 * i + 4):
-                if 3 < q < 2 * GROUPS:
+                if q < 2 * GROUPS and (i >= RAMP or q % 2 == 0):
                     product(q)
+            if i == 0:
+                d_product(1, z_banks[2], range(PACK))
             if 0 <= g < last:
-                add_steep(g, 1, 0, start=True)
-            if i + AHEAD <= last:
-                quantise(i + AHEAD)
-            if i + 4 <= last:
-                modulate(i + 4)
+                add_steep(g, 1, 3, start=True)
+            if i >= RAMP:
+                prepare(i)
             if i + 2 < last:
                 demodulate(nc.vector, 2 * i + 4, parts[: on_vector(i + 2)])
             elif i + 2 == last:

@@ -36,6 +36,7 @@ ON_VECTOR = 0
 AHEAD = 3
 LAG = 1
 RAMP = 2
+PERIOD = 2
 PRELOADED = 8
 
 
@@ -51,6 +52,9 @@ def tile_modulatemlp_pa_kernel(tc, x, w_bytes, w_scale, weight, style_w, style_b
 
         def ring(name, count, shape, dtype):
             return [keep.tile(shape, dtype, name="%s%d" % (name, r), align_bytes=64) for r in range(count)]
+
+        def at(tiles, index):
+            return tiles[index % len(tiles)]
 
         x_banks = [psum.tile([P, BANK], F32, name="x_bank%d" % r) for r in range(2)]
         y_banks = [psum.tile([P, BANK], F32, name="y_bank%d" % r) for r in range(3)]
@@ -73,10 +77,10 @@ def tile_modulatemlp_pa_kernel(tc, x, w_bytes, w_scale, weight, style_w, style_b
         for h in range(2):
             nc.sync.dma_start(out=weight_sb[h][:], in_=weight_view[h])
 
-        x_sb = ring("x_sb", GROUPS, [P, J, C], BF16)
+        x_sb = ring("x_sb", PRELOADED + 2, [P, J, C], BF16)
 
         def load(u):
-            nc.sync.dma_start(out=x_sb[u][:], in_=x_view[u])
+            nc.sync.dma_start(out=at(x_sb, u)[:], in_=x_view[u])
 
         for u in range(PRELOADED):
             load(u)
@@ -115,14 +119,10 @@ def tile_modulatemlp_pa_kernel(tc, x, w_bytes, w_scale, weight, style_w, style_b
         shared = ring("shared", 5, [P, J * O], F32)
         codes = ring("codes", 4, [P, TOKENS], U32)
         scales = ring("scales", 4, [P, TOKENS], U8)
-        z = ring("z", 4, [P, J * O], F32)
-        negative = ring("negative", 4, [P, O], F32)
-        steeper = ring("steeper", 4, [P, O], F32)
+        z = ring("z", 3, [P, J * O], F32)
+        negative = ring("negative", 3, [P, 2 * P], F32)
         relu = ring("relu", 3, [P, O], F32)
-        finished = ring("finished", 4, [P, J, O], F32)
-
-        def at(tiles, index):
-            return tiles[index % len(tiles)]
+        finished = ring("finished", GROUPS, [P, J, O], F32)
 
         def modulated(u):
             return at(shared, u)[:, : TOKENS * PACK // 2].bitcast(BF16)
@@ -178,7 +178,7 @@ def tile_modulatemlp_pa_kernel(tc, x, w_bytes, w_scale, weight, style_w, style_b
                                  func=ACT.Abs_reciprocal_sqrt, scale=0.5, bias=half_eps[:])
 
         def turn(u):
-            turn_rows(at(x_banks, u), x_sb[u])
+            turn_rows(at(x_banks, u), at(x_sb, u))
 
         def modulate(u, first=0, count=GROUP_SAMPLES):
             half, sample = divmod(u * GROUP_SAMPLES + first, HALF)
@@ -225,6 +225,9 @@ def tile_modulatemlp_pa_kernel(tc, x, w_bytes, w_scale, weight, style_w, style_b
                     nc.vector.tensor_scalar(out=dst, in0=src, scalar1=factor, scalar2=bias_gain[:, k : k + 1],
                                             op0=ALU.mult, op1=ALU.add)
 
+        def scalar_empties(u):
+            return u % PERIOD == PERIOD - 1 and u < GROUPS - 5
+
         def clip(u, cols):
             nc.gpsimd.tensor_scalar(out=clipped(u)[:, cols], in0=at(z, u)[:, cols],
                                     scalar1=CLAMP, scalar2=-CLAMP / SLOPE, op0=ALU.min, op1=ALU.max)
@@ -233,10 +236,6 @@ def tile_modulatemlp_pa_kernel(tc, x, w_bytes, w_scale, weight, style_w, style_b
             summed = (len(BLOCKS) - len(PLAIN)) * P
             nc.gpsimd.tensor_scalar(out=at(negative, u)[:, :summed], in0=at(z, u)[:, len(PLAIN) * P :], scalar1=0.0,
                                     scalar2=-CLAMP / SLOPE, op0=ALU.min, op1=ALU.max)
-            if BY_TURN:
-                nc.gpsimd.tensor_scalar(out=at(steeper, u)[:, : len(BY_TURN) * P],
-                                        in0=at(negative, u)[:, len(BY_PRODUCT) * P : summed],
-                                        scalar1=-(1.0 - SLOPE), scalar2=1.0, op0=ALU.mult, op1=ALU.mult)
 
         def z_bank(u, j):
             return at(z_banks, J * u + j) if u < last else x_banks[j]
@@ -256,20 +255,26 @@ def tile_modulatemlp_pa_kernel(tc, x, w_bytes, w_scale, weight, style_w, style_b
                 if u == last or (j, k) in PLAIN:
                     turn_block(u, j, k, clipped(u)[:, place(u, j, k)], True, True)
                 else:
-                    turn_block(u, j, k, at(z, u)[:, place(u, j, k)], k == 2, k == 3)
+                    source = clipped(u) if scalar_empties(u) else at(z, u)
+                    turn_block(u, j, k, source[:, place(u, j, k)], k == 2, k == 3)
+
+        def plain_width(u, j):
+            return O if u == last or j == 0 else 2 * P
+
+        def take_relu(u, j):
+            width = plain_width(u, j)
+            nc.scalar.activation(out=at(relu, J * u + j)[:, :width], in_=z_bank(u, j)[:, :width], func=ACT.Relu,
+                                 scale=-(1.0 - SLOPE))
+            if width < O and scalar_empties(u):
+                nc.scalar.copy(out=finished[u][:, j, width:], in_=z_bank(u, j)[:, width:])
 
         def finish(u, j):
+            width = plain_width(u, j)
             bank = z_bank(u, j)
-            plain = [k for k in range(PACK) if u == last or (j, k) in PLAIN]
-            summed = [k for k in range(PACK) if k not in plain]
-            if plain:
-                cols = slice(plain[0] * P, (plain[-1] + 1) * P)
-                steep = at(relu, J * u + j)[:, cols]
-                nc.scalar.activation(out=steep, in_=bank[:, cols], func=ACT.Relu, scale=-(1.0 - SLOPE))
-                nc.vector.tensor_tensor(out=at(finished, u)[:, j, cols], in0=bank[:, cols], in1=steep, op=ALU.add)
-            if summed:
-                cols = slice(summed[0] * P, (summed[-1] + 1) * P)
-                nc.vector.tensor_scalar(out=at(finished, u)[:, j, cols], in0=bank[:, cols],
+            nc.vector.tensor_tensor(out=finished[u][:, j, :width], in0=bank[:, :width], in1=at(relu, J * u + j)[:, :width],
+                                    op=ALU.add)
+            if width < O and not scalar_empties(u):
+                nc.vector.tensor_scalar(out=finished[u][:, j, width:], in0=bank[:, width:],
                                         scalar1=CLAMP, scalar2=-CLAMP, op0=ALU.min, op1=ALU.max)
 
         def store(u, tiles):
@@ -353,7 +358,7 @@ def tile_modulatemlp_pa_kernel(tc, x, w_bytes, w_scale, weight, style_w, style_b
 
         def clip_group(i):
             if i < last:
-                clip(i, slice(0, len(PLAIN) * P))
+                clip(i, slice(0, len(BLOCKS if scalar_empties(i) else PLAIN) * P))
                 take_negative(i)
             elif i == last:
                 for j in range(J):
@@ -378,8 +383,11 @@ def tile_modulatemlp_pa_kernel(tc, x, w_bytes, w_scale, weight, style_w, style_b
             if 0 <= g <= last:
                 turn_back(g, 0, range(PACK))
             if g >= 1:
+                take_relu(g - 1, 1)
                 finish(g - 1, 1)
                 store(g - 1, slice(0, J) if g - 1 < last - 1 else slice(1, 2))
+            if 0 <= g <= last:
+                take_relu(g, 0)
             if i + PRELOADED <= last:
                 load(i + PRELOADED)
             if 0 <= g <= last:

@@ -244,7 +244,8 @@ def tile_modulatemlp_pa_kernel(tc, x, w_bytes, w_scale, weight, style_w, style_b
             return z_bank(u, j)[:, k * P : (k + 1) * P]
 
         def turn_block(u, j, k, source, start, stop):
-            nc.tensor.matmul(out=block(u, j, k), lhsT=source, rhs=ident[:], is_transpose=True, start=start, stop=stop)
+            nc.tensor.matmul(out=block(u, j, k), lhsT=source, rhs=ident[:], is_transpose=(j, k) != (1, 3) or u == last,
+                             start=start, stop=stop)
 
         def add_steep(u, j, k, start):
             nc.tensor.matmul(out=block(u, j, k), lhsT=at(negative, u)[:, place(u, j, k, len(PLAIN))], rhs=steep_ident[:],

@@ -29,20 +29,23 @@ J = TOKENS // P
 GROUPS = SAMPLES // GROUP_SAMPLES
 HALF = SAMPLES // 2
 PLAIN = ((0, 0), (0, 1), (0, 2), (0, 3), (1, 0), (1, 1))
-BY_PRODUCT = ((1, 2), (1, 3))
+BY_PRODUCT = ((1, 3), (1, 2))
 BY_TURN = ()
 BLOCKS = PLAIN + BY_PRODUCT + BY_TURN
 ON_VECTOR = 0
 AHEAD = 3
 LAG = 1
-RAMP = 2
-PERIOD = 2
-PRELOADED = 8
+RAMP = 1
+FIRST_SORTED = 7
+BEFORE_QUANTISE = 3
+ON_SCALAR = 64
+SHARED_GROUPS = GROUPS - 6
+PRELOADED = 10
 
 
 def tile_modulatemlp_pa_kernel(tc, x, w_bytes, w_scale, weight, style_w, style_b, bias, out):
     nc = tc.nc
-    x_view = x.rearrange("n l c -> (n l) c").rearrange("(g j r) c -> g r j c", r=P, j=J)
+    x_view = x.rearrange("n l c -> (n l) c").rearrange("(t r) c -> r t c", r=P)
     out_view = out.rearrange("n l o -> (n l) o").rearrange("(g j r) o -> g r j o", r=P, j=J)
 
     with ExitStack() as ctx:
@@ -77,13 +80,19 @@ def tile_modulatemlp_pa_kernel(tc, x, w_bytes, w_scale, weight, style_w, style_b
         for h in range(2):
             nc.sync.dma_start(out=weight_sb[h][:], in_=weight_view[h])
 
-        x_sb = ring("x_sb", PRELOADED + 2, [P, J, C], BF16)
+        x_pairs = ring("x_pair", PRELOADED // 2 - 1, [P, 2 * J, C], BF16)
+        x_first = ring("x_first", 4, [P, J, C], BF16)
 
-        def load(u):
-            nc.sync.dma_start(out=at(x_sb, u)[:], in_=x_view[u])
+        def x_rows(u):
+            return x_first[u] if u < len(x_first) else at(x_pairs, u // 2)[:, u % 2 * J : (u % 2 + 1) * J, :]
 
-        for u in range(PRELOADED):
-            load(u)
+        def load_pair(u):
+            nc.sync.dma_start(out=at(x_pairs, u // 2)[:], in_=x_view[:, u * J : (u + 2) * J, :])
+
+        for u in range(len(x_first)):
+            nc.sync.dma_start(out=x_first[u][:], in_=x_view[:, u * J : (u + 1) * J, :])
+        for u in range(len(x_first), PRELOADED, 2):
+            load_pair(u)
 
         ident = keep.tile([P, P], F32)
         make_identity(nc, ident[:])
@@ -116,7 +125,8 @@ def tile_modulatemlp_pa_kernel(tc, x, w_bytes, w_scale, weight, style_w, style_b
         decoef = ring("decoef", 2, [P, PACK, HALF], F32)
         bias_gain = keep.tile([P, PACK], F32)
 
-        shared = ring("shared", 5, [P, J * O], F32)
+        shared = ring("shared", 4, [P, J * O], F32)
+        x_sorted = ring("x_sorted", 4, [P, C // 2], U32)
         codes = ring("codes", 4, [P, TOKENS], U32)
         scales = ring("scales", 4, [P, TOKENS], U8)
         z = ring("z", 3, [P, J * O], F32)
@@ -177,8 +187,19 @@ def tile_modulatemlp_pa_kernel(tc, x, w_bytes, w_scale, weight, style_w, style_b
             nc.scalar.activation(out=decoef[half][:].rearrange("p k n -> p (k n)")[:, cols], in_=bank[:, cols],
                                  func=ACT.Abs_reciprocal_sqrt, scale=0.5, bias=half_eps[:])
 
+        def sort_words(u):
+            nc.gpsimd.tensor_copy(out=at(x_sorted, u)[:].rearrange("p (u q) -> p u q", u=2),
+                                  in_=x_rows(u)[:, 0, :].bitcast(U32).rearrange("p (q u) -> p u q", u=2))
+
         def turn(u):
-            turn_rows(at(x_banks, u), at(x_sb, u))
+            if u < FIRST_SORTED:
+                turn_rows(at(x_banks, u), x_rows(u))
+                return
+            parts = at(x_banks, u)[:].rearrange("p (u j r) -> p u j r", u=2, j=2)
+            for half in range(2):
+                nc.tensor.transpose(parts[:, half, 0, :], at(x_sorted, u)[:, half * P : (half + 1) * P].bitcast(F32), ident[:])
+            for half in range(2):
+                nc.tensor.transpose(parts[:, half, 1, :], x_rows(u)[:, 1, :].bitcast(F32)[:, half::2], ident[:])
 
         def modulate(u, first=0, count=GROUP_SAMPLES):
             half, sample = divmod(u * GROUP_SAMPLES + first, HALF)
@@ -225,9 +246,6 @@ def tile_modulatemlp_pa_kernel(tc, x, w_bytes, w_scale, weight, style_w, style_b
                     nc.vector.tensor_scalar(out=dst, in0=src, scalar1=factor, scalar2=bias_gain[:, k : k + 1],
                                             op0=ALU.mult, op1=ALU.add)
 
-        def scalar_empties(u):
-            return u % PERIOD == PERIOD - 1 and u < GROUPS - 5
-
         def clip(u, cols):
             nc.gpsimd.tensor_scalar(out=clipped(u)[:, cols], in0=at(z, u)[:, cols],
                                     scalar1=CLAMP, scalar2=-CLAMP / SLOPE, op0=ALU.min, op1=ALU.max)
@@ -256,7 +274,7 @@ def tile_modulatemlp_pa_kernel(tc, x, w_bytes, w_scale, weight, style_w, style_b
                 if u == last or (j, k) in PLAIN:
                     turn_block(u, j, k, clipped(u)[:, place(u, j, k)], True, True)
                 else:
-                    source = clipped(u) if scalar_empties(u) else at(z, u)
+                    source = clipped(u) if k == 3 else at(z, u)
                     turn_block(u, j, k, source[:, place(u, j, k)], k == 2, k == 3)
 
         def plain_width(u, j):
@@ -266,16 +284,17 @@ def tile_modulatemlp_pa_kernel(tc, x, w_bytes, w_scale, weight, style_w, style_b
             width = plain_width(u, j)
             nc.scalar.activation(out=at(relu, J * u + j)[:, :width], in_=z_bank(u, j)[:, :width], func=ACT.Relu,
                                  scale=-(1.0 - SLOPE))
-            if width < O and scalar_empties(u):
-                nc.scalar.copy(out=finished[u][:, j, width:], in_=z_bank(u, j)[:, width:])
+            if width < O and u < SHARED_GROUPS:
+                nc.scalar.copy(out=at(finished, u)[:, j, O - ON_SCALAR :], in_=z_bank(u, j)[:, O - ON_SCALAR :])
 
         def finish(u, j):
             width = plain_width(u, j)
             bank = z_bank(u, j)
-            nc.vector.tensor_tensor(out=finished[u][:, j, :width], in0=bank[:, :width], in1=at(relu, J * u + j)[:, :width],
+            nc.vector.tensor_tensor(out=at(finished, u)[:, j, :width], in0=bank[:, :width], in1=at(relu, J * u + j)[:, :width],
                                     op=ALU.add)
-            if width < O and not scalar_empties(u):
-                nc.vector.tensor_scalar(out=finished[u][:, j, width:], in0=bank[:, width:],
+            if width < O:
+                end = O - ON_SCALAR if u < SHARED_GROUPS else O
+                nc.vector.tensor_scalar(out=at(finished, u)[:, j, width:end], in0=bank[:, width:end],
                                         scalar1=CLAMP, scalar2=-CLAMP, op0=ALU.min, op1=ALU.max)
 
         def store(u, tiles):
@@ -352,62 +371,67 @@ def tile_modulatemlp_pa_kernel(tc, x, w_bytes, w_scale, weight, style_w, style_b
             return len(parts) if u in (0, last - 1) else ON_VECTOR if u > 3 else 0
 
         def prepare(i):
+            if i + AHEAD + 1 <= last:
+                modulate(i + AHEAD + 1, 0, BEFORE_QUANTISE)
             if i + AHEAD <= last:
                 quantise(i + AHEAD)
             if i + AHEAD + 1 <= last:
-                modulate(i + AHEAD + 1)
+                modulate(i + AHEAD + 1, BEFORE_QUANTISE, GROUP_SAMPLES - BEFORE_QUANTISE)
 
         def clip_group(i):
             if i < last:
-                clip(i, slice(0, len(BLOCKS if scalar_empties(i) else PLAIN) * P))
                 take_negative(i)
+                clip(i, slice(0, (len(PLAIN) + 1) * P))
             elif i == last:
                 for j in range(J):
                     clip(i, slice(j * O, (j + 1) * O))
 
         for i in range(GROUPS + LAG + 1):
             g = i - LAG
-            if g >= 1:
-                turn_back(g - 1, 1, range(3, PACK))
-            if i < last:
-                demodulate(nc.scalar, 2 * i, parts[on_vector(i) :])
-                demodulate(nc.scalar, 2 * i + 1, parts)
-                if i == 1:
-                    take_root(1, z_banks[2], range(PACK))
-            elif i == last:
-                demodulate(nc.scalar, 2 * i + 1, by_tile)
-            clip_group(i)
-            if i < RAMP:
-                product(2 * i + 3)
-            if i + 4 <= last:
+            if RAMP <= i <= last - 4:
                 turn(i + 4)
             if 0 <= g <= last:
                 turn_back(g, 0, range(PACK))
+                turn_back(g, 1, range(3 if g < last else PACK))
+            if i < last:
+                if i != 2:
+                    demodulate(nc.scalar, 2 * i, parts[on_vector(i) :])
+                demodulate(nc.scalar, 2 * i + 1, parts)
+            elif i == last:
+                demodulate(nc.scalar, 2 * i + 1, by_tile)
+            clip_group(i)
+            if i == 1:
+                demodulate(nc.scalar, 4, parts)
+                take_root(1, z_banks[2], range(PACK))
+            if i + FIRST_SORTED <= last:
+                sort_words(i + FIRST_SORTED)
+            if i < RAMP:
+                product(2 * i + 3)
+                turn(i + 4)
             if g >= 1:
                 take_relu(g - 1, 1)
                 finish(g - 1, 1)
                 store(g - 1, slice(0, J) if g - 1 < last - 1 else slice(1, 2))
             if 0 <= g <= last:
                 take_relu(g, 0)
-            if i + PRELOADED <= last:
-                load(i + PRELOADED)
-            if 0 <= g <= last:
-                turn_back(g, 1, range(3))
-            if 0 <= g < last:
-                add_steep(g, 1, 2, start=False)
+            if i % 2 == 0 and i + PRELOADED <= last:
+                load_pair(i + PRELOADED)
             if i < RAMP:
                 prepare(i)
             if 0 <= g <= last:
                 finish(g, 0)
             if last - 1 <= g <= last:
                 store(g, slice(0, 1))
-            for q in (2 * i + 3, 2 * i + 4):
+            if 0 <= g < last:
+                add_steep(g, 1, 2, start=False)
+            for q in sorted((2 * i + 3, 2 * i + 4), reverse=i > 1):
                 if q < 2 * GROUPS and (i >= RAMP or q % 2 == 0):
                     product(q)
-            if i == 0:
-                d_product(1, z_banks[2], range(PACK))
             if 0 <= g < last:
                 add_steep(g, 1, 3, start=True)
+                turn_back(g, 1, range(3, PACK))
+            if i == 0:
+                d_product(1, z_banks[2], range(PACK))
             if i >= RAMP:
                 prepare(i)
             if i + 2 < last:

@@ -36,11 +36,10 @@ ON_VECTOR = 0
 AHEAD = 3
 LAG = 1
 RAMP = 1
-FIRST_SORTED = 7
-BEFORE_QUANTISE = 3
+BEFORE_QUANTISE = 2
 ON_SCALAR = 64
 SHARED_GROUPS = GROUPS - 6
-PRELOADED = 10
+PRELOADED = 8
 
 
 def tile_modulatemlp_pa_kernel(tc, x, w_bytes, w_scale, weight, style_w, style_b, bias, out):
@@ -125,8 +124,7 @@ def tile_modulatemlp_pa_kernel(tc, x, w_bytes, w_scale, weight, style_w, style_b
         decoef = ring("decoef", 2, [P, PACK, HALF], F32)
         bias_gain = keep.tile([P, PACK], F32)
 
-        shared = ring("shared", 4, [P, J * O], F32)
-        x_sorted = ring("x_sorted", 4, [P, C // 2], U32)
+        shared = ring("shared", 5, [P, J * O], F32)
         codes = ring("codes", 4, [P, TOKENS], U32)
         scales = ring("scales", 4, [P, TOKENS], U8)
         z = ring("z", 3, [P, J * O], F32)
@@ -187,19 +185,8 @@ def tile_modulatemlp_pa_kernel(tc, x, w_bytes, w_scale, weight, style_w, style_b
             nc.scalar.activation(out=decoef[half][:].rearrange("p k n -> p (k n)")[:, cols], in_=bank[:, cols],
                                  func=ACT.Abs_reciprocal_sqrt, scale=0.5, bias=half_eps[:])
 
-        def sort_words(u):
-            nc.gpsimd.tensor_copy(out=at(x_sorted, u)[:].rearrange("p (u q) -> p u q", u=2),
-                                  in_=x_rows(u)[:, 0, :].bitcast(U32).rearrange("p (q u) -> p u q", u=2))
-
         def turn(u):
-            if u < FIRST_SORTED:
-                turn_rows(at(x_banks, u), x_rows(u))
-                return
-            parts = at(x_banks, u)[:].rearrange("p (u j r) -> p u j r", u=2, j=2)
-            for half in range(2):
-                nc.tensor.transpose(parts[:, half, 0, :], at(x_sorted, u)[:, half * P : (half + 1) * P].bitcast(F32), ident[:])
-            for half in range(2):
-                nc.tensor.transpose(parts[:, half, 1, :], x_rows(u)[:, 1, :].bitcast(F32)[:, half::2], ident[:])
+            turn_rows(at(x_banks, u), x_rows(u))
 
         def modulate(u, first=0, count=GROUP_SAMPLES):
             half, sample = divmod(u * GROUP_SAMPLES + first, HALF)
@@ -380,8 +367,8 @@ def tile_modulatemlp_pa_kernel(tc, x, w_bytes, w_scale, weight, style_w, style_b
 
         def clip_group(i):
             if i < last:
-                take_negative(i)
                 clip(i, slice(0, (len(PLAIN) + 1) * P))
+                take_negative(i)
             elif i == last:
                 for j in range(J):
                     clip(i, slice(j * O, (j + 1) * O))
@@ -403,8 +390,6 @@ def tile_modulatemlp_pa_kernel(tc, x, w_bytes, w_scale, weight, style_w, style_b
             if i == 1:
                 demodulate(nc.scalar, 4, parts)
                 take_root(1, z_banks[2], range(PACK))
-            if i + FIRST_SORTED <= last:
-                sort_words(i + FIRST_SORTED)
             if i < RAMP:
                 product(2 * i + 3)
                 turn(i + 4)
@@ -424,7 +409,7 @@ def tile_modulatemlp_pa_kernel(tc, x, w_bytes, w_scale, weight, style_w, style_b
                 store(g, slice(0, 1))
             if 0 <= g < last:
                 add_steep(g, 1, 2, start=False)
-            for q in sorted((2 * i + 3, 2 * i + 4), reverse=i > 1):
+            for q in (2 * i + 3, 2 * i + 4):
                 if q < 2 * GROUPS and (i >= RAMP or q % 2 == 0):
                     product(q)
             if 0 <= g < last:

@@ -36,8 +36,9 @@ ON_VECTOR = 0
 AHEAD = 3
 LAG = 1
 RAMP = 1
-BEFORE_QUANTISE = 2
+BEFORE_QUANTISE = 1
 ON_SCALAR = 64
+THIRD_PRODUCT = set(range(3)) | set(range(GROUPS - 6, GROUPS - 1))
 SHARED_GROUPS = GROUPS - 6
 PRELOADED = 8
 
@@ -249,7 +250,7 @@ def tile_modulatemlp_pa_kernel(tc, x, w_bytes, w_scale, weight, style_w, style_b
             return z_bank(u, j)[:, k * P : (k + 1) * P]
 
         def turn_block(u, j, k, source, start, stop):
-            nc.tensor.matmul(out=block(u, j, k), lhsT=source, rhs=ident[:], is_transpose=(j, k) != (1, 3) or u == last,
+            nc.tensor.matmul(out=block(u, j, k), lhsT=source, rhs=ident[:], is_transpose=(j, k) != (1, 3) or u not in THIRD_PRODUCT,
                              start=start, stop=stop)
 
         def add_steep(u, j, k, start):
@@ -288,6 +289,7 @@ def tile_modulatemlp_pa_kernel(tc, x, w_bytes, w_scale, weight, style_w, style_b
             nc.sync.dma_start(out=out_view[u][:, tiles], in_=at(finished, u)[:, tiles])
 
         parts = [(e, n) for e in range(2) for n in range(GROUP_SAMPLES)]
+        clipped_first = [(0, 0), (0, 1), (1, 0), (1, 1), (1, 2), (1, 3), (0, 2), (0, 3)]
         by_tile = [(e, n) for n in range(GROUP_SAMPLES) for e in range(2)]
 
         nc.vector.tensor_copy(out=w_bf[:], in_=w_codes[:].bitcast(FP8))
@@ -375,6 +377,8 @@ def tile_modulatemlp_pa_kernel(tc, x, w_bytes, w_scale, weight, style_w, style_b
 
         for i in range(GROUPS + LAG + 1):
             g = i - LAG
+            if 0 <= g - 1 < last and g - 1 not in THIRD_PRODUCT:
+                turn_back(g - 1, 1, range(3, PACK))
             if RAMP <= i <= last - 4:
                 turn(i + 4)
             if 0 <= g <= last:
@@ -383,7 +387,7 @@ def tile_modulatemlp_pa_kernel(tc, x, w_bytes, w_scale, weight, style_w, style_b
             if i < last:
                 if i != 2:
                     demodulate(nc.scalar, 2 * i, parts[on_vector(i) :])
-                demodulate(nc.scalar, 2 * i + 1, parts)
+                demodulate(nc.scalar, 2 * i + 1, clipped_first)
             elif i == last:
                 demodulate(nc.scalar, 2 * i + 1, by_tile)
             clip_group(i)
@@ -414,6 +418,7 @@ def tile_modulatemlp_pa_kernel(tc, x, w_bytes, w_scale, weight, style_w, style_b
                     product(q)
             if 0 <= g < last:
                 add_steep(g, 1, 3, start=True)
+            if g in THIRD_PRODUCT:
                 turn_back(g, 1, range(3, PACK))
             if i == 0:
                 d_product(1, z_banks[2], range(PACK))

@@ -38,7 +38,7 @@ LAG = 1
 RAMP = 1
 BEFORE_QUANTISE = 1
 ON_SCALAR = 64
-THIRD_PRODUCT = set(range(3)) | set(range(GROUPS - 6, GROUPS - 1))
+THIRD_PRODUCT = set(range(GROUPS - 1))
 SHARED_GROUPS = GROUPS - 6
 PRELOADED = 8
 
@@ -382,8 +382,11 @@ def tile_modulatemlp_pa_kernel(tc, x, w_bytes, w_scale, weight, style_w, style_b
             if RAMP <= i <= last - 4:
                 turn(i + 4)
             if 0 <= g <= last:
+                if g < last:
+                    turn_back(g, 1, range(3))
                 turn_back(g, 0, range(PACK))
-                turn_back(g, 1, range(3 if g < last else PACK))
+                if g == last:
+                    turn_back(g, 1, range(PACK))
             if i < last:
                 if i != 2:
                     demodulate(nc.scalar, 2 * i, parts[on_vector(i) :])
@@ -413,11 +416,12 @@ def tile_modulatemlp_pa_kernel(tc, x, w_bytes, w_scale, weight, style_w, style_b
                 store(g, slice(0, 1))
             if 0 <= g < last:
                 add_steep(g, 1, 2, start=False)
-            for q in (2 * i + 3, 2 * i + 4):
-                if q < 2 * GROUPS and (i >= RAMP or q % 2 == 0):
-                    product(q)
+            if RAMP <= i and 2 * i + 3 < 2 * GROUPS:
+                product(2 * i + 3)
             if 0 <= g < last:
                 add_steep(g, 1, 3, start=True)
+            if 2 * i + 4 < 2 * GROUPS:
+                product(2 * i + 4)
             if g in THIRD_PRODUCT:
                 turn_back(g, 1, range(3, PACK))
             if i == 0:

@@ -28,19 +28,29 @@ TOKENS = GROUP_SAMPLES * POINTS
 J = TOKENS // P
 GROUPS = SAMPLES // GROUP_SAMPLES
 HALF = SAMPLES // 2
-PLAIN = ((0, 0), (0, 1), (0, 2), (0, 3), (1, 0), (1, 1))
-BY_PRODUCT = ((1, 3), (1, 2))
-BY_TURN = ()
-BLOCKS = PLAIN + BY_PRODUCT + BY_TURN
-ON_VECTOR = 0
+LAST = GROUPS - 1
+BLOCKS = J * PACK
 AHEAD = 3
-LAG = 1
-RAMP = 1
+PRELOADED = 8
+ALONE = 4
 BEFORE_QUANTISE = 1
 ON_SCALAR = 64
-THIRD_PRODUCT = set(range(GROUPS - 1))
 SHARED_GROUPS = GROUPS - 6
-PRELOADED = 8
+
+
+def plain_count(u):
+    return BLOCKS if u == LAST else BLOCKS - 1 - u % 2
+
+
+def scalar_helps(u):
+    return plain_count(u) == BLOCKS - 2 and u < SHARED_GROUPS
+
+
+def place(u, j, k, first=0):
+    number = j * PACK + k
+    if number >= plain_count(u):
+        number = plain_count(u) + BLOCKS - 1 - number
+    return slice((number - first) * P, (number - first + 1) * P)
 
 
 def tile_modulatemlp_pa_kernel(tc, x, w_bytes, w_scale, weight, style_w, style_b, bias, out):
@@ -80,18 +90,18 @@ def tile_modulatemlp_pa_kernel(tc, x, w_bytes, w_scale, weight, style_w, style_b
         for h in range(2):
             nc.sync.dma_start(out=weight_sb[h][:], in_=weight_view[h])
 
-        x_pairs = ring("x_pair", PRELOADED // 2 - 1, [P, 2 * J, C], BF16)
-        x_first = ring("x_first", 4, [P, J, C], BF16)
+        x_pairs = ring("x_pair", (PRELOADED - ALONE) // 2 + 1, [P, 2 * J, C], BF16)
+        x_alone = ring("x_alone", ALONE, [P, J, C], BF16)
 
         def x_rows(u):
-            return x_first[u] if u < len(x_first) else at(x_pairs, u // 2)[:, u % 2 * J : (u % 2 + 1) * J, :]
+            return x_alone[u] if u < ALONE else at(x_pairs, u // 2)[:, u % 2 * J : (u % 2 + 1) * J, :]
 
         def load_pair(u):
             nc.sync.dma_start(out=at(x_pairs, u // 2)[:], in_=x_view[:, u * J : (u + 2) * J, :])
 
-        for u in range(len(x_first)):
-            nc.sync.dma_start(out=x_first[u][:], in_=x_view[:, u * J : (u + 1) * J, :])
-        for u in range(len(x_first), PRELOADED, 2):
+        for u in range(ALONE):
+            nc.sync.dma_start(out=x_alone[u][:], in_=x_view[:, u * J : (u + 1) * J, :])
+        for u in range(ALONE, PRELOADED, 2):
             load_pair(u)
 
         ident = keep.tile([P, P], F32)
@@ -139,9 +149,9 @@ def tile_modulatemlp_pa_kernel(tc, x, w_bytes, w_scale, weight, style_w, style_b
         def clipped(u):
             return at(shared, u + AHEAD - 1)
 
-        def turn_rows(bank, rows):
+        def turn_rows(bank, rows, tiles=range(2)):
             parts = bank[:].rearrange("p (u j r) -> p u j r", u=2, j=2)
-            for j in range(2):
+            for j in tiles:
                 words = rows[:, j, :].bitcast(F32)
                 for u in range(2):
                     nc.tensor.transpose(parts[:, u, j, :], words[:, u::2], ident[:])
@@ -186,8 +196,8 @@ def tile_modulatemlp_pa_kernel(tc, x, w_bytes, w_scale, weight, style_w, style_b
             nc.scalar.activation(out=decoef[half][:].rearrange("p k n -> p (k n)")[:, cols], in_=bank[:, cols],
                                  func=ACT.Abs_reciprocal_sqrt, scale=0.5, bias=half_eps[:])
 
-        def turn(u):
-            turn_rows(at(x_banks, u), x_rows(u))
+        def turn(u, tiles=range(J)):
+            turn_rows(at(x_banks, u), x_rows(u), tiles)
 
         def modulate(u, first=0, count=GROUP_SAMPLES):
             half, sample = divmod(u * GROUP_SAMPLES + first, HALF)
@@ -211,12 +221,6 @@ def tile_modulatemlp_pa_kernel(tc, x, w_bytes, w_scale, weight, style_w, style_b
                                     lhsT_scale=weight_s[:, cols], rhs=at(codes, u)[:, tokens].bitcast(X4),
                                     rhs_scale=at(scales, u)[:, tokens], start=True, stop=True)
 
-        last = GROUPS - 1
-
-        def place(u, j, k, first=0):
-            number = BLOCKS.index((j, k)) if u < last else j * PACK + k
-            return slice((number - first) * P, (number - first + 1) * P)
-
         def demodulate(engine, q, parts, bank=None):
             u, h = divmod(q, 2)
             bank = at(y_banks, q + 1) if bank is None else bank
@@ -239,58 +243,50 @@ def tile_modulatemlp_pa_kernel(tc, x, w_bytes, w_scale, weight, style_w, style_b
                                     scalar1=CLAMP, scalar2=-CLAMP / SLOPE, op0=ALU.min, op1=ALU.max)
 
         def take_negative(u):
-            summed = (len(BLOCKS) - len(PLAIN)) * P
-            nc.gpsimd.tensor_scalar(out=at(negative, u)[:, :summed], in0=at(z, u)[:, len(PLAIN) * P :], scalar1=0.0,
+            first = plain_count(u) * P
+            nc.gpsimd.tensor_scalar(out=at(negative, u)[:, : BLOCKS * P - first], in0=at(z, u)[:, first:], scalar1=0.0,
                                     scalar2=-CLAMP / SLOPE, op0=ALU.min, op1=ALU.max)
 
         def z_bank(u, j):
-            return at(z_banks, J * u + j) if u < last else x_banks[j]
+            return at(z_banks, J * u + j) if u < LAST else x_banks[j]
 
-        def block(u, j, k):
-            return z_bank(u, j)[:, k * P : (k + 1) * P]
+        def turn_back(u, j, k, by_product=False):
+            plain = j * PACK + k < plain_count(u)
+            source = clipped(u) if plain or (k == 3 and scalar_helps(u)) else at(z, u)
+            nc.tensor.matmul(out=z_bank(u, j)[:, k * P : (k + 1) * P], lhsT=source[:, place(u, j, k)], rhs=ident[:],
+                             is_transpose=not by_product, start=plain or k == 2, stop=plain or k == 3)
 
-        def turn_block(u, j, k, source, start, stop):
-            nc.tensor.matmul(out=block(u, j, k), lhsT=source, rhs=ident[:], is_transpose=(j, k) != (1, 3) or u not in THIRD_PRODUCT,
-                             start=start, stop=stop)
-
-        def add_steep(u, j, k, start):
-            nc.tensor.matmul(out=block(u, j, k), lhsT=at(negative, u)[:, place(u, j, k, len(PLAIN))], rhs=steep_ident[:],
-                             start=start, stop=not start)
-
-        def turn_back(u, j, blocks):
-            for k in blocks:
-                if u == last or (j, k) in PLAIN:
-                    turn_block(u, j, k, clipped(u)[:, place(u, j, k)], True, True)
-                else:
-                    source = clipped(u) if k == 3 else at(z, u)
-                    turn_block(u, j, k, source[:, place(u, j, k)], k == 2, k == 3)
+        def add_steep(u, k):
+            nc.tensor.matmul(out=z_bank(u, 1)[:, k * P : (k + 1) * P], lhsT=at(negative, u)[:, place(u, 1, k, plain_count(u))],
+                             rhs=steep_ident[:], start=k == 3, stop=k == 2)
 
         def plain_width(u, j):
-            return O if u == last or j == 0 else 2 * P
+            return min(plain_count(u) * P - j * O, O)
 
         def take_relu(u, j):
             width = plain_width(u, j)
             nc.scalar.activation(out=at(relu, J * u + j)[:, :width], in_=z_bank(u, j)[:, :width], func=ACT.Relu,
                                  scale=-(1.0 - SLOPE))
-            if width < O and u < SHARED_GROUPS:
-                nc.scalar.copy(out=at(finished, u)[:, j, O - ON_SCALAR :], in_=z_bank(u, j)[:, O - ON_SCALAR :])
+            if j == 1 and scalar_helps(u):
+                nc.scalar.copy(out=finished[u][:, j, O - ON_SCALAR :], in_=z_bank(u, j)[:, O - ON_SCALAR :])
 
         def finish(u, j):
             width = plain_width(u, j)
             bank = z_bank(u, j)
-            nc.vector.tensor_tensor(out=at(finished, u)[:, j, :width], in0=bank[:, :width], in1=at(relu, J * u + j)[:, :width],
+            nc.vector.tensor_tensor(out=finished[u][:, j, :width], in0=bank[:, :width], in1=at(relu, J * u + j)[:, :width],
                                     op=ALU.add)
             if width < O:
-                end = O - ON_SCALAR if u < SHARED_GROUPS else O
-                nc.vector.tensor_scalar(out=at(finished, u)[:, j, width:end], in0=bank[:, width:end],
+                end = O - ON_SCALAR if scalar_helps(u) else O
+                nc.vector.tensor_scalar(out=finished[u][:, j, width:end], in0=bank[:, width:end],
                                         scalar1=CLAMP, scalar2=-CLAMP, op0=ALU.min, op1=ALU.max)
 
         def store(u, tiles):
-            nc.sync.dma_start(out=out_view[u][:, tiles], in_=at(finished, u)[:, tiles])
+            nc.sync.dma_start(out=out_view[u][:, tiles], in_=finished[u][:, tiles])
 
-        parts = [(e, n) for e in range(2) for n in range(GROUP_SAMPLES)]
-        clipped_first = [(0, 0), (0, 1), (1, 0), (1, 1), (1, 2), (1, 3), (0, 2), (0, 3)]
+        by_block = [(e, n) for e in range(2) for n in range(GROUP_SAMPLES)]
         by_tile = [(e, n) for n in range(GROUP_SAMPLES) for e in range(2)]
+        unclipped = [(0, n) for n in range(GROUP_SAMPLES // J, GROUP_SAMPLES)]
+        clipped_first = [part for part in by_block if part not in unclipped] + unclipped
 
         nc.vector.tensor_copy(out=w_bf[:], in_=w_codes[:].bitcast(FP8))
         w_bank = y_banks[2]
@@ -339,96 +335,98 @@ def tile_modulatemlp_pa_kernel(tc, x, w_bytes, w_scale, weight, style_w, style_b
         quantise_half(weight2_q, weight2_s, 1, weight2_t[1])
         quantise(0, slice(P, TOKENS))
         quantise_half(weight_q, weight_s, 1, weight_t[1])
+        turn(2)
         product(0, slice(P, TOKENS))
         d_product(0, z_banks[1], range(2, PACK))
         product(1)
         demodulate(nc.scalar, 0, by_tile[PACK:])
         take_root(0, z_banks[1], range(2, PACK))
-        turn(2)
         modulate(1)
         make_style(1)
         quantise(1)
-        product(2)
         turn(3)
+        product(2)
         square_style(1)
         modulate(2)
         quantise_style2(1)
         quantise(2)
         modulate(3)
 
-        def on_vector(u):
-            return len(parts) if u in (0, last - 1) else ON_VECTOR if u > 3 else 0
-
         def prepare(i):
-            if i + AHEAD + 1 <= last:
+            if i + AHEAD + 1 <= LAST:
                 modulate(i + AHEAD + 1, 0, BEFORE_QUANTISE)
-            if i + AHEAD <= last:
+            if i + AHEAD <= LAST:
                 quantise(i + AHEAD)
-            if i + AHEAD + 1 <= last:
+            if i + AHEAD + 1 <= LAST:
                 modulate(i + AHEAD + 1, BEFORE_QUANTISE, GROUP_SAMPLES - BEFORE_QUANTISE)
 
-        def clip_group(i):
-            if i < last:
-                clip(i, slice(0, (len(PLAIN) + 1) * P))
+        elsewhere = (0, 2, LAST - 1, LAST)
+
+        for i in range(GROUPS + 2):
+            g = i - 1
+            ahead = i + AHEAD + 1
+            summing = 0 <= g < LAST
+
+            if 0 < i and ahead <= LAST:
+                turn(ahead, range(1))
+            if 0 <= g <= LAST:
+                for k in range(PACK):
+                    turn_back(g, 0, k)
+                for k in range(PACK if g == LAST else 3 if plain_count(g) == BLOCKS - 2 else 2):
+                    turn_back(g, 1, k)
+            if 0 < i and ahead <= LAST:
+                turn(ahead, range(1, J))
+
+            if i <= LAST and i not in elsewhere:
+                demodulate(nc.scalar, 2 * i, by_block)
+            if i < LAST:
+                demodulate(nc.scalar, 2 * i + 1, clipped_first if plain_count(i) == BLOCKS - 2 else by_block)
+                clip(i, slice(0, (plain_count(i) + scalar_helps(i)) * P))
                 take_negative(i)
-            elif i == last:
+            elif i == LAST:
+                demodulate(nc.scalar, 2 * i + 1, by_tile)
                 for j in range(J):
                     clip(i, slice(j * O, (j + 1) * O))
-
-        for i in range(GROUPS + LAG + 1):
-            g = i - LAG
-            if 0 <= g - 1 < last and g - 1 not in THIRD_PRODUCT:
-                turn_back(g - 1, 1, range(3, PACK))
-            if RAMP <= i <= last - 4:
-                turn(i + 4)
-            if 0 <= g <= last:
-                if g < last:
-                    turn_back(g, 1, range(3))
-                turn_back(g, 0, range(PACK))
-                if g == last:
-                    turn_back(g, 1, range(PACK))
-            if i < last:
-                if i != 2:
-                    demodulate(nc.scalar, 2 * i, parts[on_vector(i) :])
-                demodulate(nc.scalar, 2 * i + 1, clipped_first)
-            elif i == last:
-                demodulate(nc.scalar, 2 * i + 1, by_tile)
-            clip_group(i)
+            if i == 0:
+                product(3)
+                turn(ahead)
             if i == 1:
-                demodulate(nc.scalar, 4, parts)
-                take_root(1, z_banks[2], range(PACK))
-            if i < RAMP:
-                product(2 * i + 3)
-                turn(i + 4)
+                demodulate(nc.scalar, 4, by_block)
+                take_root(1, style_bank, range(PACK))
+
             if g >= 1:
                 take_relu(g - 1, 1)
                 finish(g - 1, 1)
-                store(g - 1, slice(0, J) if g - 1 < last - 1 else slice(1, 2))
-            if 0 <= g <= last:
+                store(g - 1, slice(0, J) if g - 1 < LAST - 1 else slice(1, J))
+            if 0 <= g <= LAST:
                 take_relu(g, 0)
-            if i % 2 == 0 and i + PRELOADED <= last:
+            if i % 2 == 0 and i + PRELOADED <= LAST:
                 load_pair(i + PRELOADED)
-            if i < RAMP:
-                prepare(i)
-            if 0 <= g <= last:
+            if 0 <= g <= LAST:
                 finish(g, 0)
-            if last - 1 <= g <= last:
+            if LAST - 1 <= g <= LAST:
                 store(g, slice(0, 1))
-            if 0 <= g < last:
-                add_steep(g, 1, 2, start=False)
-            if RAMP <= i and 2 * i + 3 < 2 * GROUPS:
+            if i == 0:
+                prepare(i)
+
+            if summing and plain_count(g) == BLOCKS - 2:
+                add_steep(g, 2)
+            elif summing:
+                turn_back(g, 1, 2, by_product=True)
+            if 0 < i and 2 * i + 3 < 2 * GROUPS:
                 product(2 * i + 3)
-            if 0 <= g < last:
-                add_steep(g, 1, 3, start=True)
+            if summing:
+                add_steep(g, 3)
             if 2 * i + 4 < 2 * GROUPS:
                 product(2 * i + 4)
-            if g in THIRD_PRODUCT:
-                turn_back(g, 1, range(3, PACK))
+            if summing:
+                turn_back(g, 1, 3, by_product=True)
             if i == 0:
-                d_product(1, z_banks[2], range(PACK))
-            if i >= RAMP:
+                d_product(1, style_bank, range(PACK))
+
+            if i > 0:
                 prepare(i)
-            if i + 2 < last:
-                demodulate(nc.vector, 2 * i + 4, parts[: on_vector(i + 2)])
-            elif i + 2 == last:
-                demodulate(nc.vector, 2 * last, by_tile)
+            if i + 2 == LAST - 1:
+                demodulate(nc.vector, 2 * (i + 2), by_block)
+            elif i + 2 == LAST:
+                demodulate(nc.vector, 2 * (i + 2), by_tile)

@@ -27,36 +27,37 @@ GROUP_SAMPLES = 4
 TOKENS = GROUP_SAMPLES * POINTS
 J = TOKENS // P
 GROUPS = SAMPLES // GROUP_SAMPLES
+PAIRS = GROUPS // 2
 HALF = SAMPLES // 2
 LAST = GROUPS - 1
-BLOCKS = J * PACK
-AHEAD = 3
-PRELOADED = 8
-ALONE = 4
-BEFORE_QUANTISE = 1
-ON_SCALAR = 64
-SHARED_GROUPS = GROUPS - 6
-
-
-def plain_count(u):
-    return BLOCKS if u == LAST else BLOCKS - 1 - u % 2
-
-
-def scalar_helps(u):
-    return plain_count(u) == BLOCKS - 2 and u < SHARED_GROUPS
-
-
-def place(u, j, k, first=0):
-    number = j * PACK + k
-    if number >= plain_count(u):
-        number = plain_count(u) + BLOCKS - 1 - number
-    return slice((number - first) * P, (number - first + 1) * P)
+FIRST_RAW = 2
+LAST_RAW = PAIRS - 1
+EARLY_BANKS = 3
+EARLY_AT = (-1, -1, 0, 2)
+PLAIN_FROM = GROUPS - 2
+ON_VECTOR = (1, 2)
+VECTOR_FROM = 2
+RELU1_AT = 2
+RELU1_TAIL = 8
+RAW_TILES = 2 * EARLY_BANKS
+TAIL_VECTOR = (8, 8, 4)
+TAIL_FROM = GROUPS - 3
+FINE_FROM = 14
+SPARE_FROM = 26
+VCLIP_FROM = 64
+PROMPT_FROM = 30
+BY_MATMUL = 2
+BY_TURN = 0
+ON_SCALAR = 0
+COPY_UNTIL = 26
 
 
 def tile_modulatemlp_pa_kernel(tc, x, w_bytes, w_scale, weight, style_w, style_b, bias, out):
     nc = tc.nc
     x_view = x.rearrange("n l c -> (n l) c").rearrange("(t r) c -> r t c", r=P)
-    out_view = out.rearrange("n l o -> (n l) o").rearrange("(g j r) o -> g r j o", r=P, j=J)
+    out_view = out.rearrange("n l o -> (n l) o").rearrange("(t r) o -> r t o", r=P)
+    raw_pairs = range(FIRST_RAW, LAST_RAW + 1)
+    early_pairs = raw_pairs[: 2 * EARLY_BANKS]
 
     with ExitStack() as ctx:
         ctx.enter_context(tc.manual_schedule())
@@ -90,19 +91,36 @@ def tile_modulatemlp_pa_kernel(tc, x, w_bytes, w_scale, weight, style_w, style_b
         for h in range(2):
             nc.sync.dma_start(out=weight_sb[h][:], in_=weight_view[h])
 
-        x_pairs = ring("x_pair", (PRELOADED - ALONE) // 2 + 1, [P, 2 * J, C], BF16)
-        x_alone = ring("x_alone", ALONE, [P, J, C], BF16)
+        x_first = ring("x_first", 2, [P, J, C], BF16)
+        x_pairs = ring("x_pair", PAIRS, [P, 2 * J, C], BF16)
+        x_early = ring("x_early", EARLY_BANKS, [P, 2, C], BF16)
+        raw = ring("raw", RAW_TILES, [P, P * PACK], BF16)
 
-        def x_rows(u):
-            return x_alone[u] if u < ALONE else at(x_pairs, u // 2)[:, u % 2 * J : (u % 2 + 1) * J, :]
+        def own_tiles(p):
+            return 3 if p in raw_pairs else 4
 
-        def load_pair(u):
-            nc.sync.dma_start(out=at(x_pairs, u // 2)[:], in_=x_view[:, u * J : (u + 2) * J, :])
+        def x_rows(t):
+            p, j = divmod(t, 2 * J)
+            if p == 0:
+                return x_first[j // J][:, j % J, :]
+            if p in early_pairs and j == 3:
+                return x_early[(p - FIRST_RAW) // 2][:, (p - FIRST_RAW) % 2, :]
+            return x_pairs[p][:, j, :]
 
-        for u in range(ALONE):
-            nc.sync.dma_start(out=x_alone[u][:], in_=x_view[:, u * J : (u + 1) * J, :])
-        for u in range(ALONE, PRELOADED, 2):
-            load_pair(u)
+        def load_pair(p):
+            n = 3 if p in early_pairs else 4
+            nc.sync.dma_start(out=x_pairs[p][:, :n, :], in_=x_view[:, 4 * p : 4 * p + n, :])
+
+        def load_early(b):
+            first = 4 * (FIRST_RAW + 2 * b) + 3
+            nc.sync.dma_start(out=x_early[b][:], in_=x_view[:, first : first + 5 : 4, :])
+
+        for u in range(2):
+            nc.sync.dma_start(out=x_first[u][:], in_=x_view[:, u * J : (u + 1) * J, :])
+        for p in range(1, PAIRS):
+            if p <= EARLY_BANKS:
+                load_early(p - 1)
+            load_pair(p)
 
         ident = keep.tile([P, P], F32)
         make_identity(nc, ident[:])
@@ -135,39 +153,37 @@ def tile_modulatemlp_pa_kernel(tc, x, w_bytes, w_scale, weight, style_w, style_b
         decoef = ring("decoef", 2, [P, PACK, HALF], F32)
         bias_gain = keep.tile([P, PACK], F32)
 
-        shared = ring("shared", 5, [P, J * O], F32)
-        codes = ring("codes", 4, [P, TOKENS], U32)
-        scales = ring("scales", 4, [P, TOKENS], U8)
-        z = ring("z", 3, [P, J * O], F32)
-        negative = ring("negative", 3, [P, 2 * P], F32)
-        relu = ring("relu", 3, [P, O], F32)
-        finished = ring("finished", GROUPS, [P, J, O], F32)
+        modulated = keep.tile([P, 2 * TOKENS * PACK], BF16, align_bytes=64)
+        codes = ring("codes", 2, [P, 2 * TOKENS], U32)
+        scales = ring("scales", 2, [P, 2 * TOKENS], U8)
+        z = ring("z", 3, [P, 2 * J * O], F32)
+        negative = ring("negative", 2, [P, 2 * (BY_MATMUL + BY_TURN) * P], F32)
+        relu = ring("relu", 6, [P, O], F32)
+        finished = ring("finished", 6, [P, 2 * J * O], F32)
 
-        def modulated(u):
-            return at(shared, u)[:, : TOKENS * PACK // 2].bitcast(BF16)
-
-        def clipped(u):
-            return at(shared, u + AHEAD - 1)
-
-        def turn_rows(bank, rows, tiles=range(2)):
+        def turn_tile(bank, j, rows):
             parts = bank[:].rearrange("p (u j r) -> p u j r", u=2, j=2)
-            for j in tiles:
-                words = rows[:, j, :].bitcast(F32)
-                for u in range(2):
-                    nc.tensor.transpose(parts[:, u, j, :], words[:, u::2], ident[:])
+            words = rows.bitcast(F32)
+            for u in range(2):
+                nc.tensor.transpose(parts[:, u, j, :], words[:, u::2], ident[:])
+
+        def turn_rows(bank, rows):
+            for j in range(2):
+                turn_tile(bank, j, rows[:, j, :])
 
         def side_by_side(bank):
             return bank[:].bitcast(BF16).rearrange("p (u r e) -> p r u e", u=2, e=2)
 
-        def copy_words(engine_copy, dst, bank):
-            engine_copy(out=dst[:].bitcast(F32).rearrange("p (r u) -> p r u", u=2),
-                        in_=bank[:].rearrange("p (u r) -> p r u", u=2))
+        def copy_words(dst, bank, rows=slice(0, 2 * P)):
+            nc.scalar.copy(out=dst.bitcast(F32).rearrange("p (r u) -> p r u", u=2),
+                           in_=bank[:].rearrange("p (u r) -> p r u", u=2)[:, rows])
 
         def quantise_half(q, s, h, source):
             cols = slice(2 * P * h, 2 * P * (h + 1))
             nc.vector.quantize_mx(out=q[:, cols].bitcast(X4), scales=s[:, cols], in_=source[:])
 
         style_bank = z_banks[2]
+        style_bank2 = z_banks[1]
 
         def make_style(h):
             sums = style_bank[:].rearrange("p (t n) -> p n t", t=PACK)[:, h * HALF : (h + 1) * HALF, :]
@@ -196,30 +212,73 @@ def tile_modulatemlp_pa_kernel(tc, x, w_bytes, w_scale, weight, style_w, style_b
             nc.scalar.activation(out=decoef[half][:].rearrange("p k n -> p (k n)")[:, cols], in_=bank[:, cols],
                                  func=ACT.Abs_reciprocal_sqrt, scale=0.5, bias=half_eps[:])
 
-        def turn(u, tiles=range(J)):
-            turn_rows(at(x_banks, u), x_rows(u), tiles)
+        def turn_x(t):
+            turn_tile(at(x_banks, t // J), t % J, x_rows(t))
+
+        def turn_early(b):
+            turn_rows(at(z_banks[:2], b), x_early[b])
+
+        def copy_early(b):
+            for e in range(2):
+                copy_words(raw[2 * b + e][:], at(z_banks[:2], b), slice(e * P, (e + 1) * P))
 
         def modulate(u, first=0, count=GROUP_SAMPLES):
             half, sample = divmod(u * GROUP_SAMPLES + first, HALF)
             factors = style[half][:, sample : sample + count, :].rearrange("p n (u e) -> p n u e", e=2)
-            ns = slice(first, first + count)
+            place = u % 2 * GROUP_SAMPLES + first
             nc.vector.tensor_tensor(
-                out=modulated(u).rearrange("p (n l u e) -> p n l u e", n=GROUP_SAMPLES, u=2, e=2)[:, ns],
-                in0=side_by_side(at(x_banks, u)).rearrange("p (n l) u e -> p n l u e", n=GROUP_SAMPLES)[:, ns],
+                out=modulated[:].rearrange("p (n l u e) -> p n l u e", l=POINTS, u=2, e=2)[:, place : place + count],
+                in0=side_by_side(at(x_banks, u)).rearrange("p (n l) u e -> p n l u e", n=GROUP_SAMPLES)[:, first : first + count],
                 in1=factors.unsqueeze(2).to_broadcast([P, count, POINTS, 2, 2]), op=ALU.mult)
 
-        def quantise(u, tokens=slice(0, TOKENS)):
-            nc.vector.quantize_mx(out=at(codes, u)[:, tokens].bitcast(X4), scales=at(scales, u)[:, tokens],
-                                  in_=modulated(u)[:, tokens.start * PACK : tokens.stop * PACK])
+        def modulate_raw(p):
+            half, sample = divmod((2 * p + 1) * GROUP_SAMPLES + 2, HALF)
+            nc.gpsimd.tensor_tensor(
+                out=modulated[:, 3 * P * PACK :].rearrange("p (n l t) -> p n l t", n=2, t=PACK),
+                in0=at(raw, p - FIRST_RAW)[:].rearrange("p (n l t) -> p n l t", n=2, t=PACK),
+                in1=style[half][:, sample : sample + 2, :].unsqueeze(2).to_broadcast([P, 2, POINTS, PACK]), op=ALU.mult)
+
+        def quantise(p, tokens=slice(0, 2 * TOKENS)):
+            nc.vector.quantize_mx(out=at(codes, p)[:, tokens].bitcast(X4), scales=at(scales, p)[:, tokens],
+                                  in_=modulated[:, tokens.start * PACK : tokens.stop * PACK])
 
         def product(q, tokens=slice(0, TOKENS), bank=None):
             u, h = divmod(q, 2)
             bank = at(y_banks, q + 1) if bank is None else bank
+            moving = slice(u % 2 * TOKENS + tokens.start, u % 2 * TOKENS + tokens.stop)
             for e in range(2):
                 cols = slice((2 * h + e) * P, (2 * h + e + 1) * P)
                 nc.tensor.matmul_mx(out=bank[:, e * TOKENS : (e + 1) * TOKENS][:, tokens], lhsT=weight_q[:, cols].bitcast(X4),
-                                    lhsT_scale=weight_s[:, cols], rhs=at(codes, u)[:, tokens].bitcast(X4),
-                                    rhs_scale=at(scales, u)[:, tokens], start=True, stop=True)
+                                    lhsT_scale=weight_s[:, cols], rhs=at(codes, u // 2)[:, moving].bitcast(X4),
+                                    rhs_scale=at(scales, u // 2)[:, moving], start=True, stop=True)
+
+        def z_block(u, j, k):
+            first = ((j if u % 2 == 0 else 3 - j) * PACK + k) * P
+            return slice(first, first + P)
+
+        SUMMED = BY_MATMUL + BY_TURN
+        summed_start = J * O - SUMMED * P
+        scaled_start = BY_MATMUL * P
+
+        def summed(u):
+            if u >= PLAIN_FROM:
+                return ()
+            return tuple(range(PACK - SUMMED, PACK)) if u % 2 == 0 else tuple(range(SUMMED - 1, -1, -1))
+
+        def by_matmul(u):
+            return summed(u)[:BY_MATMUL]
+
+        def by_turn(u):
+            return summed(u)[BY_MATMUL:]
+
+        def part_of_tile(u, first, last):
+            return slice(first, last) if u % 2 == 0 else slice(O - last, O - first)
+
+        def plain_cols(u, j):
+            return part_of_tile(u, 0, O - len(summed(u)) * P if j else O)
+
+        def copied(u):
+            return ON_SCALAR if u < COPY_UNTIL else 0
 
         def demodulate(engine, q, parts, bank=None):
             u, h = divmod(q, 2)
@@ -229,7 +288,7 @@ def tile_modulatemlp_pa_kernel(tc, x, w_bytes, w_scale, weight, style_w, style_b
                 half, sample = divmod(u * GROUP_SAMPLES + n, HALF)
                 j, r = divmod(n * POINTS, P)
                 first = e * TOKENS + n * POINTS
-                dst = at(z, u)[:, place(u, j, k)][:, r : r + POINTS]
+                dst = at(z, u // 2)[:, z_block(u, j, k)][:, r : r + POINTS]
                 src = bank[:, first : first + POINTS]
                 factor = decoef[half][:, k, sample : sample + 1]
                 if engine is nc.scalar:
@@ -238,55 +297,104 @@ def tile_modulatemlp_pa_kernel(tc, x, w_bytes, w_scale, weight, style_w, style_b
                     nc.vector.tensor_scalar(out=dst, in0=src, scalar1=factor, scalar2=bias_gain[:, k : k + 1],
                                             op0=ALU.mult, op1=ALU.add)
 
-        def clip(u, cols):
-            nc.gpsimd.tensor_scalar(out=clipped(u)[:, cols], in0=at(z, u)[:, cols],
-                                    scalar1=CLAMP, scalar2=-CLAMP / SLOPE, op0=ALU.min, op1=ALU.max)
-
-        def take_negative(u):
-            first = plain_count(u) * P
-            nc.gpsimd.tensor_scalar(out=at(negative, u)[:, : BLOCKS * P - first], in0=at(z, u)[:, first:], scalar1=0.0,
+        def take_negative(p):
+            nc.gpsimd.tensor_scalar(out=at(negative, p)[:], in0=at(z, p)[:, summed_start : summed_start + 2 * SUMMED * P], scalar1=0.0,
                                     scalar2=-CLAMP / SLOPE, op0=ALU.min, op1=ALU.max)
+            if BY_TURN:
+                middle = at(negative, p)[:, scaled_start : scaled_start + 2 * BY_TURN * P]
+                nc.gpsimd.tensor_scalar(out=middle, in0=middle, scalar1=-(1.0 - SLOPE), scalar2=1.0, op0=ALU.mult, op1=ALU.mult)
 
         def z_bank(u, j):
-            return at(z_banks, J * u + j) if u < LAST else x_banks[j]
+            if u + j <= SPARE_FROM:
+                return at(z_banks, 2 * u + 2)
+            if j == 1 and summed(u):
+                return x_banks[u % 2]
+            return at(z_banks, u + SPARE_FROM + 3 + max(0, u - PLAIN_FROM) + j)
 
-        def turn_back(u, j, k, by_product=False):
-            plain = j * PACK + k < plain_count(u)
-            source = clipped(u) if plain or (k == 3 and scalar_helps(u)) else at(z, u)
-            nc.tensor.matmul(out=z_bank(u, j)[:, k * P : (k + 1) * P], lhsT=source[:, place(u, j, k)], rhs=ident[:],
-                             is_transpose=not by_product, start=plain or k == 2, stop=plain or k == 3)
+        def turn_back(u, j, k, start=True, stop=True):
+            nc.tensor.matmul(out=z_bank(u, j)[:, k * P : (k + 1) * P], lhsT=at(z, u // 2)[:, z_block(u, j, k)], rhs=ident[:],
+                             is_transpose=True, start=start, stop=stop)
 
-        def add_steep(u, k):
-            nc.tensor.matmul(out=z_bank(u, 1)[:, k * P : (k + 1) * P], lhsT=at(negative, u)[:, place(u, 1, k, plain_count(u))],
-                             rhs=steep_ident[:], start=k == 3, stop=k == 2)
+        def add_steep(u, k, start, stop):
+            first = z_block(u, 1, k).start - summed_start
+            turned = k in by_turn(u)
+            nc.tensor.matmul(out=z_bank(u, 1)[:, k * P : (k + 1) * P], lhsT=at(negative, u // 2)[:, first : first + P],
+                             rhs=ident[:] if turned else steep_ident[:], is_transpose=turned, start=start, stop=stop)
 
-        def plain_width(u, j):
-            return min(plain_count(u) * P - j * O, O)
+        def take_steep(u, j):
+            first = z_block(u, j, 0).start
+            nc.vector.tensor_scalar(out=relu_tile(u, j)[:], in0=at(z, u // 2)[:, first : first + O], scalar1=0.0,
+                                    scalar2=-(1.0 - SLOPE), op0=ALU.min, op1=ALU.mult)
+
+        def turn_both(u, j):
+            for k in range(PACK):
+                turn_back(u, j, k, stop=False)
+                nc.tensor.matmul(out=z_bank(u, j)[:, k * P : (k + 1) * P], lhsT=relu_tile(u, j)[:, k * P : (k + 1) * P],
+                                 rhs=ident[:], is_transpose=True, start=False, stop=True)
+
+        def finish_sum(u, j):
+            nc.vector.tensor_scalar(out=rows(u, j), in0=z_bank(u, j)[:], scalar1=CLAMP, scalar2=-CLAMP, op0=ALU.min, op1=ALU.max)
+            nc.sync.dma_start(out=out_view[:, J * u + j, :], in_=rows(u, j))
+
+        def batch(u, j):
+            return (u + 1) // 2 if j == 0 else u // 2 + 1
+
+        def rows(u, j):
+            place = 2 - u % 2 if j == 0 else 3 - u % 2 * 3
+            return at(finished, batch(u, j))[:, place * O : (place + 1) * O]
+
+        def relu_tile(u, j):
+            return at(relu, 2 * u + j)
 
         def take_relu(u, j):
-            width = plain_width(u, j)
-            nc.scalar.activation(out=at(relu, J * u + j)[:, :width], in_=z_bank(u, j)[:, :width], func=ACT.Relu,
-                                 scale=-(1.0 - SLOPE))
-            if j == 1 and scalar_helps(u):
-                nc.scalar.copy(out=finished[u][:, j, O - ON_SCALAR :], in_=z_bank(u, j)[:, O - ON_SCALAR :])
+            cols = plain_cols(u, j)
+            width = cols.stop - cols.start
+            if width:
+                nc.scalar.activation(out=relu_tile(u, j)[:, cols], in_=z_bank(u, j)[:, cols], func=ACT.Relu, scale=-(1.0 - SLOPE))
+            if width < O and copied(u):
+                cols = part_of_tile(u, width, width + copied(u))
+                nc.scalar.copy(out=rows(u, j)[:, cols], in_=z_bank(u, j)[:, cols])
 
         def finish(u, j):
-            width = plain_width(u, j)
+            cols = plain_cols(u, j)
+            width = cols.stop - cols.start
             bank = z_bank(u, j)
-            nc.vector.tensor_tensor(out=finished[u][:, j, :width], in0=bank[:, :width], in1=at(relu, J * u + j)[:, :width],
-                                    op=ALU.add)
+            if width:
+                nc.vector.tensor_tensor(out=rows(u, j)[:, cols], in0=bank[:, cols], in1=relu_tile(u, j)[:, cols], op=ALU.add)
             if width < O:
-                end = O - ON_SCALAR if scalar_helps(u) else O
-                nc.vector.tensor_scalar(out=finished[u][:, j, width:end], in0=bank[:, width:end],
+                other = part_of_tile(u, width + copied(u), O)
+                nc.vector.tensor_scalar(out=rows(u, j)[:, other], in0=bank[:, other],
                                         scalar1=CLAMP, scalar2=-CLAMP, op0=ALU.min, op1=ALU.max)
+                cols = part_of_tile(u, 0, width + copied(u))
+            if batch(u, j) >= FINE_FROM or batch(u, j) == 0:
+                clip(nc.vector if J * u + j >= VCLIP_FROM else nc.gpsimd, rows(u, j)[:, cols])
+                nc.sync.dma_start(out=out_view[:, J * u + j, :], in_=rows(u, j))
 
-        def store(u, tiles):
-            nc.sync.dma_start(out=out_view[u][:, tiles], in_=finished[u][:, tiles])
+        def clip(engine, tile):
+            engine.tensor_scalar(out=tile, in0=tile, scalar1=CLAMP, scalar2=-CLAMP, op0=ALU.min, op1=ALU.max)
+
+        def close_batch(b):
+            clip(nc.gpsimd, at(finished, b)[:, SUMMED * P - copied(2 * b - 1) : 2 * J * O - SUMMED * P + copied(2 * b - 2)])
+            tiles = at(finished, b)[:].rearrange("p (t o) -> p t o", o=O)
+            nc.sync.dma_start(out=out_view[:, 4 * b - 2 : 4 * b + 1 : 2, :], in_=tiles[:, 1:3, :])
+            nc.sync.dma_start(out=out_view[:, 4 * b - 3, :], in_=tiles[:, 3, :])
+            nc.sync.dma_start(out=out_view[:, 4 * b - 1, :], in_=tiles[:, 0, :])
 
         by_block = [(e, n) for e in range(2) for n in range(GROUP_SAMPLES)]
         by_tile = [(e, n) for n in range(GROUP_SAMPLES) for e in range(2)]
-        unclipped = [(0, n) for n in range(GROUP_SAMPLES // J, GROUP_SAMPLES)]
-        clipped_first = [part for part in by_block if part not in unclipped] + unclipped
+
+        def on_vector(u):
+            count = 0 if u < VECTOR_FROM else ON_VECTOR[u % 2] if u < TAIL_FROM else TAIL_VECTOR[u - TAIL_FROM]
+            return by_tile[:count]
+
+        def on_scalar(u):
+            first = [part for part in by_tile if part not in on_vector(u)]
+            if u % 2 and summed(u):
+                first = first[::-1]
+            if u == LAST:
+                return [(2 * u + h, (e, n)) for j in range(J) for h in range(2) for n in (2 * j, 2 * j + 1) for e in range(2)
+                        if h or (e, n) in first]
+            return [(2 * u, part) for part in first] + [(2 * u + 1, part) for part in by_tile]
 
         nc.vector.tensor_copy(out=w_bf[:], in_=w_codes[:].bitcast(FP8))
         w_bank = y_banks[2]
@@ -300,10 +408,10 @@ def tile_modulatemlp_pa_kernel(tc, x, w_bytes, w_scale, weight, style_w, style_b
             in0=w_bank[:, : 2 * P].bitcast(BF16).rearrange("p (u n e) -> p n u e", u=2, e=2),
             in1=w_scale_sb[:].rearrange("p (u e) -> p u e", e=2).unsqueeze(1).to_broadcast([P, SAMPLES, 2, 2]),
             op=ALU.mult)
-        copy_words(nc.scalar.copy, style_w_t[0], y_banks[0])
+        copy_words(style_w_t[0][:], y_banks[0])
         nc.vector.tensor_scalar(out=bias_rows[:PACK, :], in0=bias_sb[:], scalar1=GAIN, scalar2=None, op0=ALU.mult)
         nc.vector.quantize_mx(out=w_q[:].bitcast(X4), scales=w_s[:], in_=w_t[:].rearrange("p n k -> p (n k)"))
-        copy_words(nc.scalar.copy, style_w_t[1], y_banks[1])
+        copy_words(style_w_t[1][:], y_banks[1])
         for h in range(2):
             quantise_half(style_w_q, style_w_s, h, style_w_t[h])
         for h in range(2):
@@ -313,10 +421,10 @@ def tile_modulatemlp_pa_kernel(tc, x, w_bytes, w_scale, weight, style_w, style_b
             cols = slice(t * P, (t + 1) * P)
             nc.tensor.matmul_mx(out=style_bank[:, cols], lhsT=style_w_q[:, cols].bitcast(X4), lhsT_scale=style_w_s[:, cols],
                                 rhs=w_q[:].bitcast(X4), rhs_scale=w_s[:], start=True, stop=True)
-        turn(0)
-        turn(1)
+        for t in range(2 * J):
+            turn_x(t)
         for h in range(2):
-            copy_words(nc.scalar.copy, weight_t[h], z_banks[h])
+            copy_words(weight_t[h][:], z_banks[h])
         nc.scalar.activation(out=weight2_t[1][:], in_=weight_t[1][:], func=ACT.Square)
         nc.vector.tensor_copy(out=bias_gain[:], in_=w_bank[:, :PACK])
         nc.vector.tensor_tensor(out=weight2_t[0][:], in0=weight_t[0][:], in1=weight_t[0][:], op=ALU.mult)
@@ -324,109 +432,177 @@ def tile_modulatemlp_pa_kernel(tc, x, w_bytes, w_scale, weight, style_w, style_b
         make_style(0)
         quantise_half(weight2_q, weight2_s, 0, weight2_t[0])
         square_style(0)
+        early_now = [b for b in range(EARLY_BANKS) if EARLY_AT[b] < 0]
+        for b in early_now[:1]:
+            turn_early(b + 0)
+            copy_early(b + 0)
         modulate(0, 0, 2)
         quantise_style2(0)
         quantise(0, slice(0, P))
-        d_product(0, z_banks[0], range(0, 2))
+        d_product(0, z_banks[1], range(0, 2))
         product(0, slice(0, P), y_banks[0])
-        take_root(0, z_banks[0], range(0, 2))
+        take_root(0, z_banks[1], range(0, 2))
         demodulate(nc.scalar, 0, by_tile[:PACK], y_banks[0])
         modulate(0, 2, 2)
         quantise_half(weight2_q, weight2_s, 1, weight2_t[1])
         quantise(0, slice(P, TOKENS))
         quantise_half(weight_q, weight_s, 1, weight_t[1])
-        turn(2)
+        turn_x(4)
+        turn_x(5)
         product(0, slice(P, TOKENS))
-        d_product(0, z_banks[1], range(2, PACK))
+        d_product(0, z_banks[0], range(2, PACK))
         product(1)
         demodulate(nc.scalar, 0, by_tile[PACK:])
-        take_root(0, z_banks[1], range(2, PACK))
+        take_root(0, z_banks[0], range(2, PACK))
         modulate(1)
         make_style(1)
-        quantise(1)
-        turn(3)
+        quantise(0, slice(TOKENS, 2 * TOKENS))
+        for b in early_now[1:]:
+            turn_early(b)
+            copy_early(b)
+        turn_x(6)
+        turn_x(7)
         product(2)
         square_style(1)
         modulate(2)
         quantise_style2(1)
-        quantise(2)
+        quantise(1, slice(0, TOKENS))
         modulate(3)
 
-        def prepare(i):
-            if i + AHEAD + 1 <= LAST:
-                modulate(i + AHEAD + 1, 0, BEFORE_QUANTISE)
-            if i + AHEAD <= LAST:
-                quantise(i + AHEAD)
-            if i + AHEAD + 1 <= LAST:
-                modulate(i + AHEAD + 1, BEFORE_QUANTISE, GROUP_SAMPLES - BEFORE_QUANTISE)
-
-        elsewhere = (0, 2, LAST - 1, LAST)
-
-        for i in range(GROUPS + 2):
-            g = i - 1
-            ahead = i + AHEAD + 1
-            summing = 0 <= g < LAST
-
-            if 0 < i and ahead <= LAST:
-                turn(ahead, range(1))
-            if 0 <= g <= LAST:
-                for k in range(PACK):
-                    turn_back(g, 0, k)
-                for k in range(PACK if g == LAST else 3 if plain_count(g) == BLOCKS - 2 else 2):
-                    turn_back(g, 1, k)
-            if 0 < i and ahead <= LAST:
-                turn(ahead, range(1, J))
-
-            if i <= LAST and i not in elsewhere:
-                demodulate(nc.scalar, 2 * i, by_block)
-            if i < LAST:
-                demodulate(nc.scalar, 2 * i + 1, clipped_first if plain_count(i) == BLOCKS - 2 else by_block)
-                clip(i, slice(0, (plain_count(i) + scalar_helps(i)) * P))
-                take_negative(i)
-            elif i == LAST:
-                demodulate(nc.scalar, 2 * i + 1, by_tile)
-                for j in range(J):
-                    clip(i, slice(j * O, (j + 1) * O))
+        for i in range(PLAIN_FROM):
+            p = i // 2 + 2
+            even = i % 2 == 0
+            ahead = p + 1 if even else p + 2
+            late = ahead in raw_pairs and ahead not in early_pairs
+            if 0 <= i - 2:
+                finish(i - 2, 0)
             if i == 0:
+                quantise(1, slice(TOKENS, 2 * TOKENS))
                 product(3)
-                turn(ahead)
+            elif even and p - 1 < PAIRS:
+                quantise(p - 1)
+            if even and p in raw_pairs:
+                modulate_raw(p)
+            if i + 1 <= LAST:
+                demodulate(nc.vector, 2 * i + 2, on_vector(i + 1))
+
+            if 0 <= i - 3 and len(by_matmul(i - 3)) == 2:
+                turn_back(i - 3, 1, by_matmul(i - 3)[1], start=False)
+            if p < PAIRS:
+                for t in range(4 * p, 4 * p + 2) if even else range(4 * p + 2, 4 * p + own_tiles(p)):
+                    turn_x(t)
+                if late and not even:
+                    turn_tile(x_banks[1], 1, x_rows(4 * ahead + 3))
+            for b in range(EARLY_BANKS):
+                if EARLY_AT[b] == i:
+                    turn_early(b)
+            summing = 0 <= i - 2 and summed(i - 2)
+            first_tile = list(range(PACK)) if 0 <= i - 1 < PLAIN_FROM else []
+            turned = by_turn(i - 2) if summing else ()
+            for k in first_tile[len(turned) :]:
+                turn_back(i - 1, 0, k)
+            if summing:
+                for k in range(PACK):
+                    if k not in summed(i - 2):
+                        turn_back(i - 2, 1, k)
+                for n, k in enumerate(turned):
+                    turn_back(i - 2, 1, k, stop=False)
+                    turn_back(i - 1, 0, first_tile[n])
+                    add_steep(i - 2, k, False, True)
+                if BY_MATMUL:
+                    turn_back(i - 2, 1, by_matmul(i - 2)[0], stop=False)
+
+            parts = [] if i > LAST else on_scalar(i)[2 * PACK :] if i == 0 else on_scalar(i)
+            cut = len(parts) - 2 * PACK + (RELU1_AT if i < TAIL_FROM else RELU1_TAIL)
+            for q, part in parts[:cut]:
+                demodulate(nc.scalar, q, [part])
+            if not even and i <= LAST and summed(i):
+                take_negative(i // 2)
+            if 0 <= i - 3 and summed(i - 3):
+                take_relu(i - 3, 1)
+                finish(i - 3, 1)
+                if even and 0 < i // 2 - 1 < FINE_FROM:
+                    close_batch(i // 2 - 1)
+            if p < PAIRS:
+                modulate(2 * p, 0, 3) if even else modulate(2 * p, 3, 1)
+            if p < PAIRS and not even:
+                modulate(2 * p + 1, 0, 2 * own_tiles(p) - GROUP_SAMPLES)
+            for q, part in parts[cut:]:
+                demodulate(nc.scalar, q, [part])
+            for b in range(EARLY_BANKS):
+                if EARLY_AT[b] == i:
+                    copy_early(b)
             if i == 1:
-                demodulate(nc.scalar, 4, by_block)
-                take_root(1, style_bank, range(PACK))
+                take_root(1, style_bank2, range(PACK))
+            if 0 <= i - 1 < PLAIN_FROM:
+                take_relu(i - 1, 0)
+            if late and even:
+                copy_words(at(raw, p + 1 - FIRST_RAW)[:], x_banks[1], slice(P, 2 * P))
 
-            if g >= 1:
-                take_relu(g - 1, 1)
-                finish(g - 1, 1)
-                store(g - 1, slice(0, J) if g - 1 < LAST - 1 else slice(1, J))
-            if 0 <= g <= LAST:
-                take_relu(g, 0)
-            if i % 2 == 0 and i + PRELOADED <= LAST:
-                load_pair(i + PRELOADED)
-            if 0 <= g <= LAST:
-                finish(g, 0)
-            if LAST - 1 <= g <= LAST:
-                store(g, slice(0, 1))
-            if i == 0:
-                prepare(i)
-
-            if summing and plain_count(g) == BLOCKS - 2:
-                add_steep(g, 2)
-            elif summing:
-                turn_back(g, 1, 2, by_product=True)
             if 0 < i and 2 * i + 3 < 2 * GROUPS:
                 product(2 * i + 3)
-            if summing:
-                add_steep(g, 3)
+            if summing and BY_MATMUL:
+                add_steep(i - 2, summed(i - 2)[0], False, True)
             if 2 * i + 4 < 2 * GROUPS:
                 product(2 * i + 4)
-            if summing:
-                turn_back(g, 1, 3, by_product=True)
+            if summing and BY_MATMUL == 2:
+                add_steep(i - 2, summed(i - 2)[1], True, False)
             if i == 0:
-                d_product(1, style_bank, range(PACK))
+                d_product(1, style_bank2, range(PACK))
 
-            if i > 0:
-                prepare(i)
-            if i + 2 == LAST - 1:
-                demodulate(nc.vector, 2 * (i + 2), by_block)
-            elif i + 2 == LAST:
-                demodulate(nc.vector, 2 * (i + 2), by_tile)
+        def open_tile(u):
+            for k in range(PACK):
+                if k not in summed(u):
+                    turn_back(u, 1, k)
+            turn_back(u, 1, summed(u)[0], stop=False)
+
+        def sum_tile(u):
+            add_steep(u, summed(u)[0], False, True)
+            add_steep(u, summed(u)[1], True, False)
+
+        def close_tile(u):
+            turn_back(u, 1, summed(u)[1], start=False)
+
+        def turn_plain(u, j):
+            for k in range(PACK):
+                turn_back(u, j, k)
+
+        def scalar_parts(u, first, last):
+            for q, part in on_scalar(u)[first:last]:
+                demodulate(nc.scalar, q, [part])
+
+        u = PLAIN_FROM
+        finish(u - 2, 0)
+        close_tile(u - 3)
+        turn_plain(u - 1, 0)
+        open_tile(u - 2)
+        scalar_parts(u, 0, None)
+        demodulate(nc.vector, 2 * u + 2, on_vector(u + 1))
+        take_relu(u - 3, 1)
+        finish(u - 3, 1)
+        product(2 * u + 3)
+        sum_tile(u - 2)
+        take_relu(u - 1, 0)
+        close_tile(u - 2)
+        turn_plain(u, 0)
+        open_tile(u - 1)
+        scalar_parts(u + 1, 0, -2 * PACK)
+        finish(u - 1, 0)
+        sum_tile(u - 1)
+        take_relu(u - 2, 1)
+        close_tile(u - 1)
+        turn_plain(u, 1)
+        finish(u - 2, 1)
+        take_relu(u, 0)
+        turn_plain(u + 1, 0)
+        scalar_parts(u + 1, -2 * PACK, None)
+        finish(u, 0)
+        take_relu(u - 1, 1)
+        take_steep(u + 1, 1)
+        take_relu(u, 1)
+        finish(u - 1, 1)
+        turn_both(u + 1, 1)
+        take_relu(u + 1, 0)
+        finish(u, 1)
+        finish(u + 1, 0)
+        finish_sum(u + 1, 1)

@@ -30,21 +30,20 @@ GROUPS = SAMPLES // GROUP_SAMPLES
 PAIRS = GROUPS // 2
 HALF = SAMPLES // 2
 LAST = GROUPS - 1
-FIRST_RAW = 2
+FIRST_RAW = 1
 LAST_RAW = PAIRS - 1
 EARLY_BANKS = 3
-EARLY_AT = (-1, -1, 0, 2)
 PLAIN_FROM = GROUPS - 2
 ON_VECTOR = (1, 2)
-VECTOR_FROM = 2
-RELU1_AT = 2
+RAMP_VECTOR = (8, 4)
+RELU1_AT = 0
 RELU1_TAIL = 8
 RAW_TILES = 2 * EARLY_BANKS
-TAIL_VECTOR = (8, 8, 4)
+TAIL_VECTOR = (6, 8, 8)
 TAIL_FROM = GROUPS - 3
 FINE_FROM = 14
 SPARE_FROM = 26
-VCLIP_FROM = 64
+VCLIP_FROM = 62
 PROMPT_FROM = 30
 BY_MATMUL = 2
 BY_TURN = 0
@@ -174,8 +173,8 @@ def tile_modulatemlp_pa_kernel(tc, x, w_bytes, w_scale, weight, style_w, style_b
         def side_by_side(bank):
             return bank[:].bitcast(BF16).rearrange("p (u r e) -> p r u e", u=2, e=2)
 
-        def copy_words(dst, bank, rows=slice(0, 2 * P)):
-            nc.scalar.copy(out=dst.bitcast(F32).rearrange("p (r u) -> p r u", u=2),
+        def copy_words(engine_copy, dst, bank, rows=slice(0, 2 * P)):
+            engine_copy(out=dst.bitcast(F32).rearrange("p (r u) -> p r u", u=2),
                            in_=bank[:].rearrange("p (u r) -> p r u", u=2)[:, rows])
 
         def quantise_half(q, s, h, source):
@@ -215,12 +214,14 @@ def tile_modulatemlp_pa_kernel(tc, x, w_bytes, w_scale, weight, style_w, style_b
         def turn_x(t):
             turn_tile(at(x_banks, t // J), t % J, x_rows(t))
 
-        def turn_early(b):
-            turn_rows(at(z_banks[:2], b), x_early[b])
+        early_banks = [y_banks[2], z_banks[0], z_banks[1]]
 
-        def copy_early(b):
-            for e in range(2):
-                copy_words(raw[2 * b + e][:], at(z_banks[:2], b), slice(e * P, (e + 1) * P))
+        def turn_early(b):
+            turn_rows(early_banks[b], x_early[b])
+
+        def copy_early(b, tiles=range(2)):
+            for e in tiles:
+                copy_words(nc.scalar.copy, raw[2 * b + e][:], early_banks[b], slice(e * P, (e + 1) * P))
 
         def modulate(u, first=0, count=GROUP_SAMPLES):
             half, sample = divmod(u * GROUP_SAMPLES + first, HALF)
@@ -321,8 +322,12 @@ def tile_modulatemlp_pa_kernel(tc, x, w_bytes, w_scale, weight, style_w, style_b
             nc.tensor.matmul(out=z_bank(u, 1)[:, k * P : (k + 1) * P], lhsT=at(negative, u // 2)[:, first : first + P],
                              rhs=ident[:] if turned else steep_ident[:], is_transpose=turned, start=start, stop=stop)
 
-        def take_steep(u, j):
+        def take_steep(u, j, engine=nc.vector):
             first = z_block(u, j, 0).start
+            if engine is nc.scalar:
+                nc.scalar.activation(out=relu_tile(u, j)[:], in_=at(z, u // 2)[:, first : first + O], func=ACT.Relu,
+                                     scale=-(1.0 - SLOPE))
+                return
             nc.vector.tensor_scalar(out=relu_tile(u, j)[:], in0=at(z, u // 2)[:, first : first + O], scalar1=0.0,
                                     scalar2=-(1.0 - SLOPE), op0=ALU.min, op1=ALU.mult)
 
@@ -384,7 +389,7 @@ def tile_modulatemlp_pa_kernel(tc, x, w_bytes, w_scale, weight, style_w, style_b
         by_tile = [(e, n) for n in range(GROUP_SAMPLES) for e in range(2)]
 
         def on_vector(u):
-            count = 0 if u < VECTOR_FROM else ON_VECTOR[u % 2] if u < TAIL_FROM else TAIL_VECTOR[u - TAIL_FROM]
+            count = 0 if u < 2 else RAMP_VECTOR[u - 2] if u < 2 + len(RAMP_VECTOR) else ON_VECTOR[u % 2] if u < TAIL_FROM else TAIL_VECTOR[u - TAIL_FROM]
             return by_tile[:count]
 
         def on_scalar(u):
@@ -408,66 +413,61 @@ def tile_modulatemlp_pa_kernel(tc, x, w_bytes, w_scale, weight, style_w, style_b
             in0=w_bank[:, : 2 * P].bitcast(BF16).rearrange("p (u n e) -> p n u e", u=2, e=2),
             in1=w_scale_sb[:].rearrange("p (u e) -> p u e", e=2).unsqueeze(1).to_broadcast([P, SAMPLES, 2, 2]),
             op=ALU.mult)
-        copy_words(style_w_t[0][:], y_banks[0])
+        copy_words(nc.scalar.copy, style_w_t[0][:], y_banks[0])
         nc.vector.tensor_scalar(out=bias_rows[:PACK, :], in0=bias_sb[:], scalar1=GAIN, scalar2=None, op0=ALU.mult)
         nc.vector.quantize_mx(out=w_q[:].bitcast(X4), scales=w_s[:], in_=w_t[:].rearrange("p n k -> p (n k)"))
-        copy_words(style_w_t[1][:], y_banks[1])
-        for h in range(2):
-            quantise_half(style_w_q, style_w_s, h, style_w_t[h])
+        copy_words(nc.scalar.copy, style_w_t[1][:], y_banks[1])
+        nc.tensor.transpose(w_bank[:, :P], bias_rows[:], ident[:])
+        quantise_half(style_w_q, style_w_s, 0, style_w_t[0])
+        nc.vector.tensor_copy(out=bias_gain[:], in_=w_bank[:, :PACK])
+        quantise_half(style_w_q, style_w_s, 1, style_w_t[1])
         for h in range(2):
             turn_rows(z_banks[h], weight_sb[h])
-        nc.tensor.transpose(w_bank[:, :P], bias_rows[:], ident[:])
         for t in range(PACK):
             cols = slice(t * P, (t + 1) * P)
             nc.tensor.matmul_mx(out=style_bank[:, cols], lhsT=style_w_q[:, cols].bitcast(X4), lhsT_scale=style_w_s[:, cols],
                                 rhs=w_q[:].bitcast(X4), rhs_scale=w_s[:], start=True, stop=True)
         for t in range(2 * J):
             turn_x(t)
+        turn_early(0)
         for h in range(2):
-            copy_words(weight_t[h][:], z_banks[h])
+            copy_words(nc.scalar.copy, weight_t[h][:], z_banks[h])
         nc.scalar.activation(out=weight2_t[1][:], in_=weight_t[1][:], func=ACT.Square)
-        nc.vector.tensor_copy(out=bias_gain[:], in_=w_bank[:, :PACK])
         nc.vector.tensor_tensor(out=weight2_t[0][:], in0=weight_t[0][:], in1=weight_t[0][:], op=ALU.mult)
         quantise_half(weight_q, weight_s, 0, weight_t[0])
         make_style(0)
         quantise_half(weight2_q, weight2_s, 0, weight2_t[0])
         square_style(0)
-        early_now = [b for b in range(EARLY_BANKS) if EARLY_AT[b] < 0]
-        for b in early_now[:1]:
-            turn_early(b + 0)
-            copy_early(b + 0)
         modulate(0, 0, 2)
         quantise_style2(0)
         quantise(0, slice(0, P))
-        d_product(0, z_banks[1], range(0, 2))
+        d_product(0, z_banks[0], range(0, 2))
         product(0, slice(0, P), y_banks[0])
-        take_root(0, z_banks[1], range(0, 2))
+        copy_early(0)
+        take_root(0, z_banks[0], range(0, 2))
         demodulate(nc.scalar, 0, by_tile[:PACK], y_banks[0])
         modulate(0, 2, 2)
         quantise_half(weight2_q, weight2_s, 1, weight2_t[1])
         quantise(0, slice(P, TOKENS))
         quantise_half(weight_q, weight_s, 1, weight_t[1])
+        product(0, slice(P, TOKENS))
+        d_product(0, z_banks[1], range(2, PACK))
+        product(1)
         turn_x(4)
         turn_x(5)
-        product(0, slice(P, TOKENS))
-        d_product(0, z_banks[0], range(2, PACK))
-        product(1)
         demodulate(nc.scalar, 0, by_tile[PACK:])
-        take_root(0, z_banks[0], range(2, PACK))
+        take_root(0, z_banks[1], range(2, PACK))
         modulate(1)
         make_style(1)
         quantise(0, slice(TOKENS, 2 * TOKENS))
-        for b in early_now[1:]:
-            turn_early(b)
-            copy_early(b)
+        modulate_raw(1)
         turn_x(6)
-        turn_x(7)
         product(2)
-        square_style(1)
+        product(3)
+        turn_early(1)
         modulate(2)
-        quantise_style2(1)
-        quantise(1, slice(0, TOKENS))
-        modulate(3)
+        modulate(3, 0, 2)
+        square_style(1)
 
         for i in range(PLAIN_FROM):
             p = i // 2 + 2
@@ -476,25 +476,22 @@ def tile_modulatemlp_pa_kernel(tc, x, w_bytes, w_scale, weight, style_w, style_b
             late = ahead in raw_pairs and ahead not in early_pairs
             if 0 <= i - 2:
                 finish(i - 2, 0)
-            if i == 0:
-                quantise(1, slice(TOKENS, 2 * TOKENS))
-                product(3)
-            elif even and p - 1 < PAIRS:
+            if even and p - 1 < PAIRS:
                 quantise(p - 1)
+            if i == 0:
+                quantise_style2(1)
             if even and p in raw_pairs:
                 modulate_raw(p)
             if i + 1 <= LAST:
                 demodulate(nc.vector, 2 * i + 2, on_vector(i + 1))
 
-            if 0 <= i - 3 and len(by_matmul(i - 3)) == 2:
-                turn_back(i - 3, 1, by_matmul(i - 3)[1], start=False)
             if p < PAIRS:
                 for t in range(4 * p, 4 * p + 2) if even else range(4 * p + 2, 4 * p + own_tiles(p)):
                     turn_x(t)
                 if late and not even:
                     turn_tile(x_banks[1], 1, x_rows(4 * ahead + 3))
-            for b in range(EARLY_BANKS):
-                if EARLY_AT[b] == i:
+            if i < 1:
+                for b in range(2, EARLY_BANKS):
                     turn_early(b)
             summing = 0 <= i - 2 and summed(i - 2)
             first_tile = list(range(PACK)) if 0 <= i - 1 < PLAIN_FROM else []
@@ -509,13 +506,15 @@ def tile_modulatemlp_pa_kernel(tc, x, w_bytes, w_scale, weight, style_w, style_b
                     turn_back(i - 2, 1, k, stop=False)
                     turn_back(i - 1, 0, first_tile[n])
                     add_steep(i - 2, k, False, True)
-                if BY_MATMUL:
-                    turn_back(i - 2, 1, by_matmul(i - 2)[0], stop=False)
+                for k in by_matmul(i - 2):
+                    turn_back(i - 2, 1, k, start=k == by_matmul(i - 2)[0], stop=False)
 
             parts = [] if i > LAST else on_scalar(i)[2 * PACK :] if i == 0 else on_scalar(i)
             cut = len(parts) - 2 * PACK + (RELU1_AT if i < TAIL_FROM else RELU1_TAIL)
             for q, part in parts[:cut]:
                 demodulate(nc.scalar, q, [part])
+            if i == 1:
+                copy_early(1)
             if not even and i <= LAST and summed(i):
                 take_negative(i // 2)
             if 0 <= i - 3 and summed(i - 3):
@@ -529,39 +528,36 @@ def tile_modulatemlp_pa_kernel(tc, x, w_bytes, w_scale, weight, style_w, style_b
                 modulate(2 * p + 1, 0, 2 * own_tiles(p) - GROUP_SAMPLES)
             for q, part in parts[cut:]:
                 demodulate(nc.scalar, q, [part])
-            for b in range(EARLY_BANKS):
-                if EARLY_AT[b] == i:
-                    copy_early(b)
-            if i == 1:
-                take_root(1, style_bank2, range(PACK))
+            if i == 1 and EARLY_BANKS > 2:
+                copy_early(2)
+            if i == 2:
+                take_root(1, z_banks[0], range(PACK))
             if 0 <= i - 1 < PLAIN_FROM:
                 take_relu(i - 1, 0)
             if late and even:
-                copy_words(at(raw, p + 1 - FIRST_RAW)[:], x_banks[1], slice(P, 2 * P))
+                copy_words(nc.scalar.copy, at(raw, p + 1 - FIRST_RAW)[:], x_banks[1], slice(P, 2 * P))
 
             if 0 < i and 2 * i + 3 < 2 * GROUPS:
                 product(2 * i + 3)
             if summing and BY_MATMUL:
-                add_steep(i - 2, summed(i - 2)[0], False, True)
+                add_steep(i - 2, summed(i - 2)[0], False, False)
             if 2 * i + 4 < 2 * GROUPS:
                 product(2 * i + 4)
             if summing and BY_MATMUL == 2:
-                add_steep(i - 2, summed(i - 2)[1], True, False)
-            if i == 0:
-                d_product(1, style_bank2, range(PACK))
+                add_steep(i - 2, summed(i - 2)[1], False, True)
+            if i == 1:
+                d_product(1, z_banks[0], range(PACK))
 
         def open_tile(u):
             for k in range(PACK):
                 if k not in summed(u):
                     turn_back(u, 1, k)
-            turn_back(u, 1, summed(u)[0], stop=False)
+            for k in summed(u):
+                turn_back(u, 1, k, start=k == summed(u)[0], stop=False)
 
         def sum_tile(u):
-            add_steep(u, summed(u)[0], False, True)
-            add_steep(u, summed(u)[1], True, False)
-
-        def close_tile(u):
-            turn_back(u, 1, summed(u)[1], start=False)
+            for k in summed(u):
+                add_steep(u, k, False, k == summed(u)[-1])
 
         def turn_plain(u, j):
             for k in range(PACK):
@@ -573,36 +569,33 @@ def tile_modulatemlp_pa_kernel(tc, x, w_bytes, w_scale, weight, style_w, style_b
 
         u = PLAIN_FROM
         finish(u - 2, 0)
-        close_tile(u - 3)
         turn_plain(u - 1, 0)
         open_tile(u - 2)
         scalar_parts(u, 0, None)
-        demodulate(nc.vector, 2 * u + 2, on_vector(u + 1))
+        demodulate(nc.vector, 2 * u + 2, by_tile)
         take_relu(u - 3, 1)
         finish(u - 3, 1)
         product(2 * u + 3)
         sum_tile(u - 2)
         take_relu(u - 1, 0)
-        close_tile(u - 2)
-        turn_plain(u, 0)
+        take_steep(u, 0, nc.scalar)
         open_tile(u - 1)
-        scalar_parts(u + 1, 0, -2 * PACK)
+        turn_both(u, 0)
         finish(u - 1, 0)
-        sum_tile(u - 1)
+        demodulate(nc.vector, 2 * u + 3, by_tile[:PACK])
+        take_steep(u, 1, nc.scalar)
         take_relu(u - 2, 1)
-        close_tile(u - 1)
-        turn_plain(u, 1)
+        sum_tile(u - 1)
+        demodulate(nc.scalar, 2 * u + 3, by_tile[PACK:])
         finish(u - 2, 1)
-        take_relu(u, 0)
-        turn_plain(u + 1, 0)
-        scalar_parts(u + 1, -2 * PACK, None)
-        finish(u, 0)
+        turn_both(u, 1)
+        finish_sum(u, 0)
+        take_steep(u + 1, 0, nc.scalar)
         take_relu(u - 1, 1)
-        take_steep(u + 1, 1)
-        take_relu(u, 1)
+        take_steep(u + 1, 1, nc.scalar)
+        turn_both(u + 1, 0)
         finish(u - 1, 1)
+        finish_sum(u, 1)
         turn_both(u + 1, 1)
-        take_relu(u + 1, 0)
-        finish(u, 1)
-        finish(u + 1, 0)
+        finish_sum(u + 1, 0)
         finish_sum(u + 1, 1)

@@ -34,7 +34,7 @@ FIRST_RAW = 1
 LAST_RAW = PAIRS - 1
 EARLY_BANKS = 3
 PLAIN_FROM = GROUPS - 2
-ON_VECTOR = (1, 2)
+ON_VECTOR = (2, 3)
 RAMP_VECTOR = (8, 4)
 RELU1_AT = 0
 RELU1_TAIL = 8
@@ -43,9 +43,10 @@ TAIL_VECTOR = (6, 8, 8)
 TAIL_FROM = GROUPS - 3
 FINE_FROM = 14
 SPARE_FROM = 26
-VCLIP_FROM = 62
+VCLIP_FROM = 63
 PROMPT_FROM = 30
-BY_MATMUL = 2
+BY_MATMUL = 1
+PRODUCT_EVERY = 1
 BY_TURN = 0
 ON_SCALAR = 0
 COPY_UNTIL = 26
@@ -272,6 +273,9 @@ def tile_modulatemlp_pa_kernel(tc, x, w_bytes, w_scale, weight, style_w, style_b
         def by_turn(u):
             return summed(u)[BY_MATMUL:]
 
+        def by_product(u):
+            return 0 if u % 2 == 0 else PACK - 1
+
         def part_of_tile(u, first, last):
             return slice(first, last) if u % 2 == 0 else slice(O - last, O - first)
 
@@ -310,11 +314,13 @@ def tile_modulatemlp_pa_kernel(tc, x, w_bytes, w_scale, weight, style_w, style_b
                 return at(z_banks, 2 * u + 2)
             if j == 1 and summed(u):
                 return x_banks[u % 2]
+            if (u, j) == (LAST, 1):
+                return y_banks[2]
             return at(z_banks, u + SPARE_FROM + 3 + max(0, u - PLAIN_FROM) + j)
 
-        def turn_back(u, j, k, start=True, stop=True):
+        def turn_back(u, j, k, start=True, stop=True, as_product=False):
             nc.tensor.matmul(out=z_bank(u, j)[:, k * P : (k + 1) * P], lhsT=at(z, u // 2)[:, z_block(u, j, k)], rhs=ident[:],
-                             is_transpose=True, start=start, stop=stop)
+                             is_transpose=not as_product, start=start, stop=stop)
 
         def add_steep(u, k, start, stop):
             first = z_block(u, 1, k).start - summed_start
@@ -371,19 +377,25 @@ def tile_modulatemlp_pa_kernel(tc, x, w_bytes, w_scale, weight, style_w, style_b
                 nc.vector.tensor_scalar(out=rows(u, j)[:, other], in0=bank[:, other],
                                         scalar1=CLAMP, scalar2=-CLAMP, op0=ALU.min, op1=ALU.max)
                 cols = part_of_tile(u, 0, width + copied(u))
-            if batch(u, j) >= FINE_FROM or batch(u, j) == 0:
+            if batch(u, j) >= FINE_FROM or batch(u, j) == 0 or (u, j) == (2 * FINE_FROM - 3, 1):
                 clip(nc.vector if J * u + j >= VCLIP_FROM else nc.gpsimd, rows(u, j)[:, cols])
                 nc.sync.dma_start(out=out_view[:, J * u + j, :], in_=rows(u, j))
 
         def clip(engine, tile):
             engine.tensor_scalar(out=tile, in0=tile, scalar1=CLAMP, scalar2=-CLAMP, op0=ALU.min, op1=ALU.max)
 
-        def close_batch(b):
-            clip(nc.gpsimd, at(finished, b)[:, SUMMED * P - copied(2 * b - 1) : 2 * J * O - SUMMED * P + copied(2 * b - 2)])
+        def clip_before(u, j, count=1):
+            first = min(z_block(u, j, 0).start, z_block(u, j + count - 1, 0).start)
+            tile = at(z, u // 2)[:, first : first + count * O]
+            nc.gpsimd.tensor_scalar(out=tile, in0=tile, scalar1=CLAMP, scalar2=-CLAMP / SLOPE, op0=ALU.min, op1=ALU.max)
+
+        def close_batch(b, first=0):
+            clip(nc.gpsimd, at(finished, b)[:, first * O or SUMMED * P - copied(2 * b - 1) : 2 * J * O - SUMMED * P + copied(2 * b - 2)])
             tiles = at(finished, b)[:].rearrange("p (t o) -> p t o", o=O)
             nc.sync.dma_start(out=out_view[:, 4 * b - 2 : 4 * b + 1 : 2, :], in_=tiles[:, 1:3, :])
             nc.sync.dma_start(out=out_view[:, 4 * b - 3, :], in_=tiles[:, 3, :])
-            nc.sync.dma_start(out=out_view[:, 4 * b - 1, :], in_=tiles[:, 0, :])
+            if not first:
+                nc.sync.dma_start(out=out_view[:, 4 * b - 1, :], in_=tiles[:, 0, :])
 
         by_block = [(e, n) for e in range(2) for n in range(GROUP_SAMPLES)]
         by_tile = [(e, n) for n in range(GROUP_SAMPLES) for e in range(2)]
@@ -478,6 +490,8 @@ def tile_modulatemlp_pa_kernel(tc, x, w_bytes, w_scale, weight, style_w, style_b
                 finish(i - 2, 0)
             if even and p - 1 < PAIRS:
                 quantise(p - 1)
+            if i == 2 * FINE_FROM:
+                close_batch(FINE_FROM - 1, 1)
             if i == 0:
                 quantise_style2(1)
             if even and p in raw_pairs:
@@ -500,7 +514,7 @@ def tile_modulatemlp_pa_kernel(tc, x, w_bytes, w_scale, weight, style_w, style_b
                 turn_back(i - 1, 0, k)
             if summing:
                 for k in range(PACK):
-                    if k not in summed(i - 2):
+                    if k not in summed(i - 2) and not (i % PRODUCT_EVERY == 0 and k == by_product(i - 2)):
                         turn_back(i - 2, 1, k)
                 for n, k in enumerate(turned):
                     turn_back(i - 2, 1, k, stop=False)
@@ -513,6 +527,8 @@ def tile_modulatemlp_pa_kernel(tc, x, w_bytes, w_scale, weight, style_w, style_b
             cut = len(parts) - 2 * PACK + (RELU1_AT if i < TAIL_FROM else RELU1_TAIL)
             for q, part in parts[:cut]:
                 demodulate(nc.scalar, q, [part])
+            if late and even:
+                copy_words(nc.scalar.copy, at(raw, p + 1 - FIRST_RAW)[:], x_banks[1], slice(P, 2 * P))
             if i == 1:
                 copy_early(1)
             if not even and i <= LAST and summed(i):
@@ -520,7 +536,7 @@ def tile_modulatemlp_pa_kernel(tc, x, w_bytes, w_scale, weight, style_w, style_b
             if 0 <= i - 3 and summed(i - 3):
                 take_relu(i - 3, 1)
                 finish(i - 3, 1)
-                if even and 0 < i // 2 - 1 < FINE_FROM:
+                if even and 0 < i // 2 - 1 < FINE_FROM - 1:
                     close_batch(i // 2 - 1)
             if p < PAIRS:
                 modulate(2 * p, 0, 3) if even else modulate(2 * p, 3, 1)
@@ -532,19 +548,17 @@ def tile_modulatemlp_pa_kernel(tc, x, w_bytes, w_scale, weight, style_w, style_b
                 copy_early(2)
             if i == 2:
                 take_root(1, z_banks[0], range(PACK))
-            if 0 <= i - 1 < PLAIN_FROM:
-                take_relu(i - 1, 0)
-            if late and even:
-                copy_words(nc.scalar.copy, at(raw, p + 1 - FIRST_RAW)[:], x_banks[1], slice(P, 2 * P))
 
+            if 0 <= i - 1:
+                take_relu(i - 1, 0)
             if 0 < i and 2 * i + 3 < 2 * GROUPS:
                 product(2 * i + 3)
             if summing and BY_MATMUL:
-                add_steep(i - 2, summed(i - 2)[0], False, False)
+                add_steep(i - 2, summed(i - 2)[0], False, True)
+            if summing and i % PRODUCT_EVERY == 0:
+                turn_back(i - 2, 1, by_product(i - 2), as_product=True)
             if 2 * i + 4 < 2 * GROUPS:
                 product(2 * i + 4)
-            if summing and BY_MATMUL == 2:
-                add_steep(i - 2, summed(i - 2)[1], False, True)
             if i == 1:
                 d_product(1, z_banks[0], range(PACK))
 
@@ -577,25 +591,25 @@ def tile_modulatemlp_pa_kernel(tc, x, w_bytes, w_scale, weight, style_w, style_b
         finish(u - 3, 1)
         product(2 * u + 3)
         sum_tile(u - 2)
-        take_relu(u - 1, 0)
-        take_steep(u, 0, nc.scalar)
-        open_tile(u - 1)
-        turn_both(u, 0)
-        finish(u - 1, 0)
         demodulate(nc.vector, 2 * u + 3, by_tile[:PACK])
-        take_steep(u, 1, nc.scalar)
+        take_relu(u - 1, 0)
+        demodulate(nc.scalar, 2 * u + 3, by_tile[PACK:])
+        turn_plain(u, 0)
+        open_tile(u - 1)
+        finish(u - 1, 0)
         take_relu(u - 2, 1)
         sum_tile(u - 1)
-        demodulate(nc.scalar, 2 * u + 3, by_tile[PACK:])
         finish(u - 2, 1)
-        turn_both(u, 1)
-        finish_sum(u, 0)
-        take_steep(u + 1, 0, nc.scalar)
+        turn_plain(u, 1)
+        take_relu(u, 0)
+        turn_plain(u + 1, 0)
+        finish(u, 0)
         take_relu(u - 1, 1)
-        take_steep(u + 1, 1, nc.scalar)
-        turn_both(u + 1, 0)
+        turn_plain(u + 1, 1)
+        take_relu(u, 1)
         finish(u - 1, 1)
-        finish_sum(u, 1)
-        turn_both(u + 1, 1)
-        finish_sum(u + 1, 0)
-        finish_sum(u + 1, 1)
+        take_relu(u + 1, 0)
+        finish(u, 1)
+        take_relu(u + 1, 1)
+        finish(u + 1, 0)
+        finish(u + 1, 1)

@@ -34,22 +34,18 @@ FIRST_RAW = 1
 LAST_RAW = PAIRS - 1
 EARLY_BANKS = 3
 PLAIN_FROM = GROUPS - 2
-ON_VECTOR = (2, 3)
-RAMP_VECTOR = (8, 4)
+ON_VECTOR = (1, 1)
+RAMP_VECTOR = (4, 2)
 RELU1_AT = 0
 RELU1_TAIL = 8
 RAW_TILES = 2 * EARLY_BANKS
 TAIL_VECTOR = (6, 8, 8)
 TAIL_FROM = GROUPS - 3
 FINE_FROM = 14
+FINISHED = 9
 SPARE_FROM = 26
 VCLIP_FROM = 63
-PROMPT_FROM = 30
-BY_MATMUL = 1
 PRODUCT_EVERY = 1
-BY_TURN = 0
-ON_SCALAR = 0
-COPY_UNTIL = 26
 
 
 def tile_modulatemlp_pa_kernel(tc, x, w_bytes, w_scale, weight, style_w, style_b, bias, out):
@@ -153,13 +149,14 @@ def tile_modulatemlp_pa_kernel(tc, x, w_bytes, w_scale, weight, style_w, style_b
         decoef = ring("decoef", 2, [P, PACK, HALF], F32)
         bias_gain = keep.tile([P, PACK], F32)
 
-        modulated = keep.tile([P, 2 * TOKENS * PACK], BF16, align_bytes=64)
+        modulated = ring("modulated", 2, [P, 3 * P * PACK], BF16)
+        modulated_raw = keep.tile([P, P * PACK], BF16, align_bytes=64)
         codes = ring("codes", 2, [P, 2 * TOKENS], U32)
         scales = ring("scales", 2, [P, 2 * TOKENS], U8)
-        z = ring("z", 3, [P, 2 * J * O], F32)
-        negative = ring("negative", 2, [P, 2 * (BY_MATMUL + BY_TURN) * P], F32)
-        relu = ring("relu", 6, [P, O], F32)
-        finished = ring("finished", 6, [P, 2 * J * O], F32)
+        z = ring("z", 2, [P, 2 * J * O], F32)
+        negative = ring("negative", 2, [P, 2 * P], F32)
+        relu = ring("relu", 5, [P, O], F32)
+        finished = ring("finished", FINISHED, [P, 2 * J * O], F32)
 
         def turn_tile(bank, j, rows):
             parts = bank[:].rearrange("p (u j r) -> p u j r", u=2, j=2)
@@ -228,21 +225,25 @@ def tile_modulatemlp_pa_kernel(tc, x, w_bytes, w_scale, weight, style_w, style_b
             half, sample = divmod(u * GROUP_SAMPLES + first, HALF)
             factors = style[half][:, sample : sample + count, :].rearrange("p n (u e) -> p n u e", e=2)
             place = u % 2 * GROUP_SAMPLES + first
+            target, place = (at(modulated, u // 2), place) if place < 6 else (modulated_raw, place - 6)
             nc.vector.tensor_tensor(
-                out=modulated[:].rearrange("p (n l u e) -> p n l u e", l=POINTS, u=2, e=2)[:, place : place + count],
+                out=target[:].rearrange("p (n l u e) -> p n l u e", l=POINTS, u=2, e=2)[:, place : place + count],
                 in0=side_by_side(at(x_banks, u)).rearrange("p (n l) u e -> p n l u e", n=GROUP_SAMPLES)[:, first : first + count],
                 in1=factors.unsqueeze(2).to_broadcast([P, count, POINTS, 2, 2]), op=ALU.mult)
 
         def modulate_raw(p):
             half, sample = divmod((2 * p + 1) * GROUP_SAMPLES + 2, HALF)
             nc.gpsimd.tensor_tensor(
-                out=modulated[:, 3 * P * PACK :].rearrange("p (n l t) -> p n l t", n=2, t=PACK),
+                out=modulated_raw[:].rearrange("p (n l t) -> p n l t", n=2, t=PACK),
                 in0=at(raw, p - FIRST_RAW)[:].rearrange("p (n l t) -> p n l t", n=2, t=PACK),
                 in1=style[half][:, sample : sample + 2, :].unsqueeze(2).to_broadcast([P, 2, POINTS, PACK]), op=ALU.mult)
 
-        def quantise(p, tokens=slice(0, 2 * TOKENS)):
+        def quantise(p, tokens=slice(0, 3 * P)):
             nc.vector.quantize_mx(out=at(codes, p)[:, tokens].bitcast(X4), scales=at(scales, p)[:, tokens],
-                                  in_=modulated[:, tokens.start * PACK : tokens.stop * PACK])
+                                  in_=at(modulated, p)[:, tokens.start * PACK : tokens.stop * PACK])
+
+        def quantise_raw(p):
+            nc.vector.quantize_mx(out=at(codes, p)[:, 3 * P :].bitcast(X4), scales=at(scales, p)[:, 3 * P :], in_=modulated_raw[:])
 
         def product(q, tokens=slice(0, TOKENS), bank=None):
             u, h = divmod(q, 2)
@@ -255,35 +256,14 @@ def tile_modulatemlp_pa_kernel(tc, x, w_bytes, w_scale, weight, style_w, style_b
                                     rhs_scale=at(scales, u // 2)[:, moving], start=True, stop=True)
 
         def z_block(u, j, k):
-            first = ((j if u % 2 == 0 else 3 - j) * PACK + k) * P
+            first = ((u % 2 * J + j) * PACK + k) * P
             return slice(first, first + P)
 
-        SUMMED = BY_MATMUL + BY_TURN
-        summed_start = J * O - SUMMED * P
-        scaled_start = BY_MATMUL * P
-
         def summed(u):
-            if u >= PLAIN_FROM:
-                return ()
-            return tuple(range(PACK - SUMMED, PACK)) if u % 2 == 0 else tuple(range(SUMMED - 1, -1, -1))
-
-        def by_matmul(u):
-            return summed(u)[:BY_MATMUL]
-
-        def by_turn(u):
-            return summed(u)[BY_MATMUL:]
-
-        def by_product(u):
-            return 0 if u % 2 == 0 else PACK - 1
-
-        def part_of_tile(u, first, last):
-            return slice(first, last) if u % 2 == 0 else slice(O - last, O - first)
+            return 0 <= u < PLAIN_FROM
 
         def plain_cols(u, j):
-            return part_of_tile(u, 0, O - len(summed(u)) * P if j else O)
-
-        def copied(u):
-            return ON_SCALAR if u < COPY_UNTIL else 0
+            return slice(P if j and summed(u) else 0, O)
 
         def demodulate(engine, q, parts, bank=None):
             u, h = divmod(q, 2)
@@ -303,11 +283,9 @@ def tile_modulatemlp_pa_kernel(tc, x, w_bytes, w_scale, weight, style_w, style_b
                                             op0=ALU.mult, op1=ALU.add)
 
         def take_negative(p):
-            nc.gpsimd.tensor_scalar(out=at(negative, p)[:], in0=at(z, p)[:, summed_start : summed_start + 2 * SUMMED * P], scalar1=0.0,
+            nc.gpsimd.tensor_scalar(out=at(negative, p)[:].rearrange("p (g r) -> p g r", g=2),
+                                    in0=at(z, p)[:].rearrange("p (g c) -> p g c", g=2)[:, :, O : O + P], scalar1=0.0,
                                     scalar2=-CLAMP / SLOPE, op0=ALU.min, op1=ALU.max)
-            if BY_TURN:
-                middle = at(negative, p)[:, scaled_start : scaled_start + 2 * BY_TURN * P]
-                nc.gpsimd.tensor_scalar(out=middle, in0=middle, scalar1=-(1.0 - SLOPE), scalar2=1.0, op0=ALU.mult, op1=ALU.mult)
 
         def z_bank(u, j):
             if u + j <= SPARE_FROM:
@@ -322,36 +300,15 @@ def tile_modulatemlp_pa_kernel(tc, x, w_bytes, w_scale, weight, style_w, style_b
             nc.tensor.matmul(out=z_bank(u, j)[:, k * P : (k + 1) * P], lhsT=at(z, u // 2)[:, z_block(u, j, k)], rhs=ident[:],
                              is_transpose=not as_product, start=start, stop=stop)
 
-        def add_steep(u, k, start, stop):
-            first = z_block(u, 1, k).start - summed_start
-            turned = k in by_turn(u)
-            nc.tensor.matmul(out=z_bank(u, 1)[:, k * P : (k + 1) * P], lhsT=at(negative, u // 2)[:, first : first + P],
-                             rhs=ident[:] if turned else steep_ident[:], is_transpose=turned, start=start, stop=stop)
-
-        def take_steep(u, j, engine=nc.vector):
-            first = z_block(u, j, 0).start
-            if engine is nc.scalar:
-                nc.scalar.activation(out=relu_tile(u, j)[:], in_=at(z, u // 2)[:, first : first + O], func=ACT.Relu,
-                                     scale=-(1.0 - SLOPE))
-                return
-            nc.vector.tensor_scalar(out=relu_tile(u, j)[:], in0=at(z, u // 2)[:, first : first + O], scalar1=0.0,
-                                    scalar2=-(1.0 - SLOPE), op0=ALU.min, op1=ALU.mult)
-
-        def turn_both(u, j):
-            for k in range(PACK):
-                turn_back(u, j, k, stop=False)
-                nc.tensor.matmul(out=z_bank(u, j)[:, k * P : (k + 1) * P], lhsT=relu_tile(u, j)[:, k * P : (k + 1) * P],
-                                 rhs=ident[:], is_transpose=True, start=False, stop=True)
-
-        def finish_sum(u, j):
-            nc.vector.tensor_scalar(out=rows(u, j), in0=z_bank(u, j)[:], scalar1=CLAMP, scalar2=-CLAMP, op0=ALU.min, op1=ALU.max)
-            nc.sync.dma_start(out=out_view[:, J * u + j, :], in_=rows(u, j))
+        def add_steep(u):
+            nc.tensor.matmul(out=z_bank(u, 1)[:, :P], lhsT=at(negative, u // 2)[:, u % 2 * P : (u % 2 + 1) * P],
+                             rhs=steep_ident[:], start=False, stop=True)
 
         def batch(u, j):
-            return (u + 1) // 2 if j == 0 else u // 2 + 1
+            return (J * u + j + 3) // 4
 
         def rows(u, j):
-            place = 2 - u % 2 if j == 0 else 3 - u % 2 * 3
+            place = (J * u + j + 3) % 4
             return at(finished, batch(u, j))[:, place * O : (place + 1) * O]
 
         def relu_tile(u, j):
@@ -359,43 +316,25 @@ def tile_modulatemlp_pa_kernel(tc, x, w_bytes, w_scale, weight, style_w, style_b
 
         def take_relu(u, j):
             cols = plain_cols(u, j)
-            width = cols.stop - cols.start
-            if width:
-                nc.scalar.activation(out=relu_tile(u, j)[:, cols], in_=z_bank(u, j)[:, cols], func=ACT.Relu, scale=-(1.0 - SLOPE))
-            if width < O and copied(u):
-                cols = part_of_tile(u, width, width + copied(u))
-                nc.scalar.copy(out=rows(u, j)[:, cols], in_=z_bank(u, j)[:, cols])
+            nc.scalar.activation(out=relu_tile(u, j)[:, cols], in_=z_bank(u, j)[:, cols], func=ACT.Relu, scale=-(1.0 - SLOPE))
 
         def finish(u, j):
             cols = plain_cols(u, j)
-            width = cols.stop - cols.start
             bank = z_bank(u, j)
-            if width:
-                nc.vector.tensor_tensor(out=rows(u, j)[:, cols], in0=bank[:, cols], in1=relu_tile(u, j)[:, cols], op=ALU.add)
-            if width < O:
-                other = part_of_tile(u, width + copied(u), O)
-                nc.vector.tensor_scalar(out=rows(u, j)[:, other], in0=bank[:, other],
+            nc.vector.tensor_tensor(out=rows(u, j)[:, cols], in0=bank[:, cols], in1=relu_tile(u, j)[:, cols], op=ALU.add)
+            if cols.start:
+                nc.vector.tensor_scalar(out=rows(u, j)[:, :P], in0=bank[:, :P],
                                         scalar1=CLAMP, scalar2=-CLAMP, op0=ALU.min, op1=ALU.max)
-                cols = part_of_tile(u, 0, width + copied(u))
-            if batch(u, j) >= FINE_FROM or batch(u, j) == 0 or (u, j) == (2 * FINE_FROM - 3, 1):
+            if batch(u, j) >= FINE_FROM or batch(u, j) == 0:
                 clip(nc.vector if J * u + j >= VCLIP_FROM else nc.gpsimd, rows(u, j)[:, cols])
                 nc.sync.dma_start(out=out_view[:, J * u + j, :], in_=rows(u, j))
 
         def clip(engine, tile):
             engine.tensor_scalar(out=tile, in0=tile, scalar1=CLAMP, scalar2=-CLAMP, op0=ALU.min, op1=ALU.max)
 
-        def clip_before(u, j, count=1):
-            first = min(z_block(u, j, 0).start, z_block(u, j + count - 1, 0).start)
-            tile = at(z, u // 2)[:, first : first + count * O]
-            nc.gpsimd.tensor_scalar(out=tile, in0=tile, scalar1=CLAMP, scalar2=-CLAMP / SLOPE, op0=ALU.min, op1=ALU.max)
-
-        def close_batch(b, first=0):
-            clip(nc.gpsimd, at(finished, b)[:, first * O or SUMMED * P - copied(2 * b - 1) : 2 * J * O - SUMMED * P + copied(2 * b - 2)])
-            tiles = at(finished, b)[:].rearrange("p (t o) -> p t o", o=O)
-            nc.sync.dma_start(out=out_view[:, 4 * b - 2 : 4 * b + 1 : 2, :], in_=tiles[:, 1:3, :])
-            nc.sync.dma_start(out=out_view[:, 4 * b - 3, :], in_=tiles[:, 3, :])
-            if not first:
-                nc.sync.dma_start(out=out_view[:, 4 * b - 1, :], in_=tiles[:, 0, :])
+        def close_batch(b):
+            clip(nc.gpsimd, at(finished, b)[:].rearrange("p (g c) -> p g c", g=2)[:, :, P:])
+            nc.sync.dma_start(out=out_view[:, 4 * b - 3 : 4 * b + 1, :], in_=at(finished, b)[:].rearrange("p (t o) -> p t o", o=O))
 
         by_block = [(e, n) for e in range(2) for n in range(GROUP_SAMPLES)]
         by_tile = [(e, n) for n in range(GROUP_SAMPLES) for e in range(2)]
@@ -469,9 +408,11 @@ def tile_modulatemlp_pa_kernel(tc, x, w_bytes, w_scale, weight, style_w, style_b
         turn_x(5)
         demodulate(nc.scalar, 0, by_tile[PACK:])
         take_root(0, z_banks[1], range(2, PACK))
-        modulate(1)
+        modulate(1, 0, 2)
+        modulate(1, 2, 2)
+        quantise(0, slice(TOKENS, 3 * P))
         make_style(1)
-        quantise(0, slice(TOKENS, 2 * TOKENS))
+        quantise_raw(0)
         modulate_raw(1)
         turn_x(6)
         product(2)
@@ -480,6 +421,15 @@ def tile_modulatemlp_pa_kernel(tc, x, w_bytes, w_scale, weight, style_w, style_b
         modulate(2)
         modulate(3, 0, 2)
         square_style(1)
+
+        def turn_plain(u, j):
+            for k in range(PACK):
+                turn_back(u, j, k)
+
+        def open_tile(u, end=PACK):
+            for k in range(1, end):
+                turn_back(u, 1, k)
+            turn_back(u, 1, 0, stop=False)
 
         for i in range(PLAIN_FROM):
             p = i // 2 + 2
@@ -490,8 +440,7 @@ def tile_modulatemlp_pa_kernel(tc, x, w_bytes, w_scale, weight, style_w, style_b
                 finish(i - 2, 0)
             if even and p - 1 < PAIRS:
                 quantise(p - 1)
-            if i == 2 * FINE_FROM:
-                close_batch(FINE_FROM - 1, 1)
+                quantise_raw(p - 1)
             if i == 0:
                 quantise_style2(1)
             if even and p in raw_pairs:
@@ -507,21 +456,10 @@ def tile_modulatemlp_pa_kernel(tc, x, w_bytes, w_scale, weight, style_w, style_b
             if i < 1:
                 for b in range(2, EARLY_BANKS):
                     turn_early(b)
-            summing = 0 <= i - 2 and summed(i - 2)
-            first_tile = list(range(PACK)) if 0 <= i - 1 < PLAIN_FROM else []
-            turned = by_turn(i - 2) if summing else ()
-            for k in first_tile[len(turned) :]:
-                turn_back(i - 1, 0, k)
-            if summing:
-                for k in range(PACK):
-                    if k not in summed(i - 2) and not (i % PRODUCT_EVERY == 0 and k == by_product(i - 2)):
-                        turn_back(i - 2, 1, k)
-                for n, k in enumerate(turned):
-                    turn_back(i - 2, 1, k, stop=False)
-                    turn_back(i - 1, 0, first_tile[n])
-                    add_steep(i - 2, k, False, True)
-                for k in by_matmul(i - 2):
-                    turn_back(i - 2, 1, k, start=k == by_matmul(i - 2)[0], stop=False)
+            if 0 <= i - 1:
+                turn_plain(i - 1, 0)
+            if summed(i - 2):
+                open_tile(i - 2, PACK - 1 if i % PRODUCT_EVERY == 0 else PACK)
 
             parts = [] if i > LAST else on_scalar(i)[2 * PACK :] if i == 0 else on_scalar(i)
             cut = len(parts) - 2 * PACK + (RELU1_AT if i < TAIL_FROM else RELU1_TAIL)
@@ -533,10 +471,10 @@ def tile_modulatemlp_pa_kernel(tc, x, w_bytes, w_scale, weight, style_w, style_b
                 copy_early(1)
             if not even and i <= LAST and summed(i):
                 take_negative(i // 2)
-            if 0 <= i - 3 and summed(i - 3):
+            if summed(i - 3):
                 take_relu(i - 3, 1)
                 finish(i - 3, 1)
-                if even and 0 < i // 2 - 1 < FINE_FROM - 1:
+                if even and 0 < i // 2 - 1 < FINE_FROM:
                     close_batch(i // 2 - 1)
             if p < PAIRS:
                 modulate(2 * p, 0, 3) if even else modulate(2 * p, 3, 1)
@@ -553,29 +491,14 @@ def tile_modulatemlp_pa_kernel(tc, x, w_bytes, w_scale, weight, style_w, style_b
                 take_relu(i - 1, 0)
             if 0 < i and 2 * i + 3 < 2 * GROUPS:
                 product(2 * i + 3)
-            if summing and BY_MATMUL:
-                add_steep(i - 2, summed(i - 2)[0], False, True)
-            if summing and i % PRODUCT_EVERY == 0:
-                turn_back(i - 2, 1, by_product(i - 2), as_product=True)
+            if summed(i - 2):
+                add_steep(i - 2)
+                if i % PRODUCT_EVERY == 0:
+                    turn_back(i - 2, 1, PACK - 1, as_product=True)
             if 2 * i + 4 < 2 * GROUPS:
                 product(2 * i + 4)
             if i == 1:
                 d_product(1, z_banks[0], range(PACK))
-
-        def open_tile(u):
-            for k in range(PACK):
-                if k not in summed(u):
-                    turn_back(u, 1, k)
-            for k in summed(u):
-                turn_back(u, 1, k, start=k == summed(u)[0], stop=False)
-
-        def sum_tile(u):
-            for k in summed(u):
-                add_steep(u, k, False, k == summed(u)[-1])
-
-        def turn_plain(u, j):
-            for k in range(PACK):
-                turn_back(u, j, k)
 
         def scalar_parts(u, first, last):
             for q, part in on_scalar(u)[first:last]:
@@ -590,7 +513,7 @@ def tile_modulatemlp_pa_kernel(tc, x, w_bytes, w_scale, weight, style_w, style_b
         take_relu(u - 3, 1)
         finish(u - 3, 1)
         product(2 * u + 3)
-        sum_tile(u - 2)
+        add_steep(u - 2)
         demodulate(nc.vector, 2 * u + 3, by_tile[:PACK])
         take_relu(u - 1, 0)
         demodulate(nc.scalar, 2 * u + 3, by_tile[PACK:])
@@ -598,7 +521,7 @@ def tile_modulatemlp_pa_kernel(tc, x, w_bytes, w_scale, weight, style_w, style_b
         open_tile(u - 1)
         finish(u - 1, 0)
         take_relu(u - 2, 1)
-        sum_tile(u - 1)
+        add_steep(u - 1)
         finish(u - 2, 1)
         turn_plain(u, 1)
         take_relu(u, 0)

@@ -30,29 +30,25 @@ GROUPS = SAMPLES // GROUP_SAMPLES
 PAIRS = GROUPS // 2
 HALF = SAMPLES // 2
 LAST = GROUPS - 1
-FIRST_RAW = 1
-LAST_RAW = PAIRS - 1
+RAW_PAIRS = range(1, PAIRS)
 EARLY_BANKS = 3
-PLAIN_FROM = GROUPS - 2
-ON_VECTOR = (1, 1)
-RAMP_VECTOR = (4, 2)
-RELU1_AT = 0
-RELU1_TAIL = 8
-RAW_TILES = 2 * EARLY_BANKS
-TAIL_VECTOR = (6, 8, 8)
+PLAIN_FROM = GROUPS - 3
+ON_VECTOR = (1, 2)
+RAMP_VECTOR = (0, 4)
+TAIL_VECTOR = (8, 0)
+TAIL_LAST = 8
+TAIL_CUT = 12
 TAIL_FROM = GROUPS - 3
-FINE_FROM = 14
+ON_SCALAR = 0
+FINE_FROM = 27
 FINISHED = 9
-SPARE_FROM = 26
-VCLIP_FROM = 63
-PRODUCT_EVERY = 1
 
 
 def tile_modulatemlp_pa_kernel(tc, x, w_bytes, w_scale, weight, style_w, style_b, bias, out):
     nc = tc.nc
     x_view = x.rearrange("n l c -> (n l) c").rearrange("(t r) c -> r t c", r=P)
     out_view = out.rearrange("n l o -> (n l) o").rearrange("(t r) o -> r t o", r=P)
-    raw_pairs = range(FIRST_RAW, LAST_RAW + 1)
+    raw_pairs = list(RAW_PAIRS)
     early_pairs = raw_pairs[: 2 * EARLY_BANKS]
 
     with ExitStack() as ctx:
@@ -67,8 +63,8 @@ def tile_modulatemlp_pa_kernel(tc, x, w_bytes, w_scale, weight, style_w, style_b
             return tiles[index % len(tiles)]
 
         x_banks = [psum.tile([P, BANK], F32, name="x_bank%d" % r) for r in range(2)]
-        y_banks = [psum.tile([P, BANK], F32, name="y_bank%d" % r) for r in range(3)]
-        z_banks = [psum.tile([P, BANK], F32, name="z_bank%d" % r) for r in range(3)]
+        y_banks = [psum.tile([P, BANK], F32, name="y_bank%d" % r) for r in range(2)]
+        z_banks = [psum.tile([P, BANK], F32, name="z_bank%d" % r) for r in range(4)]
 
         style_w_sb = ring("style_w_sb", 2, [P, 2, LATENT], BF16)
         weight_sb = ring("weight_sb", 2, [P, 2, C], BF16)
@@ -88,9 +84,9 @@ def tile_modulatemlp_pa_kernel(tc, x, w_bytes, w_scale, weight, style_w, style_b
             nc.sync.dma_start(out=weight_sb[h][:], in_=weight_view[h])
 
         x_first = ring("x_first", 2, [P, J, C], BF16)
-        x_pairs = ring("x_pair", PAIRS, [P, 2 * J, C], BF16)
-        x_early = ring("x_early", EARLY_BANKS, [P, 2, C], BF16)
-        raw = ring("raw", RAW_TILES, [P, P * PACK], BF16)
+        x_pairs = [None] + ring("x_pair", PAIRS - 1, [P, 2 * J, C], BF16)
+        x_early = ring("x_early", len(early_pairs), [P, C], BF16)
+        raw = ring("raw", max(2, len(early_pairs)), [P, P * PACK], BF16)
 
         def own_tiles(p):
             return 3 if p in raw_pairs else 4
@@ -100,22 +96,21 @@ def tile_modulatemlp_pa_kernel(tc, x, w_bytes, w_scale, weight, style_w, style_b
             if p == 0:
                 return x_first[j // J][:, j % J, :]
             if p in early_pairs and j == 3:
-                return x_early[(p - FIRST_RAW) // 2][:, (p - FIRST_RAW) % 2, :]
+                return x_early[early_pairs.index(p)][:]
             return x_pairs[p][:, j, :]
 
         def load_pair(p):
             n = 3 if p in early_pairs else 4
             nc.sync.dma_start(out=x_pairs[p][:, :n, :], in_=x_view[:, 4 * p : 4 * p + n, :])
 
-        def load_early(b):
-            first = 4 * (FIRST_RAW + 2 * b) + 3
-            nc.sync.dma_start(out=x_early[b][:], in_=x_view[:, first : first + 5 : 4, :])
+        def load_early(n):
+            nc.sync.dma_start(out=x_early[n][:], in_=x_view[:, 4 * early_pairs[n] + 3, :])
 
         for u in range(2):
             nc.sync.dma_start(out=x_first[u][:], in_=x_view[:, u * J : (u + 1) * J, :])
         for p in range(1, PAIRS):
-            if p <= EARLY_BANKS:
-                load_early(p - 1)
+            for n in range(2 * p - 2, min(2 * p, len(early_pairs))):
+                load_early(n)
             load_pair(p)
 
         ident = keep.tile([P, P], F32)
@@ -154,8 +149,8 @@ def tile_modulatemlp_pa_kernel(tc, x, w_bytes, w_scale, weight, style_w, style_b
         codes = ring("codes", 2, [P, 2 * TOKENS], U32)
         scales = ring("scales", 2, [P, 2 * TOKENS], U8)
         z = ring("z", 2, [P, 2 * J * O], F32)
-        negative = ring("negative", 2, [P, 2 * P], F32)
-        relu = ring("relu", 5, [P, O], F32)
+        negative = ring("negative", 2, [P, 2 * J * P], F32)
+        relu = ring("relu", 6, [P, O], F32)
         finished = ring("finished", FINISHED, [P, 2 * J * O], F32)
 
         def turn_tile(bank, j, rows):
@@ -180,7 +175,6 @@ def tile_modulatemlp_pa_kernel(tc, x, w_bytes, w_scale, weight, style_w, style_b
             nc.vector.quantize_mx(out=q[:, cols].bitcast(X4), scales=s[:, cols], in_=source[:])
 
         style_bank = z_banks[2]
-        style_bank2 = z_banks[1]
 
         def make_style(h):
             sums = style_bank[:].rearrange("p (t n) -> p n t", t=PACK)[:, h * HALF : (h + 1) * HALF, :]
@@ -212,14 +206,21 @@ def tile_modulatemlp_pa_kernel(tc, x, w_bytes, w_scale, weight, style_w, style_b
         def turn_x(t):
             turn_tile(at(x_banks, t // J), t % J, x_rows(t))
 
-        early_banks = [y_banks[2], z_banks[0], z_banks[1]]
+        early_banks = [z_banks[3], z_banks[0], z_banks[1]]
 
         def turn_early(b):
-            turn_rows(early_banks[b], x_early[b])
+            for n in range(2 * b, min(2 * b + 2, len(early_pairs))):
+                turn_tile(early_banks[b], n % 2, x_early[n][:])
 
-        def copy_early(b, tiles=range(2)):
-            for e in tiles:
-                copy_words(nc.scalar.copy, raw[2 * b + e][:], early_banks[b], slice(e * P, (e + 1) * P))
+        def raw_tile(p):
+            return at(raw, raw_pairs.index(p))
+
+        def copy_raw(p, bank, j):
+            copy_words(nc.scalar.copy, raw_tile(p)[:], bank, slice(j * P, (j + 1) * P))
+
+        def copy_early(b):
+            for n in range(2 * b, min(2 * b + 2, len(early_pairs))):
+                copy_raw(early_pairs[n], early_banks[b], n % 2)
 
         def modulate(u, first=0, count=GROUP_SAMPLES):
             half, sample = divmod(u * GROUP_SAMPLES + first, HALF)
@@ -235,7 +236,7 @@ def tile_modulatemlp_pa_kernel(tc, x, w_bytes, w_scale, weight, style_w, style_b
             half, sample = divmod((2 * p + 1) * GROUP_SAMPLES + 2, HALF)
             nc.gpsimd.tensor_tensor(
                 out=modulated_raw[:].rearrange("p (n l t) -> p n l t", n=2, t=PACK),
-                in0=at(raw, p - FIRST_RAW)[:].rearrange("p (n l t) -> p n l t", n=2, t=PACK),
+                in0=raw_tile(p)[:].rearrange("p (n l t) -> p n l t", n=2, t=PACK),
                 in1=style[half][:, sample : sample + 2, :].unsqueeze(2).to_broadcast([P, 2, POINTS, PACK]), op=ALU.mult)
 
         def quantise(p, tokens=slice(0, 3 * P)):
@@ -247,7 +248,7 @@ def tile_modulatemlp_pa_kernel(tc, x, w_bytes, w_scale, weight, style_w, style_b
 
         def product(q, tokens=slice(0, TOKENS), bank=None):
             u, h = divmod(q, 2)
-            bank = at(y_banks, q + 1) if bank is None else bank
+            bank = at(y_banks, q) if bank is None else bank
             moving = slice(u % 2 * TOKENS + tokens.start, u % 2 * TOKENS + tokens.stop)
             for e in range(2):
                 cols = slice((2 * h + e) * P, (2 * h + e + 1) * P)
@@ -256,24 +257,21 @@ def tile_modulatemlp_pa_kernel(tc, x, w_bytes, w_scale, weight, style_w, style_b
                                     rhs_scale=at(scales, u // 2)[:, moving], start=True, stop=True)
 
         def z_block(u, j, k):
-            first = ((u % 2 * J + j) * PACK + k) * P
-            return slice(first, first + P)
+            first = (((u + 1) % 2 * J + j) * PACK + k) * P
+            return at(z, (u + 1) // 2)[:, first : first + P]
 
         def summed(u):
             return 0 <= u < PLAIN_FROM
 
-        def plain_cols(u, j):
-            return slice(P if j and summed(u) else 0, O)
-
         def demodulate(engine, q, parts, bank=None):
             u, h = divmod(q, 2)
-            bank = at(y_banks, q + 1) if bank is None else bank
+            bank = at(y_banks, q) if bank is None else bank
             for e, n in parts:
                 k = 2 * h + e
                 half, sample = divmod(u * GROUP_SAMPLES + n, HALF)
                 j, r = divmod(n * POINTS, P)
                 first = e * TOKENS + n * POINTS
-                dst = at(z, u // 2)[:, z_block(u, j, k)][:, r : r + POINTS]
+                dst = z_block(u, j, k)[:, r : r + POINTS]
                 src = bank[:, first : first + POINTS]
                 factor = decoef[half][:, k, sample : sample + 1]
                 if engine is nc.scalar:
@@ -282,78 +280,76 @@ def tile_modulatemlp_pa_kernel(tc, x, w_bytes, w_scale, weight, style_w, style_b
                     nc.vector.tensor_scalar(out=dst, in0=src, scalar1=factor, scalar2=bias_gain[:, k : k + 1],
                                             op0=ALU.mult, op1=ALU.add)
 
-        def take_negative(p):
-            nc.gpsimd.tensor_scalar(out=at(negative, p)[:].rearrange("p (g r) -> p g r", g=2),
-                                    in0=at(z, p)[:].rearrange("p (g c) -> p g c", g=2)[:, :, O : O + P], scalar1=0.0,
+        def take_negative(n, first=0):
+            nc.gpsimd.tensor_scalar(out=at(negative, n)[:].rearrange("p (t r) -> p t r", r=P)[:, first:],
+                                    in0=at(z, n)[:].rearrange("p (t c) -> p t c", c=O)[:, first:, :P], scalar1=0.0,
                                     scalar2=-CLAMP / SLOPE, op0=ALU.min, op1=ALU.max)
 
+        free_banks = [z_banks[2], z_banks[0], z_banks[1], z_banks[3]]
+        taken = {}
+
         def z_bank(u, j):
-            if u + j <= SPARE_FROM:
-                return at(z_banks, 2 * u + 2)
-            if j == 1 and summed(u):
-                return x_banks[u % 2]
-            if (u, j) == (LAST, 1):
-                return y_banks[2]
-            return at(z_banks, u + SPARE_FROM + 3 + max(0, u - PLAIN_FROM) + j)
+            if (u, j) not in taken:
+                taken[(u, j)] = free_banks.pop(0)
+            return taken[(u, j)]
 
-        def turn_back(u, j, k, start=True, stop=True, as_product=False):
-            nc.tensor.matmul(out=z_bank(u, j)[:, k * P : (k + 1) * P], lhsT=at(z, u // 2)[:, z_block(u, j, k)], rhs=ident[:],
-                             is_transpose=not as_product, start=start, stop=stop)
+        def turn_back(u, j):
+            for k in (1, 2, 3, 0):
+                nc.tensor.matmul(out=z_bank(u, j)[:, k * P : (k + 1) * P], lhsT=z_block(u, j, k), rhs=ident[:],
+                                 is_transpose=True, start=True, stop=k > 0 or not summed(u))
 
-        def add_steep(u):
-            nc.tensor.matmul(out=z_bank(u, 1)[:, :P], lhsT=at(negative, u // 2)[:, u % 2 * P : (u % 2 + 1) * P],
+        def add_steep(u, j):
+            first = ((u + 1) % 2 * J + j) * P
+            nc.tensor.matmul(out=z_bank(u, j)[:, :P], lhsT=at(negative, (u + 1) // 2)[:, first : first + P],
                              rhs=steep_ident[:], start=False, stop=True)
 
-        def batch(u, j):
-            return (J * u + j + 3) // 4
-
         def rows(u, j):
-            place = (J * u + j + 3) % 4
-            return at(finished, batch(u, j))[:, place * O : (place + 1) * O]
+            place = (u + 1) % 2 * J + j
+            return at(finished, (u + 1) // 2)[:, place * O : (place + 1) * O]
 
         def relu_tile(u, j):
-            return at(relu, 2 * u + j)
+            return at(relu, J * u + j)
 
         def take_relu(u, j):
-            cols = plain_cols(u, j)
-            nc.scalar.activation(out=relu_tile(u, j)[:, cols], in_=z_bank(u, j)[:, cols], func=ACT.Relu, scale=-(1.0 - SLOPE))
+            first = P if summed(u) else 0
+            nc.scalar.activation(out=relu_tile(u, j)[:, first:], in_=z_bank(u, j)[:, first:], func=ACT.Relu, scale=-(1.0 - SLOPE))
+            if first and ON_SCALAR:
+                nc.scalar.copy(out=rows(u, j)[:, P - ON_SCALAR : P], in_=z_bank(u, j)[:, P - ON_SCALAR : P])
 
         def finish(u, j):
-            cols = plain_cols(u, j)
+            first = P if summed(u) else 0
             bank = z_bank(u, j)
-            nc.vector.tensor_tensor(out=rows(u, j)[:, cols], in0=bank[:, cols], in1=relu_tile(u, j)[:, cols], op=ALU.add)
-            if cols.start:
-                nc.vector.tensor_scalar(out=rows(u, j)[:, :P], in0=bank[:, :P],
+            nc.vector.tensor_tensor(out=rows(u, j)[:, first:], in0=bank[:, first:], in1=relu_tile(u, j)[:, first:], op=ALU.add)
+            if first:
+                first = P - ON_SCALAR
+                nc.vector.tensor_scalar(out=rows(u, j)[:, :first], in0=bank[:, :first],
                                         scalar1=CLAMP, scalar2=-CLAMP, op0=ALU.min, op1=ALU.max)
-            if batch(u, j) >= FINE_FROM or batch(u, j) == 0:
-                clip(nc.vector if J * u + j >= VCLIP_FROM else nc.gpsimd, rows(u, j)[:, cols])
+            free_banks.append(bank)
+            if u >= FINE_FROM:
+                engine = nc.vector if (u, j) == (LAST, J - 1) else nc.gpsimd
+                plain = rows(u, j)[:, first:]
+                engine.tensor_scalar(out=plain, in0=plain, scalar1=CLAMP, scalar2=-CLAMP, op0=ALU.min, op1=ALU.max)
                 nc.sync.dma_start(out=out_view[:, J * u + j, :], in_=rows(u, j))
 
-        def clip(engine, tile):
-            engine.tensor_scalar(out=tile, in0=tile, scalar1=CLAMP, scalar2=-CLAMP, op0=ALU.min, op1=ALU.max)
-
-        def close_batch(b):
-            clip(nc.gpsimd, at(finished, b)[:].rearrange("p (g c) -> p g c", g=2)[:, :, P:])
-            nc.sync.dma_start(out=out_view[:, 4 * b - 3 : 4 * b + 1, :], in_=at(finished, b)[:].rearrange("p (t o) -> p t o", o=O))
+        def close_groups(u, count):
+            place = (u + 1) % 2 * J
+            tiles = at(finished, (u + 1) // 2)[:].rearrange("p (t o) -> p t o", o=O)[:, place : place + J * count]
+            plain = tiles[:, :, P - ON_SCALAR :]
+            nc.gpsimd.tensor_scalar(out=plain, in0=plain, scalar1=CLAMP, scalar2=-CLAMP, op0=ALU.min, op1=ALU.max)
+            nc.sync.dma_start(out=out_view[:, J * u : J * (u + count), :], in_=tiles)
 
         by_block = [(e, n) for e in range(2) for n in range(GROUP_SAMPLES)]
         by_tile = [(e, n) for n in range(GROUP_SAMPLES) for e in range(2)]
 
         def on_vector(u):
-            count = 0 if u < 2 else RAMP_VECTOR[u - 2] if u < 2 + len(RAMP_VECTOR) else ON_VECTOR[u % 2] if u < TAIL_FROM else TAIL_VECTOR[u - TAIL_FROM]
+            count = 0 if u < 1 else RAMP_VECTOR[u - 1] if u < 1 + len(RAMP_VECTOR) else ON_VECTOR[u % 2] if u < TAIL_FROM else TAIL_VECTOR[u - TAIL_FROM]
             return by_tile[:count]
 
         def on_scalar(u):
-            first = [part for part in by_tile if part not in on_vector(u)]
-            if u % 2 and summed(u):
-                first = first[::-1]
-            if u == LAST:
-                return [(2 * u + h, (e, n)) for j in range(J) for h in range(2) for n in (2 * j, 2 * j + 1) for e in range(2)
-                        if h or (e, n) in first]
-            return [(2 * u, part) for part in first] + [(2 * u + 1, part) for part in by_tile]
+            return [(2 * u, part) for part in by_block] + [(2 * u + 1, part) for part in by_tile if part not in on_vector(u)]
 
         nc.vector.tensor_copy(out=w_bf[:], in_=w_codes[:].bitcast(FP8))
-        w_bank = y_banks[2]
+        w_bank = z_banks[3]
         w_words = w_bf[:].bitcast(F32)
         for u in range(2):
             nc.tensor.transpose(w_bank[:, u * P : (u + 1) * P], w_words[:, u::2], ident[:])
@@ -393,10 +389,10 @@ def tile_modulatemlp_pa_kernel(tc, x, w_bytes, w_scale, weight, style_w, style_b
         quantise_style2(0)
         quantise(0, slice(0, P))
         d_product(0, z_banks[0], range(0, 2))
-        product(0, slice(0, P), y_banks[0])
+        product(0, slice(0, P), y_banks[1])
         copy_early(0)
         take_root(0, z_banks[0], range(0, 2))
-        demodulate(nc.scalar, 0, by_tile[:PACK], y_banks[0])
+        demodulate(nc.scalar, 0, by_tile[:PACK], y_banks[1])
         modulate(0, 2, 2)
         quantise_half(weight2_q, weight2_s, 1, weight2_t[1])
         quantise(0, slice(P, TOKENS))
@@ -413,126 +409,106 @@ def tile_modulatemlp_pa_kernel(tc, x, w_bytes, w_scale, weight, style_w, style_b
         quantise(0, slice(TOKENS, 3 * P))
         make_style(1)
         quantise_raw(0)
-        modulate_raw(1)
-        turn_x(6)
-        product(2)
-        product(3)
-        turn_early(1)
-        modulate(2)
-        modulate(3, 0, 2)
-        square_style(1)
+        if 1 in raw_pairs:
+            modulate_raw(1)
+        modulate(2, 0, 3)
 
-        def turn_plain(u, j):
-            for k in range(PACK):
-                turn_back(u, j, k)
+        def turned_in(i):
+            return [u for u in (i - 2, i - 1) if 0 <= u <= LAST and summed(u) == (u == i - 2)]
 
-        def open_tile(u, end=PACK):
-            for k in range(1, end):
-                turn_back(u, 1, k)
-            turn_back(u, 1, 0, stop=False)
-
-        for i in range(PLAIN_FROM):
-            p = i // 2 + 2
+        for i in range(LAST - 1):
+            p = (i + 3) // 2
             even = i % 2 == 0
-            ahead = p + 1 if even else p + 2
-            late = ahead in raw_pairs and ahead not in early_pairs
-            if 0 <= i - 2:
-                finish(i - 2, 0)
-            if even and p - 1 < PAIRS:
-                quantise(p - 1)
-                quantise_raw(p - 1)
-            if i == 0:
-                quantise_style2(1)
-            if even and p in raw_pairs:
+            if not even and p in raw_pairs:
                 modulate_raw(p)
-            if i + 1 <= LAST:
-                demodulate(nc.vector, 2 * i + 2, on_vector(i + 1))
+            if even and p < PAIRS:
+                modulate(2 * p, 3, 1)
+            if i <= LAST:
+                demodulate(nc.vector, 2 * i + 1, on_vector(i))
+            tiles = [(u, j) for u in turned_in(i - 1) for j in range(J)]
+            held = tiles[-1:] if even and p < PAIRS else []
+            for u, j in tiles[: len(tiles) - len(held)]:
+                finish(u, j)
+            if i == 3:
+                close_groups(0, 1)
+            elif 3 < i and not even:
+                close_groups(i - 4, 2)
 
             if p < PAIRS:
-                for t in range(4 * p, 4 * p + 2) if even else range(4 * p + 2, 4 * p + own_tiles(p)):
+                for t in range(4 * p + 2, 4 * p + own_tiles(p)) if even else range(4 * p, 4 * p + 2):
                     turn_x(t)
-                if late and not even:
-                    turn_tile(x_banks[1], 1, x_rows(4 * ahead + 3))
-            if i < 1:
-                for b in range(2, EARLY_BANKS):
-                    turn_early(b)
-            if 0 <= i - 1:
-                turn_plain(i - 1, 0)
-            if summed(i - 2):
-                open_tile(i - 2, PACK - 1 if i % PRODUCT_EVERY == 0 else PACK)
+                if even and p + 2 in raw_pairs and p + 2 not in early_pairs:
+                    turn_tile(x_banks[1], 1, x_rows(4 * (p + 2) + 3))
+            for u in turned_in(i):
+                for j in range(J):
+                    turn_back(u, j)
+
+            if p < PAIRS and not even:
+                modulate(2 * p, 0, 3)
+            if p < PAIRS and even:
+                modulate(2 * p + 1, 0, 2)
+                if p not in raw_pairs:
+                    modulate(2 * p + 1, 2, 2)
+                for u, j in held:
+                    finish(u, j)
+                if i == 0:
+                    square_style(1)
+                quantise(p)
+                quantise_raw(p)
+                if i == 0:
+                    quantise_style2(1)
 
             parts = [] if i > LAST else on_scalar(i)[2 * PACK :] if i == 0 else on_scalar(i)
-            cut = len(parts) - 2 * PACK + (RELU1_AT if i < TAIL_FROM else RELU1_TAIL)
-            for q, part in parts[:cut]:
+            for q, part in parts[:PACK]:
                 demodulate(nc.scalar, q, [part])
-            if late and even:
-                copy_words(nc.scalar.copy, at(raw, p + 1 - FIRST_RAW)[:], x_banks[1], slice(P, 2 * P))
+            if even and summed(i):
+                take_negative(i // 2, 0 if i else J)
+            if not even and p + 1 in raw_pairs and p + 1 not in early_pairs:
+                copy_raw(p + 1, x_banks[1], 1)
+            for q, part in parts[PACK:]:
+                demodulate(nc.scalar, q, [part])
             if i == 1:
-                copy_early(1)
-            if not even and i <= LAST and summed(i):
-                take_negative(i // 2)
-            if summed(i - 3):
-                take_relu(i - 3, 1)
-                finish(i - 3, 1)
-                if even and 0 < i // 2 - 1 < FINE_FROM:
-                    close_batch(i // 2 - 1)
-            if p < PAIRS:
-                modulate(2 * p, 0, 3) if even else modulate(2 * p, 3, 1)
-            if p < PAIRS and not even:
-                modulate(2 * p + 1, 0, 2 * own_tiles(p) - GROUP_SAMPLES)
-            for q, part in parts[cut:]:
-                demodulate(nc.scalar, q, [part])
-            if i == 1 and EARLY_BANKS > 2:
-                copy_early(2)
+                for b in range(1, EARLY_BANKS):
+                    copy_early(b)
             if i == 2:
-                take_root(1, z_banks[0], range(PACK))
+                take_root(1, z_banks[3], range(PACK))
 
-            if 0 <= i - 1:
-                take_relu(i - 1, 0)
-            if 0 < i and 2 * i + 3 < 2 * GROUPS:
+            for u in turned_in(i):
+                for j in range(J if summed(u) else 0):
+                    add_steep(u, j)
+            if i < LAST:
+                product(2 * i + 2)
                 product(2 * i + 3)
-            if summed(i - 2):
-                add_steep(i - 2)
-                if i % PRODUCT_EVERY == 0:
-                    turn_back(i - 2, 1, PACK - 1, as_product=True)
-            if 2 * i + 4 < 2 * GROUPS:
-                product(2 * i + 4)
+            if i == 0:
+                for b in range(1, EARLY_BANKS):
+                    turn_early(b)
             if i == 1:
-                d_product(1, z_banks[0], range(PACK))
+                d_product(1, z_banks[3], range(PACK))
+            for u in turned_in(i):
+                for j in range(J):
+                    take_relu(u, j)
 
-        def scalar_parts(u, first, last):
-            for q, part in on_scalar(u)[first:last]:
-                demodulate(nc.scalar, q, [part])
-
-        u = PLAIN_FROM
-        finish(u - 2, 0)
-        turn_plain(u - 1, 0)
-        open_tile(u - 2)
-        scalar_parts(u, 0, None)
-        demodulate(nc.vector, 2 * u + 2, by_tile)
-        take_relu(u - 3, 1)
-        finish(u - 3, 1)
-        product(2 * u + 3)
-        add_steep(u - 2)
-        demodulate(nc.vector, 2 * u + 3, by_tile[:PACK])
-        take_relu(u - 1, 0)
-        demodulate(nc.scalar, 2 * u + 3, by_tile[PACK:])
-        turn_plain(u, 0)
-        open_tile(u - 1)
-        finish(u - 1, 0)
-        take_relu(u - 2, 1)
-        add_steep(u - 1)
-        finish(u - 2, 1)
-        turn_plain(u, 1)
-        take_relu(u, 0)
-        turn_plain(u + 1, 0)
-        finish(u, 0)
-        take_relu(u - 1, 1)
-        turn_plain(u + 1, 1)
-        take_relu(u, 1)
-        finish(u - 1, 1)
-        take_relu(u + 1, 0)
-        finish(u, 1)
-        take_relu(u + 1, 1)
-        finish(u + 1, 0)
-        finish(u + 1, 1)
+        u = LAST - 1
+        for h in range(2):
+            product(2 * LAST + h, bank=x_banks[h])
+        demodulate(nc.vector, 2 * LAST, by_tile, x_banks[0])
+        for j in range(J):
+            finish(u - 3, j)
+        for j in range(J):
+            turn_back(u - 2, j)
+        for j in range(J):
+            add_steep(u - 2, j)
+        for j in range(J):
+            turn_back(u - 1, j)
+        free_banks[:0] = y_banks + x_banks
+        demodulate(nc.vector, 2 * LAST + 1, by_tile[:TAIL_LAST], x_banks[1])
+        for q, part in on_scalar(u):
+            demodulate(nc.scalar, q, [part])
+        demodulate(nc.scalar, 2 * LAST + 1, by_tile[TAIL_LAST:], x_banks[1])
+        for g in (u, LAST):
+            for j in range(J):
+                turn_back(g, j)
+        for g in range(u - 2, GROUPS):
+            for j in range(J):
+                take_relu(g, j)
+                finish(g, j)

@@ -33,14 +33,11 @@ LAST = GROUPS - 1
 RAW_PAIRS = range(1, PAIRS)
 EARLY_BANKS = 3
 PLAIN_FROM = GROUPS - 3
-ON_VECTOR = (1, 2)
-RAMP_VECTOR = (0, 4)
-TAIL_VECTOR = (8, 0)
-TAIL_LAST = 8
-TAIL_CUT = 12
-TAIL_FROM = GROUPS - 3
-ON_SCALAR = 0
-FINE_FROM = 27
+ON_VECTOR = (1, 3)
+RAMP = {0: 0, 1: 0, 2: 4, 29: 4}
+SINGLY_FROM = 26
+TAIL_LAST = 6
+ONE_ADD = 1
 FINISHED = 9
 
 
@@ -150,7 +147,10 @@ def tile_modulatemlp_pa_kernel(tc, x, w_bytes, w_scale, weight, style_w, style_b
         scales = ring("scales", 2, [P, 2 * TOKENS], U8)
         z = ring("z", 2, [P, 2 * J * O], F32)
         negative = ring("negative", 2, [P, 2 * J * P], F32)
-        relu = ring("relu", 6, [P, O], F32)
+        relu = [ring("relu%d_" % j, 3, [P, O], F32) for j in range(J)]
+        for j in range(ONE_ADD):
+            for tile in relu[j]:
+                nc.vector.memset(tile[:, :P], 0.0)
         finished = ring("finished", FINISHED, [P, 2 * J * O], F32)
 
         def turn_tile(bank, j, rows):
@@ -304,45 +304,59 @@ def tile_modulatemlp_pa_kernel(tc, x, w_bytes, w_scale, weight, style_w, style_b
                              rhs=steep_ident[:], start=False, stop=True)
 
         def rows(u, j):
-            place = (u + 1) % 2 * J + j
-            return at(finished, (u + 1) // 2)[:, place * O : (place + 1) * O]
+            place = u % 2 * J + 1 - j
+            return at(finished, u // 2)[:, place * O : (place + 1) * O]
 
         def relu_tile(u, j):
-            return at(relu, J * u + j)
+            return at(relu[j], u)
 
         def take_relu(u, j):
             first = P if summed(u) else 0
             nc.scalar.activation(out=relu_tile(u, j)[:, first:], in_=z_bank(u, j)[:, first:], func=ACT.Relu, scale=-(1.0 - SLOPE))
-            if first and ON_SCALAR:
-                nc.scalar.copy(out=rows(u, j)[:, P - ON_SCALAR : P], in_=z_bank(u, j)[:, P - ON_SCALAR : P])
 
         def finish(u, j):
-            first = P if summed(u) else 0
+            first = P if summed(u) and j >= ONE_ADD else 0
             bank = z_bank(u, j)
             nc.vector.tensor_tensor(out=rows(u, j)[:, first:], in0=bank[:, first:], in1=relu_tile(u, j)[:, first:], op=ALU.add)
             if first:
-                first = P - ON_SCALAR
                 nc.vector.tensor_scalar(out=rows(u, j)[:, :first], in0=bank[:, :first],
                                         scalar1=CLAMP, scalar2=-CLAMP, op0=ALU.min, op1=ALU.max)
             free_banks.append(bank)
-            if u >= FINE_FROM:
-                engine = nc.vector if (u, j) == (LAST, J - 1) else nc.gpsimd
-                plain = rows(u, j)[:, first:]
-                engine.tensor_scalar(out=plain, in0=plain, scalar1=CLAMP, scalar2=-CLAMP, op0=ALU.min, op1=ALU.max)
-                nc.sync.dma_start(out=out_view[:, J * u + j, :], in_=rows(u, j))
 
-        def close_groups(u, count):
-            place = (u + 1) % 2 * J
-            tiles = at(finished, (u + 1) // 2)[:].rearrange("p (t o) -> p t o", o=O)[:, place : place + J * count]
-            plain = tiles[:, :, P - ON_SCALAR :]
+        def store(u, j):
+            nc.sync.dma_start(out=out_view[:, J * u + j, :], in_=rows(u, j))
+
+        def clip_rows(engine, u, j):
+            engine.tensor_scalar(out=rows(u, j), in0=rows(u, j), scalar1=CLAMP, scalar2=-CLAMP, op0=ALU.min, op1=ALU.max)
+
+        def clip_before(u):
+            first = (u + 1) % 2 * J * O
+            tiles = at(z, (u + 1) // 2)[:, first : first + J * O]
+            nc.gpsimd.tensor_scalar(out=tiles, in0=tiles, scalar1=CLAMP, scalar2=-CLAMP / SLOPE, op0=ALU.min, op1=ALU.max)
+
+        def close_group(u):
+            tiles = at(finished, u // 2)[:, u % 2 * J * O : (u % 2 + 1) * J * O]
+            plain = tiles[:, P if summed(u) else 0 :]
             nc.gpsimd.tensor_scalar(out=plain, in0=plain, scalar1=CLAMP, scalar2=-CLAMP, op0=ALU.min, op1=ALU.max)
-            nc.sync.dma_start(out=out_view[:, J * u : J * (u + count), :], in_=tiles)
+            for j in range(J):
+                store(u, j)
+
+        def close_pair(n, groups=2):
+            plain = at(finished, n)[:].rearrange("p (g c) -> p g c", g=2)[:, :groups, P:]
+            nc.gpsimd.tensor_scalar(out=plain, in0=plain, scalar1=CLAMP, scalar2=-CLAMP, op0=ALU.min, op1=ALU.max)
+            tiles = at(finished, n)[:].rearrange("p (g j o) -> p j g o", g=2, j=J)
+            for j in range(J):
+                nc.sync.dma_start(out=out_view[:, 4 * n + j : 4 * n + J * groups : 2, :], in_=tiles[:, 1 - j, :groups])
 
         by_block = [(e, n) for e in range(2) for n in range(GROUP_SAMPLES)]
         by_tile = [(e, n) for n in range(GROUP_SAMPLES) for e in range(2)]
 
+        def copies_in(i):
+            ahead = (i + 3) // 2 + 1
+            return i % 2 == 1 and ahead in raw_pairs and ahead not in early_pairs
+
         def on_vector(u):
-            count = 0 if u < 1 else RAMP_VECTOR[u - 1] if u < 1 + len(RAMP_VECTOR) else ON_VECTOR[u % 2] if u < TAIL_FROM else TAIL_VECTOR[u - TAIL_FROM]
+            count = RAMP.get(u, ON_VECTOR[1] if copies_in(u) else 0 if u % 2 or copies_in(u + 1) else ON_VECTOR[0])
             return by_tile[:count]
 
         def on_scalar(u):
@@ -411,7 +425,7 @@ def tile_modulatemlp_pa_kernel(tc, x, w_bytes, w_scale, weight, style_w, style_b
         quantise_raw(0)
         if 1 in raw_pairs:
             modulate_raw(1)
-        modulate(2, 0, 3)
+        modulate(2)
 
         def turned_in(i):
             return [u for u in (i - 2, i - 1) if 0 <= u <= LAST and summed(u) == (u == i - 2)]
@@ -419,20 +433,12 @@ def tile_modulatemlp_pa_kernel(tc, x, w_bytes, w_scale, weight, style_w, style_b
         for i in range(LAST - 1):
             p = (i + 3) // 2
             even = i % 2 == 0
-            if not even and p in raw_pairs:
-                modulate_raw(p)
-            if even and p < PAIRS:
-                modulate(2 * p, 3, 1)
             if i <= LAST:
                 demodulate(nc.vector, 2 * i + 1, on_vector(i))
             tiles = [(u, j) for u in turned_in(i - 1) for j in range(J)]
             held = tiles[-1:] if even and p < PAIRS else []
             for u, j in tiles[: len(tiles) - len(held)]:
                 finish(u, j)
-            if i == 3:
-                close_groups(0, 1)
-            elif 3 < i and not even:
-                close_groups(i - 4, 2)
 
             if p < PAIRS:
                 for t in range(4 * p + 2, 4 * p + own_tiles(p)) if even else range(4 * p, 4 * p + 2):
@@ -443,8 +449,13 @@ def tile_modulatemlp_pa_kernel(tc, x, w_bytes, w_scale, weight, style_w, style_b
                 for j in range(J):
                     turn_back(u, j)
 
+            parts = [] if i > LAST else on_scalar(i)[2 * PACK :] if i == 0 else on_scalar(i)
+            for q, part in parts[:PACK]:
+                demodulate(nc.scalar, q, [part])
+            if even and summed(i):
+                take_negative(i // 2, 0 if i else J)
             if p < PAIRS and not even:
-                modulate(2 * p, 0, 3)
+                modulate(2 * p)
             if p < PAIRS and even:
                 modulate(2 * p + 1, 0, 2)
                 if p not in raw_pairs:
@@ -453,17 +464,16 @@ def tile_modulatemlp_pa_kernel(tc, x, w_bytes, w_scale, weight, style_w, style_b
                     finish(u, j)
                 if i == 0:
                     square_style(1)
-                quantise(p)
                 quantise_raw(p)
                 if i == 0:
                     quantise_style2(1)
+                quantise(p)
+            if even and 0 <= i - 4 < SINGLY_FROM:
+                close_pair(i // 2 - 2)
+            if even and p + 1 in raw_pairs:
+                modulate_raw(p + 1)
 
-            parts = [] if i > LAST else on_scalar(i)[2 * PACK :] if i == 0 else on_scalar(i)
-            for q, part in parts[:PACK]:
-                demodulate(nc.scalar, q, [part])
-            if even and summed(i):
-                take_negative(i // 2, 0 if i else J)
-            if not even and p + 1 in raw_pairs and p + 1 not in early_pairs:
+            if copies_in(i):
                 copy_raw(p + 1, x_banks[1], 1)
             for q, part in parts[PACK:]:
                 demodulate(nc.scalar, q, [part])
@@ -488,27 +498,41 @@ def tile_modulatemlp_pa_kernel(tc, x, w_bytes, w_scale, weight, style_w, style_b
                 for j in range(J):
                     take_relu(u, j)
 
+        def each_tile(step, g):
+            for j in range(J):
+                step(g, j)
+
         u = LAST - 1
+        clip_before(u - 1)
+        close_group(u - 4)
+        each_tile(turn_back, u - 2)
+        each_tile(add_steep, u - 2)
         for h in range(2):
             product(2 * LAST + h, bank=x_banks[h])
-        demodulate(nc.vector, 2 * LAST, by_tile, x_banks[0])
-        for j in range(J):
-            finish(u - 3, j)
-        for j in range(J):
-            turn_back(u - 2, j)
-        for j in range(J):
-            add_steep(u - 2, j)
-        for j in range(J):
-            turn_back(u - 1, j)
+        each_tile(finish, u - 3)
+        close_group(u - 3)
+        each_tile(turn_back, u - 1)
         free_banks[:0] = y_banks + x_banks
+        demodulate(nc.scalar, 2 * u, by_tile)
+        demodulate(nc.vector, 2 * u + 1, by_tile)
+        each_tile(take_relu, u - 2)
+        each_tile(finish, u - 2)
+        close_group(u - 2)
+        each_tile(turn_back, u)
+        demodulate(nc.scalar, 2 * LAST, by_tile, x_banks[0])
         demodulate(nc.vector, 2 * LAST + 1, by_tile[:TAIL_LAST], x_banks[1])
-        for q, part in on_scalar(u):
-            demodulate(nc.scalar, q, [part])
+        each_tile(take_relu, u - 1)
         demodulate(nc.scalar, 2 * LAST + 1, by_tile[TAIL_LAST:], x_banks[1])
-        for g in (u, LAST):
-            for j in range(J):
-                turn_back(g, j)
-        for g in range(u - 2, GROUPS):
-            for j in range(J):
-                take_relu(g, j)
-                finish(g, j)
+        each_tile(turn_back, LAST)
+        each_tile(finish, u - 1)
+        each_tile(store, u - 1)
+        each_tile(take_relu, u)
+        for j in range(J):
+            finish(u, j)
+            clip_rows(nc.gpsimd, u, j)
+            store(u, j)
+        each_tile(take_relu, LAST)
+        each_tile(finish, LAST)
+        for j in range(J):
+            clip_rows(nc.vector, LAST, j)
+            store(LAST, j)

@@ -36,8 +36,7 @@ PLAIN_FROM = GROUPS - 3
 ON_VECTOR = (1, 3)
 RAMP = {0: 0, 1: 0, 2: 4, 29: 4}
 SINGLY_FROM = 26
-TAIL_LAST = 6
-ONE_ADD = 1
+TAIL_LAST = 4
 FINISHED = 9
 
 
@@ -147,10 +146,7 @@ def tile_modulatemlp_pa_kernel(tc, x, w_bytes, w_scale, weight, style_w, style_b
         scales = ring("scales", 2, [P, 2 * TOKENS], U8)
         z = ring("z", 2, [P, 2 * J * O], F32)
         negative = ring("negative", 2, [P, 2 * J * P], F32)
-        relu = [ring("relu%d_" % j, 3, [P, O], F32) for j in range(J)]
-        for j in range(ONE_ADD):
-            for tile in relu[j]:
-                nc.vector.memset(tile[:, :P], 0.0)
+        relu = ring("relu", 6, [P, O], F32)
         finished = ring("finished", FINISHED, [P, 2 * J * O], F32)
 
         def turn_tile(bank, j, rows):
@@ -304,18 +300,18 @@ def tile_modulatemlp_pa_kernel(tc, x, w_bytes, w_scale, weight, style_w, style_b
                              rhs=steep_ident[:], start=False, stop=True)
 
         def rows(u, j):
-            place = u % 2 * J + 1 - j
+            place = u % 2 * J + j
             return at(finished, u // 2)[:, place * O : (place + 1) * O]
 
         def relu_tile(u, j):
-            return at(relu[j], u)
+            return at(relu, J * u + j)
 
         def take_relu(u, j):
             first = P if summed(u) else 0
             nc.scalar.activation(out=relu_tile(u, j)[:, first:], in_=z_bank(u, j)[:, first:], func=ACT.Relu, scale=-(1.0 - SLOPE))
 
         def finish(u, j):
-            first = P if summed(u) and j >= ONE_ADD else 0
+            first = P if summed(u) else 0
             bank = z_bank(u, j)
             nc.vector.tensor_tensor(out=rows(u, j)[:, first:], in0=bank[:, first:], in1=relu_tile(u, j)[:, first:], op=ALU.add)
             if first:
@@ -334,19 +330,12 @@ def tile_modulatemlp_pa_kernel(tc, x, w_bytes, w_scale, weight, style_w, style_b
             tiles = at(z, (u + 1) // 2)[:, first : first + J * O]
             nc.gpsimd.tensor_scalar(out=tiles, in0=tiles, scalar1=CLAMP, scalar2=-CLAMP / SLOPE, op0=ALU.min, op1=ALU.max)
 
-        def close_group(u):
-            tiles = at(finished, u // 2)[:, u % 2 * J * O : (u % 2 + 1) * J * O]
-            plain = tiles[:, P if summed(u) else 0 :]
+        def close_groups(u, count):
+            first = u % 2 * J
+            tiles = at(finished, u // 2)[:].rearrange("p (t o) -> p t o", o=O)[:, first : first + J * count]
+            plain = tiles[:, :, P:]
             nc.gpsimd.tensor_scalar(out=plain, in0=plain, scalar1=CLAMP, scalar2=-CLAMP, op0=ALU.min, op1=ALU.max)
-            for j in range(J):
-                store(u, j)
-
-        def close_pair(n, groups=2):
-            plain = at(finished, n)[:].rearrange("p (g c) -> p g c", g=2)[:, :groups, P:]
-            nc.gpsimd.tensor_scalar(out=plain, in0=plain, scalar1=CLAMP, scalar2=-CLAMP, op0=ALU.min, op1=ALU.max)
-            tiles = at(finished, n)[:].rearrange("p (g j o) -> p j g o", g=2, j=J)
-            for j in range(J):
-                nc.sync.dma_start(out=out_view[:, 4 * n + j : 4 * n + J * groups : 2, :], in_=tiles[:, 1 - j, :groups])
+            nc.sync.dma_start(out=out_view[:, J * u : J * (u + count), :], in_=tiles)
 
         by_block = [(e, n) for e in range(2) for n in range(GROUP_SAMPLES)]
         by_tile = [(e, n) for n in range(GROUP_SAMPLES) for e in range(2)]
@@ -408,14 +397,14 @@ def tile_modulatemlp_pa_kernel(tc, x, w_bytes, w_scale, weight, style_w, style_b
         take_root(0, z_banks[0], range(0, 2))
         demodulate(nc.scalar, 0, by_tile[:PACK], y_banks[1])
         modulate(0, 2, 2)
+        turn_x(4)
+        turn_x(5)
         quantise_half(weight2_q, weight2_s, 1, weight2_t[1])
         quantise(0, slice(P, TOKENS))
         quantise_half(weight_q, weight_s, 1, weight_t[1])
         product(0, slice(P, TOKENS))
         d_product(0, z_banks[1], range(2, PACK))
         product(1)
-        turn_x(4)
-        turn_x(5)
         demodulate(nc.scalar, 0, by_tile[PACK:])
         take_root(0, z_banks[1], range(2, PACK))
         modulate(1, 0, 2)
@@ -445,6 +434,9 @@ def tile_modulatemlp_pa_kernel(tc, x, w_bytes, w_scale, weight, style_w, style_b
                     turn_x(t)
                 if even and p + 2 in raw_pairs and p + 2 not in early_pairs:
                     turn_tile(x_banks[1], 1, x_rows(4 * (p + 2) + 3))
+            if i == 1:
+                for b in range(1, EARLY_BANKS):
+                    turn_early(b)
             for u in turned_in(i):
                 for j in range(J):
                     turn_back(u, j)
@@ -452,8 +444,8 @@ def tile_modulatemlp_pa_kernel(tc, x, w_bytes, w_scale, weight, style_w, style_b
             parts = [] if i > LAST else on_scalar(i)[2 * PACK :] if i == 0 else on_scalar(i)
             for q, part in parts[:PACK]:
                 demodulate(nc.scalar, q, [part])
-            if even and summed(i):
-                take_negative(i // 2, 0 if i else J)
+            if even and i and summed(i):
+                take_negative(i // 2)
             if p < PAIRS and not even:
                 modulate(2 * p)
             if p < PAIRS and even:
@@ -469,9 +461,11 @@ def tile_modulatemlp_pa_kernel(tc, x, w_bytes, w_scale, weight, style_w, style_b
                     quantise_style2(1)
                 quantise(p)
             if even and 0 <= i - 4 < SINGLY_FROM:
-                close_pair(i // 2 - 2)
+                close_groups(i - 4, 2)
             if even and p + 1 in raw_pairs:
                 modulate_raw(p + 1)
+            if i == 0:
+                take_negative(0, J)
 
             if copies_in(i):
                 copy_raw(p + 1, x_banks[1], 1)
@@ -489,9 +483,6 @@ def tile_modulatemlp_pa_kernel(tc, x, w_bytes, w_scale, weight, style_w, style_b
             if i < LAST:
                 product(2 * i + 2)
                 product(2 * i + 3)
-            if i == 0:
-                for b in range(1, EARLY_BANKS):
-                    turn_early(b)
             if i == 1:
                 d_product(1, z_banks[3], range(PACK))
             for u in turned_in(i):
@@ -504,20 +495,20 @@ def tile_modulatemlp_pa_kernel(tc, x, w_bytes, w_scale, weight, style_w, style_b
 
         u = LAST - 1
         clip_before(u - 1)
-        close_group(u - 4)
+        close_groups(u - 4, 1)
         each_tile(turn_back, u - 2)
         each_tile(add_steep, u - 2)
         for h in range(2):
             product(2 * LAST + h, bank=x_banks[h])
         each_tile(finish, u - 3)
-        close_group(u - 3)
+        close_groups(u - 3, 1)
         each_tile(turn_back, u - 1)
         free_banks[:0] = y_banks + x_banks
         demodulate(nc.scalar, 2 * u, by_tile)
         demodulate(nc.vector, 2 * u + 1, by_tile)
         each_tile(take_relu, u - 2)
         each_tile(finish, u - 2)
-        close_group(u - 2)
+        close_groups(u - 2, 1)
         each_tile(turn_back, u)
         demodulate(nc.scalar, 2 * LAST, by_tile, x_banks[0])
         demodulate(nc.vector, 2 * LAST + 1, by_tile[:TAIL_LAST], x_banks[1])

@@ -33,10 +33,13 @@ LAST = GROUPS - 1
 RAW_PAIRS = range(1, PAIRS)
 EARLY_BANKS = 3
 PLAIN_FROM = GROUPS - 3
-ON_VECTOR = (1, 3)
+ON_VECTOR = (1, 0)
 RAMP = {0: 0, 1: 0, 2: 4, 29: 4}
 SINGLY_FROM = 26
 TAIL_LAST = 4
+VCOPY = 1
+SUMMED_FROM = 0
+TAIL_MID = 8
 FINISHED = 9
 
 
@@ -71,13 +74,13 @@ def tile_modulatemlp_pa_kernel(tc, x, w_bytes, w_scale, weight, style_w, style_b
         style_w_view = style_w.rearrange("(m h e) l -> h m e l", h=2, e=2)
         weight_view = weight.rearrange("(h e m) c -> h m e c", h=2, e=2)
         nc.sync.dma_start(out=w_codes[:], in_=w_bytes)
+        nc.sync.dma_start(out=weight_sb[0][:], in_=weight_view[0])
         for h in range(2):
             nc.sync.dma_start(out=style_w_sb[h][:], in_=style_w_view[h])
         nc.scalar.dma_start(out=w_scale_sb[:], in_=w_scale.rearrange("o (p t) -> p (o t)", t=PACK))
         nc.scalar.dma_start(out=style_b_sb[:], in_=style_b.rearrange("(p t) -> p t", t=PACK))
         nc.scalar.dma_start(out=bias_sb[:], in_=bias.rearrange("(k m) -> k m", k=PACK))
-        for h in range(2):
-            nc.sync.dma_start(out=weight_sb[h][:], in_=weight_view[h])
+        nc.sync.dma_start(out=weight_sb[1][:], in_=weight_view[1])
 
         x_first = ring("x_first", 2, [P, J, C], BF16)
         x_pairs = [None] + ring("x_pair", PAIRS - 1, [P, 2 * J, C], BF16)
@@ -204,15 +207,15 @@ def tile_modulatemlp_pa_kernel(tc, x, w_bytes, w_scale, weight, style_w, style_b
 
         early_banks = [z_banks[3], z_banks[0], z_banks[1]]
 
-        def turn_early(b):
-            for n in range(2 * b, min(2 * b + 2, len(early_pairs))):
-                turn_tile(early_banks[b], n % 2, x_early[n][:])
+        def turn_early(b, tiles=range(2)):
+            for j in tiles:
+                turn_tile(early_banks[b], j, x_early[2 * b + j][:])
 
         def raw_tile(p):
             return at(raw, raw_pairs.index(p))
 
-        def copy_raw(p, bank, j):
-            copy_words(nc.scalar.copy, raw_tile(p)[:], bank, slice(j * P, (j + 1) * P))
+        def copy_raw(p, bank, j, engine_copy=nc.scalar.copy):
+            copy_words(engine_copy, raw_tile(p)[:], bank, slice(j * P, (j + 1) * P))
 
         def copy_early(b):
             for n in range(2 * b, min(2 * b + 2, len(early_pairs))):
@@ -257,7 +260,7 @@ def tile_modulatemlp_pa_kernel(tc, x, w_bytes, w_scale, weight, style_w, style_b
             return at(z, (u + 1) // 2)[:, first : first + P]
 
         def summed(u):
-            return 0 <= u < PLAIN_FROM
+            return SUMMED_FROM <= u < PLAIN_FROM
 
         def demodulate(engine, q, parts, bank=None):
             u, h = divmod(q, 2)
@@ -333,7 +336,7 @@ def tile_modulatemlp_pa_kernel(tc, x, w_bytes, w_scale, weight, style_w, style_b
         def close_groups(u, count):
             first = u % 2 * J
             tiles = at(finished, u // 2)[:].rearrange("p (t o) -> p t o", o=O)[:, first : first + J * count]
-            plain = tiles[:, :, P:]
+            plain = tiles[:, :, P if summed(u) else 0 :]
             nc.gpsimd.tensor_scalar(out=plain, in0=plain, scalar1=CLAMP, scalar2=-CLAMP, op0=ALU.min, op1=ALU.max)
             nc.sync.dma_start(out=out_view[:, J * u : J * (u + count), :], in_=tiles)
 
@@ -356,6 +359,7 @@ def tile_modulatemlp_pa_kernel(tc, x, w_bytes, w_scale, weight, style_w, style_b
         w_words = w_bf[:].bitcast(F32)
         for u in range(2):
             nc.tensor.transpose(w_bank[:, u * P : (u + 1) * P], w_words[:, u::2], ident[:])
+        turn_rows(z_banks[0], weight_sb[0])
         for h in range(2):
             turn_rows(y_banks[h], style_w_sb[h])
         nc.vector.tensor_tensor(
@@ -363,50 +367,53 @@ def tile_modulatemlp_pa_kernel(tc, x, w_bytes, w_scale, weight, style_w, style_b
             in0=w_bank[:, : 2 * P].bitcast(BF16).rearrange("p (u n e) -> p n u e", u=2, e=2),
             in1=w_scale_sb[:].rearrange("p (u e) -> p u e", e=2).unsqueeze(1).to_broadcast([P, SAMPLES, 2, 2]),
             op=ALU.mult)
-        copy_words(nc.scalar.copy, style_w_t[0][:], y_banks[0])
+        copy_words(nc.scalar.copy, weight_t[0][:], z_banks[0])
         nc.vector.tensor_scalar(out=bias_rows[:PACK, :], in0=bias_sb[:], scalar1=GAIN, scalar2=None, op0=ALU.mult)
         nc.vector.quantize_mx(out=w_q[:].bitcast(X4), scales=w_s[:], in_=w_t[:].rearrange("p n k -> p (n k)"))
-        copy_words(nc.scalar.copy, style_w_t[1][:], y_banks[1])
-        nc.tensor.transpose(w_bank[:, :P], bias_rows[:], ident[:])
-        quantise_half(style_w_q, style_w_s, 0, style_w_t[0])
-        nc.vector.tensor_copy(out=bias_gain[:], in_=w_bank[:, :PACK])
-        quantise_half(style_w_q, style_w_s, 1, style_w_t[1])
         for h in range(2):
-            turn_rows(z_banks[h], weight_sb[h])
+            copy_words(nc.scalar.copy, style_w_t[h][:], y_banks[h])
+        nc.tensor.transpose(w_bank[:, :P], bias_rows[:], ident[:])
+        turn_rows(z_banks[1], weight_sb[1])
+        nc.vector.tensor_tensor(out=weight2_t[0][:], in0=weight_t[0][:], in1=weight_t[0][:], op=ALU.mult)
+        quantise_half(style_w_q, style_w_s, 0, style_w_t[0])
+        quantise_half(weight_q, weight_s, 0, weight_t[0])
+        quantise_half(style_w_q, style_w_s, 1, style_w_t[1])
+        turn_x(0)
         for t in range(PACK):
             cols = slice(t * P, (t + 1) * P)
             nc.tensor.matmul_mx(out=style_bank[:, cols], lhsT=style_w_q[:, cols].bitcast(X4), lhsT_scale=style_w_s[:, cols],
                                 rhs=w_q[:].bitcast(X4), rhs_scale=w_s[:], start=True, stop=True)
-        for t in range(2 * J):
+        for t in range(1, 2 * J):
             turn_x(t)
-        turn_early(0)
-        for h in range(2):
-            copy_words(nc.scalar.copy, weight_t[h][:], z_banks[h])
+        copy_words(nc.scalar.copy, weight_t[1][:], z_banks[1])
         nc.scalar.activation(out=weight2_t[1][:], in_=weight_t[1][:], func=ACT.Square)
-        nc.vector.tensor_tensor(out=weight2_t[0][:], in0=weight_t[0][:], in1=weight_t[0][:], op=ALU.mult)
-        quantise_half(weight_q, weight_s, 0, weight_t[0])
-        make_style(0)
+        nc.vector.tensor_copy(out=bias_gain[:], in_=w_bank[:, :PACK])
+        turn_early(0)
         quantise_half(weight2_q, weight2_s, 0, weight2_t[0])
+        quantise_half(weight_q, weight_s, 1, weight_t[1])
+        make_style(0)
         square_style(0)
         modulate(0, 0, 2)
         quantise_style2(0)
         quantise(0, slice(0, P))
-        d_product(0, z_banks[0], range(0, 2))
+        turn_early(1, [0])
+        d_product(0, y_banks[0], range(0, 2))
         product(0, slice(0, P), y_banks[1])
+        turn_early(1, [1])
         copy_early(0)
-        take_root(0, z_banks[0], range(0, 2))
+        take_root(0, y_banks[0], range(0, 2))
         demodulate(nc.scalar, 0, by_tile[:PACK], y_banks[1])
+        copy_early(1)
         modulate(0, 2, 2)
         turn_x(4)
         turn_x(5)
         quantise_half(weight2_q, weight2_s, 1, weight2_t[1])
         quantise(0, slice(P, TOKENS))
-        quantise_half(weight_q, weight_s, 1, weight_t[1])
         product(0, slice(P, TOKENS))
-        d_product(0, z_banks[1], range(2, PACK))
+        d_product(0, z_banks[3], range(2, PACK))
         product(1)
         demodulate(nc.scalar, 0, by_tile[PACK:])
-        take_root(0, z_banks[1], range(2, PACK))
+        take_root(0, z_banks[3], range(2, PACK))
         modulate(1, 0, 2)
         modulate(1, 2, 2)
         quantise(0, slice(TOKENS, 3 * P))
@@ -417,13 +424,15 @@ def tile_modulatemlp_pa_kernel(tc, x, w_bytes, w_scale, weight, style_w, style_b
         modulate(2)
 
         def turned_in(i):
-            return [u for u in (i - 2, i - 1) if 0 <= u <= LAST and summed(u) == (u == i - 2)]
+            return [i - 2] if i >= 2 else []
 
         for i in range(LAST - 1):
             p = (i + 3) // 2
             even = i % 2 == 0
             if i <= LAST:
                 demodulate(nc.vector, 2 * i + 1, on_vector(i))
+            if copies_in(i) and VCOPY:
+                copy_raw(p + 1, x_banks[1], 1, nc.vector.tensor_copy)
             tiles = [(u, j) for u in turned_in(i - 1) for j in range(J)]
             held = tiles[-1:] if even and p < PAIRS else []
             for u, j in tiles[: len(tiles) - len(held)]:
@@ -435,8 +444,7 @@ def tile_modulatemlp_pa_kernel(tc, x, w_bytes, w_scale, weight, style_w, style_b
                 if even and p + 2 in raw_pairs and p + 2 not in early_pairs:
                     turn_tile(x_banks[1], 1, x_rows(4 * (p + 2) + 3))
             if i == 1:
-                for b in range(1, EARLY_BANKS):
-                    turn_early(b)
+                turn_early(2)
             for u in turned_in(i):
                 for j in range(J):
                     turn_back(u, j)
@@ -464,16 +472,15 @@ def tile_modulatemlp_pa_kernel(tc, x, w_bytes, w_scale, weight, style_w, style_b
                 close_groups(i - 4, 2)
             if even and p + 1 in raw_pairs:
                 modulate_raw(p + 1)
-            if i == 0:
+            if i == 0 and summed(0):
                 take_negative(0, J)
 
-            if copies_in(i):
+            if copies_in(i) and not VCOPY:
                 copy_raw(p + 1, x_banks[1], 1)
             for q, part in parts[PACK:]:
                 demodulate(nc.scalar, q, [part])
             if i == 1:
-                for b in range(1, EARLY_BANKS):
-                    copy_early(b)
+                copy_early(2)
             if i == 2:
                 take_root(1, z_banks[3], range(PACK))
 
@@ -505,8 +512,9 @@ def tile_modulatemlp_pa_kernel(tc, x, w_bytes, w_scale, weight, style_w, style_b
         each_tile(turn_back, u - 1)
         free_banks[:0] = y_banks + x_banks
         demodulate(nc.scalar, 2 * u, by_tile)
-        demodulate(nc.vector, 2 * u + 1, by_tile)
+        demodulate(nc.vector, 2 * u + 1, by_tile[:TAIL_MID])
         each_tile(take_relu, u - 2)
+        demodulate(nc.scalar, 2 * u + 1, by_tile[TAIL_MID:])
         each_tile(finish, u - 2)
         close_groups(u - 2, 1)
         each_tile(turn_back, u)

@@ -33,11 +33,10 @@ LAST = GROUPS - 1
 RAW_PAIRS = range(1, PAIRS)
 EARLY_BANKS = 3
 PLAIN_FROM = GROUPS - 3
-ON_VECTOR = (1, 0)
+ON_VECTOR = (1, 3)
 RAMP = {0: 0, 1: 0, 2: 4, 29: 4}
 SINGLY_FROM = 26
 TAIL_LAST = 4
-VCOPY = 1
 SUMMED_FROM = 0
 TAIL_MID = 8
 FINISHED = 9
@@ -73,8 +72,9 @@ def tile_modulatemlp_pa_kernel(tc, x, w_bytes, w_scale, weight, style_w, style_b
         bias_sb = keep.tile([PACK, P], BF16)
         style_w_view = style_w.rearrange("(m h e) l -> h m e l", h=2, e=2)
         weight_view = weight.rearrange("(h e m) c -> h m e c", h=2, e=2)
+        nc.sync.dma_start(out=weight_sb[0][:, 0], in_=weight_view[0][:, 0])
         nc.sync.dma_start(out=w_codes[:], in_=w_bytes)
-        nc.sync.dma_start(out=weight_sb[0][:], in_=weight_view[0])
+        nc.sync.dma_start(out=weight_sb[0][:, 1], in_=weight_view[0][:, 1])
         for h in range(2):
             nc.sync.dma_start(out=style_w_sb[h][:], in_=style_w_view[h])
         nc.scalar.dma_start(out=w_scale_sb[:], in_=w_scale.rearrange("o (p t) -> p (o t)", t=PACK))
@@ -214,8 +214,8 @@ def tile_modulatemlp_pa_kernel(tc, x, w_bytes, w_scale, weight, style_w, style_b
         def raw_tile(p):
             return at(raw, raw_pairs.index(p))
 
-        def copy_raw(p, bank, j, engine_copy=nc.scalar.copy):
-            copy_words(engine_copy, raw_tile(p)[:], bank, slice(j * P, (j + 1) * P))
+        def copy_raw(p, bank, j):
+            copy_words(nc.scalar.copy, raw_tile(p)[:], bank, slice(j * P, (j + 1) * P))
 
         def copy_early(b):
             for n in range(2 * b, min(2 * b + 2, len(early_pairs))):
@@ -357,9 +357,9 @@ def tile_modulatemlp_pa_kernel(tc, x, w_bytes, w_scale, weight, style_w, style_b
         nc.vector.tensor_copy(out=w_bf[:], in_=w_codes[:].bitcast(FP8))
         w_bank = z_banks[3]
         w_words = w_bf[:].bitcast(F32)
+        turn_rows(z_banks[0], weight_sb[0])
         for u in range(2):
             nc.tensor.transpose(w_bank[:, u * P : (u + 1) * P], w_words[:, u::2], ident[:])
-        turn_rows(z_banks[0], weight_sb[0])
         for h in range(2):
             turn_rows(y_banks[h], style_w_sb[h])
         nc.vector.tensor_tensor(
@@ -431,8 +431,6 @@ def tile_modulatemlp_pa_kernel(tc, x, w_bytes, w_scale, weight, style_w, style_b
             even = i % 2 == 0
             if i <= LAST:
                 demodulate(nc.vector, 2 * i + 1, on_vector(i))
-            if copies_in(i) and VCOPY:
-                copy_raw(p + 1, x_banks[1], 1, nc.vector.tensor_copy)
             tiles = [(u, j) for u in turned_in(i - 1) for j in range(J)]
             held = tiles[-1:] if even and p < PAIRS else []
             for u, j in tiles[: len(tiles) - len(held)]:
@@ -475,7 +473,7 @@ def tile_modulatemlp_pa_kernel(tc, x, w_bytes, w_scale, weight, style_w, style_b
             if i == 0 and summed(0):
                 take_negative(0, J)
 
-            if copies_in(i) and not VCOPY:
+            if copies_in(i):
                 copy_raw(p + 1, x_banks[1], 1)
             for q, part in parts[PACK:]:
                 demodulate(nc.scalar, q, [part])

@@ -30,15 +30,16 @@ GROUPS = SAMPLES // GROUP_SAMPLES
 PAIRS = GROUPS // 2
 HALF = SAMPLES // 2
 LAST = GROUPS - 1
-RAW_PAIRS = range(1, PAIRS)
+RAW_PAIRS = range(1, PAIRS - 1)
 EARLY_BANKS = 3
 PLAIN_FROM = GROUPS - 3
 ON_VECTOR = (1, 3)
-RAMP = {0: 0, 1: 0, 2: 4, 29: 4}
-SINGLY_FROM = 26
-TAIL_LAST = 4
+RAMP = {0: 0, 1: 0, 2: 4, 29: 0}
+SINGLY_FROM = 24
+TAIL_LAST = 8
+EARLY_FIRST = 4
 SUMMED_FROM = 0
-TAIL_MID = 8
+TAIL_MID = 6
 FINISHED = 9
 
 
@@ -107,9 +108,15 @@ def tile_modulatemlp_pa_kernel(tc, x, w_bytes, w_scale, weight, style_w, style_b
 
         for u in range(2):
             nc.sync.dma_start(out=x_first[u][:], in_=x_view[:, u * J : (u + 1) * J, :])
-        for p in range(1, PAIRS):
-            for n in range(2 * p - 2, min(2 * p, len(early_pairs))):
-                load_early(n)
+        for n in range(EARLY_FIRST):
+            load_early(n)
+        load_pair(1)
+        for n in range(EARLY_FIRST, 4):
+            load_early(n)
+        load_pair(2)
+        for n in range(4, len(early_pairs)):
+            load_early(n)
+        for p in range(3, PAIRS):
             load_pair(p)
 
         ident = keep.tile([P, P], F32)
@@ -328,9 +335,9 @@ def tile_modulatemlp_pa_kernel(tc, x, w_bytes, w_scale, weight, style_w, style_b
         def clip_rows(engine, u, j):
             engine.tensor_scalar(out=rows(u, j), in0=rows(u, j), scalar1=CLAMP, scalar2=-CLAMP, op0=ALU.min, op1=ALU.max)
 
-        def clip_before(u):
-            first = (u + 1) % 2 * J * O
-            tiles = at(z, (u + 1) // 2)[:, first : first + J * O]
+        def clip_before(u, j):
+            first = ((u + 1) % 2 * J + j) * O
+            tiles = at(z, (u + 1) // 2)[:, first : first + O]
             nc.gpsimd.tensor_scalar(out=tiles, in0=tiles, scalar1=CLAMP, scalar2=-CLAMP / SLOPE, op0=ALU.min, op1=ALU.max)
 
         def close_groups(u, count):
@@ -436,6 +443,9 @@ def tile_modulatemlp_pa_kernel(tc, x, w_bytes, w_scale, weight, style_w, style_b
             for u, j in tiles[: len(tiles) - len(held)]:
                 finish(u, j)
 
+            if i == SINGLY_FROM + 3:
+                close_groups(i - 3, 1)
+
             if p < PAIRS:
                 for t in range(4 * p + 2, 4 * p + own_tiles(p)) if even else range(4 * p, 4 * p + 2):
                     turn_x(t)
@@ -468,6 +478,8 @@ def tile_modulatemlp_pa_kernel(tc, x, w_bytes, w_scale, weight, style_w, style_b
                 quantise(p)
             if even and 0 <= i - 4 < SINGLY_FROM:
                 close_groups(i - 4, 2)
+            if i == SINGLY_FROM + 4:
+                close_groups(i - 3, 1)
             if even and p + 1 in raw_pairs:
                 modulate_raw(p + 1)
             if i == 0 and summed(0):
@@ -485,6 +497,11 @@ def tile_modulatemlp_pa_kernel(tc, x, w_bytes, w_scale, weight, style_w, style_b
             for u in turned_in(i):
                 for j in range(J if summed(u) else 0):
                     add_steep(u, j)
+            if i == PLAIN_FROM:
+                free_banks[:0] = x_banks
+                for step in (turn_back, add_steep):
+                    for j in range(J):
+                        step(i - 1, j)
             if i < LAST:
                 product(2 * i + 2)
                 product(2 * i + 3)
@@ -499,30 +516,30 @@ def tile_modulatemlp_pa_kernel(tc, x, w_bytes, w_scale, weight, style_w, style_b
                 step(g, j)
 
         u = LAST - 1
-        clip_before(u - 1)
-        close_groups(u - 4, 1)
-        each_tile(turn_back, u - 2)
-        each_tile(add_steep, u - 2)
+        spare = [free_banks.pop(0) for h in range(2)]
         for h in range(2):
-            product(2 * LAST + h, bank=x_banks[h])
+            product(2 * LAST + h, bank=spare[h])
+        each_tile(take_relu, u - 2)
+        clip_before(u - 1, 0)
+        close_groups(u - 4, 1)
         each_tile(finish, u - 3)
         close_groups(u - 3, 1)
         each_tile(turn_back, u - 1)
-        free_banks[:0] = y_banks + x_banks
-        demodulate(nc.scalar, 2 * u, by_tile)
-        demodulate(nc.vector, 2 * u + 1, by_tile[:TAIL_MID])
-        each_tile(take_relu, u - 2)
-        demodulate(nc.scalar, 2 * u + 1, by_tile[TAIL_MID:])
         each_tile(finish, u - 2)
         close_groups(u - 2, 1)
-        each_tile(turn_back, u)
-        demodulate(nc.scalar, 2 * LAST, by_tile, x_banks[0])
-        demodulate(nc.vector, 2 * LAST + 1, by_tile[:TAIL_LAST], x_banks[1])
+        demodulate(nc.scalar, 2 * u, by_tile)
+        demodulate(nc.vector, 2 * u + 1, by_tile[:TAIL_MID])
         each_tile(take_relu, u - 1)
-        demodulate(nc.scalar, 2 * LAST + 1, by_tile[TAIL_LAST:], x_banks[1])
-        each_tile(turn_back, LAST)
+        demodulate(nc.scalar, 2 * u + 1, by_tile[TAIL_MID:])
+        each_tile(turn_back, u)
         each_tile(finish, u - 1)
-        each_tile(store, u - 1)
+        store(u - 1, 0)
+        clip_rows(nc.gpsimd, u - 1, 1)
+        store(u - 1, 1)
+        demodulate(nc.vector, 2 * LAST + 1, by_tile[:TAIL_LAST], spare[1])
+        demodulate(nc.scalar, 2 * LAST, by_tile, spare[0])
+        demodulate(nc.scalar, 2 * LAST + 1, by_tile[TAIL_LAST:], spare[1])
+        each_tile(turn_back, LAST)
         each_tile(take_relu, u)
         for j in range(J):
             finish(u, j)

@@ -439,9 +439,12 @@ def tile_modulatemlp_pa_kernel(tc, x, w_bytes, w_scale, weight, style_w, style_b
             if i <= LAST:
                 demodulate(nc.vector, 2 * i + 1, on_vector(i))
             tiles = [(u, j) for u in turned_in(i - 1) for j in range(J)]
-            held = tiles[-1:] if even and p < PAIRS else []
+            held = tiles[-1:] if even and p < PAIRS - 1 else []
             for u, j in tiles[: len(tiles) - len(held)]:
                 finish(u, j)
+                if i == PLAIN_FROM and j == 0:
+                    quantise_raw(PAIRS - 1)
+                    quantise(PAIRS - 1)
 
             if i == SINGLY_FROM + 3:
                 close_groups(i - 3, 1)
@@ -472,10 +475,11 @@ def tile_modulatemlp_pa_kernel(tc, x, w_bytes, w_scale, weight, style_w, style_b
                     finish(u, j)
                 if i == 0:
                     square_style(1)
-                quantise_raw(p)
-                if i == 0:
-                    quantise_style2(1)
-                quantise(p)
+                if p < PAIRS - 1:
+                    quantise_raw(p)
+                    if i == 0:
+                        quantise_style2(1)
+                    quantise(p)
             if even and 0 <= i - 4 < SINGLY_FROM:
                 close_groups(i - 4, 2)
             if i == SINGLY_FROM + 4:

@@ -41,6 +41,7 @@ EARLY_FIRST = 4
 SUMMED_FROM = 0
 TAIL_MID = 6
 FINISHED = 9
+HOLD = 256
 
 
 def tile_modulatemlp_pa_kernel(tc, x, w_bytes, w_scale, weight, style_w, style_b, bias, out):
@@ -119,6 +120,8 @@ def tile_modulatemlp_pa_kernel(tc, x, w_bytes, w_scale, weight, style_w, style_b
         for p in range(3, PAIRS):
             load_pair(p)
 
+        warm = keep.tile([P, BANK], F32)
+        nc.vector.memset(warm[:], 1.0)
         ident = keep.tile([P, P], F32)
         make_identity(nc, ident[:])
         ones = keep.tile([P, 1], F32)
@@ -129,6 +132,10 @@ def tile_modulatemlp_pa_kernel(tc, x, w_bytes, w_scale, weight, style_w, style_b
         nc.vector.memset(bias_rows[:], 0.0)
         steep_ident = keep.tile([P, P], F32)
         nc.vector.tensor_scalar(out=steep_ident[:], in0=ident[:], scalar1=-(1.0 - SLOPE), scalar2=None, op0=ALU.mult)
+
+
+        def warm_up(bank, columns):
+            nc.tensor.matmul(out=bank[:, :columns], lhsT=warm[:, :P], rhs=warm[:, :columns], start=True, stop=True)
 
         style_w_q = keep.tile([P, C], U32, align_bytes=64)
         style_w_s = keep.tile([P, C], U8, align_bytes=64)
@@ -364,11 +371,13 @@ def tile_modulatemlp_pa_kernel(tc, x, w_bytes, w_scale, weight, style_w, style_b
         nc.vector.tensor_copy(out=w_bf[:], in_=w_codes[:].bitcast(FP8))
         w_bank = z_banks[3]
         w_words = w_bf[:].bitcast(F32)
+        warm_up(x_banks[1], BANK)
         turn_rows(z_banks[0], weight_sb[0])
         for u in range(2):
             nc.tensor.transpose(w_bank[:, u * P : (u + 1) * P], w_words[:, u::2], ident[:])
-        for h in range(2):
-            turn_rows(y_banks[h], style_w_sb[h])
+        turn_rows(y_banks[0], style_w_sb[0])
+        turn_rows(y_banks[1], style_w_sb[1])
+        warm_up(x_banks[1], HOLD)
         nc.vector.tensor_tensor(
             out=w_t[:].rearrange("p n (u e) -> p n u e", e=2),
             in0=w_bank[:, : 2 * P].bitcast(BF16).rearrange("p (u n e) -> p n u e", u=2, e=2),
@@ -390,7 +399,9 @@ def tile_modulatemlp_pa_kernel(tc, x, w_bytes, w_scale, weight, style_w, style_b
             cols = slice(t * P, (t + 1) * P)
             nc.tensor.matmul_mx(out=style_bank[:, cols], lhsT=style_w_q[:, cols].bitcast(X4), lhsT_scale=style_w_s[:, cols],
                                 rhs=w_q[:].bitcast(X4), rhs_scale=w_s[:], start=True, stop=True)
-        for t in range(1, 2 * J):
+        turn_x(1)
+        warm_up(y_banks[0], HOLD)
+        for t in range(2, 2 * J):
             turn_x(t)
         copy_words(nc.scalar.copy, weight_t[1][:], z_banks[1])
         nc.scalar.activation(out=weight2_t[1][:], in_=weight_t[1][:], func=ACT.Square)
@@ -404,6 +415,7 @@ def tile_modulatemlp_pa_kernel(tc, x, w_bytes, w_scale, weight, style_w, style_b
         quantise_style2(0)
         quantise(0, slice(0, P))
         turn_early(1, [0])
+        warm_up(y_banks[0], HOLD)
         d_product(0, y_banks[0], range(0, 2))
         product(0, slice(0, P), y_banks[1])
         turn_early(1, [1])

@@ -36,18 +36,20 @@ PLAIN_FROM = GROUPS - 3
 ON_VECTOR = (1, 3)
 RAMP = {0: 0, 1: 0, 2: 4, 29: 0}
 SINGLY_FROM = 24
-TAIL_LAST = 8
+TAIL_LAST = 6
 EARLY_FIRST = 4
 SUMMED_FROM = 0
 TAIL_MID = 6
 FINISHED = 9
 HOLD = 256
+WIDE = range(20, GROUPS - 3)
 
 
 def tile_modulatemlp_pa_kernel(tc, x, w_bytes, w_scale, weight, style_w, style_b, bias, out):
     nc = tc.nc
     x_view = x.rearrange("n l c -> (n l) c").rearrange("(t r) c -> r t c", r=P)
     out_view = out.rearrange("n l o -> (n l) o").rearrange("(t r) o -> r t o", r=P)
+    wide_view = out.rearrange("n l o -> (n l) o").rearrange("(g r j) o -> r g (j o)", r=P, j=J)
     raw_pairs = list(RAW_PAIRS)
     early_pairs = raw_pairs[: 2 * EARLY_BANKS]
 
@@ -286,6 +288,10 @@ def tile_modulatemlp_pa_kernel(tc, x, w_bytes, w_scale, weight, style_w, style_b
                 first = e * TOKENS + n * POINTS
                 dst = z_block(u, j, k)[:, r : r + POINTS]
                 src = bank[:, first : first + POINTS]
+                if u in WIDE:
+                    both = at(z, (u + 1) // 2)[:].rearrange("p (g j k r) -> p g k j r", g=2, j=J, k=PACK)
+                    dst = both[:, (u + 1) % 2, k, :, n * POINTS // J : (n + 1) * POINTS // J]
+                    src = src.rearrange("p (r j) -> p j r", j=J)
                 factor = decoef[half][:, k, sample : sample + 1]
                 if engine is nc.scalar:
                     nc.scalar.activation(out=dst, in_=src, func=ACT.Identity, scale=factor, bias=bias_gain[:, k : k + 1])
@@ -352,7 +358,10 @@ def tile_modulatemlp_pa_kernel(tc, x, w_bytes, w_scale, weight, style_w, style_b
             tiles = at(finished, u // 2)[:].rearrange("p (t o) -> p t o", o=O)[:, first : first + J * count]
             plain = tiles[:, :, P if summed(u) else 0 :]
             nc.gpsimd.tensor_scalar(out=plain, in0=plain, scalar1=CLAMP, scalar2=-CLAMP, op0=ALU.min, op1=ALU.max)
-            nc.sync.dma_start(out=out_view[:, J * u : J * (u + count), :], in_=tiles)
+            if u in WIDE:
+                nc.sync.dma_start(out=wide_view[:, u : u + count, :], in_=tiles.rearrange("p (g j) o -> p g (j o)", j=J))
+            else:
+                nc.sync.dma_start(out=out_view[:, J * u : J * (u + count), :], in_=tiles)
 
         by_block = [(e, n) for e in range(2) for n in range(GROUP_SAMPLES)]
         by_tile = [(e, n) for n in range(GROUP_SAMPLES) for e in range(2)]
@@ -531,38 +540,69 @@ def tile_modulatemlp_pa_kernel(tc, x, w_bytes, w_scale, weight, style_w, style_b
             for j in range(J):
                 step(g, j)
 
+        def open_bank(u, j):
+            for k in range(PACK):
+                nc.tensor.matmul(out=z_bank(u, j)[:, k * P : (k + 1) * P], lhsT=z_block(u, j, k), rhs=ident[:],
+                                 is_transpose=True, start=k == 0, stop=False)
+
+        def add_term(u, j, by_turns):
+            for k in range(PACK):
+                cols = slice(k * P, (k + 1) * P)
+                nc.tensor.matmul(out=z_bank(u, j)[:, cols], lhsT=relu_tile(u, j)[:, cols], rhs=ident[:] if by_turns else steep_ident[:],
+                                 is_transpose=by_turns, start=False, stop=k == PACK - 1)
+
+        def z_tile(u, j):
+            first = ((u + 1) % 2 * J + j) * O
+            return at(z, (u + 1) // 2)[:, first : first + O]
+
+        def negative_tile(u, j):
+            nc.gpsimd.tensor_scalar(out=relu_tile(u, j)[:], in0=z_tile(u, j), scalar1=0.0, scalar2=-CLAMP / SLOPE, op0=ALU.min, op1=ALU.max)
+
+        def steep_tile(u, j):
+            nc.vector.tensor_scalar(out=relu_tile(u, j)[:], in0=z_tile(u, j), scalar1=-(1.0 - SLOPE), scalar2=0.0, op0=ALU.mult, op1=ALU.max)
+
+        def empty(u, j):
+            nc.vector.tensor_scalar(out=rows(u, j), in0=z_bank(u, j)[:], scalar1=CLAMP, scalar2=-CLAMP, op0=ALU.min, op1=ALU.max)
+            free_banks.append(z_bank(u, j))
+            store(u, j)
+
         u = LAST - 1
         spare = [free_banks.pop(0) for h in range(2)]
         for h in range(2):
             product(2 * LAST + h, bank=spare[h])
         each_tile(take_relu, u - 2)
-        clip_before(u - 1, 0)
+        negative_tile(u - 1, 0)
         close_groups(u - 4, 1)
         each_tile(finish, u - 3)
         close_groups(u - 3, 1)
-        each_tile(turn_back, u - 1)
+        turn_back(u - 1, 1)
+        open_bank(u - 1, 0)
+        add_term(u - 1, 0, False)
         each_tile(finish, u - 2)
         close_groups(u - 2, 1)
         demodulate(nc.scalar, 2 * u, by_tile)
-        demodulate(nc.vector, 2 * u + 1, by_tile[:TAIL_MID])
-        each_tile(take_relu, u - 1)
-        demodulate(nc.scalar, 2 * u + 1, by_tile[TAIL_MID:])
-        each_tile(turn_back, u)
-        each_tile(finish, u - 1)
-        store(u - 1, 0)
-        clip_rows(nc.gpsimd, u - 1, 1)
-        store(u - 1, 1)
         demodulate(nc.vector, 2 * LAST + 1, by_tile[:TAIL_LAST], spare[1])
+        take_relu(u - 1, 1)
+        demodulate(nc.scalar, 2 * u + 1, by_tile)
+        each_tile(turn_back, u)
+        finish(u - 1, 1)
+        clip_rows(nc.gpsimd, u - 1, 1)
+        empty(u - 1, 0)
+        store(u - 1, 1)
         demodulate(nc.scalar, 2 * LAST, by_tile, spare[0])
         demodulate(nc.scalar, 2 * LAST + 1, by_tile[TAIL_LAST:], spare[1])
-        each_tile(turn_back, LAST)
+        steep_tile(LAST, 0)
         each_tile(take_relu, u)
-        for j in range(J):
-            finish(u, j)
-            clip_rows(nc.gpsimd, u, j)
-            store(u, j)
-        each_tile(take_relu, LAST)
-        each_tile(finish, LAST)
-        for j in range(J):
-            clip_rows(nc.vector, LAST, j)
-            store(LAST, j)
+        open_bank(LAST, 0)
+        add_term(LAST, 0, True)
+        steep_tile(LAST, 1)
+        open_bank(LAST, 1)
+        add_term(LAST, 1, True)
+        finish(u, 0)
+        clip_rows(nc.gpsimd, u, 0)
+        empty(LAST, 0)
+        store(u, 0)
+        finish(u, 1)
+        clip_rows(nc.gpsimd, u, 1)
+        empty(LAST, 1)
+        store(u, 1)

@@ -459,7 +459,7 @@ def tile_modulatemlp_pa_kernel(tc, x, w_bytes, w_scale, weight, style_w, style_b
             even = i % 2 == 0
             if i <= LAST:
                 demodulate(nc.vector, 2 * i + 1, on_vector(i))
-            tiles = [(u, j) for u in turned_in(i - 1) for j in range(J)]
+            tiles = [(u, j) for u in turned_in(i - 1) for j in (range(J) if i in (3, PLAIN_FROM) else reversed(range(J)))]
             held = tiles[-1:] if even and p < PAIRS - 1 else []
             for u, j in tiles[: len(tiles) - len(held)]:
                 finish(u, j)

@@ -33,7 +33,7 @@ LAST = GROUPS - 1
 RAW_PAIRS = range(1, PAIRS - 1)
 EARLY_BANKS = 3
 PLAIN_FROM = GROUPS - 3
-ON_VECTOR = (1, 3)
+ON_VECTOR = (1, 2)
 RAMP = {0: 0, 1: 0, 2: 4, 29: 0}
 SINGLY_FROM = 24
 TAIL_LAST = 6
@@ -331,12 +331,12 @@ def tile_modulatemlp_pa_kernel(tc, x, w_bytes, w_scale, weight, style_w, style_b
 
         def take_relu(u, j):
             first = P if summed(u) else 0
-            nc.scalar.activation(out=relu_tile(u, j)[:, first:], in_=z_bank(u, j)[:, first:], func=ACT.Relu, scale=-(1.0 - SLOPE))
+            nc.scalar.activation(out=relu_tile(u, j)[:, first:], in_=z_bank(u, j)[:, first:], func=ACT.Copy, scale=SLOPE)
 
         def finish(u, j):
             first = P if summed(u) else 0
             bank = z_bank(u, j)
-            nc.vector.tensor_tensor(out=rows(u, j)[:, first:], in0=bank[:, first:], in1=relu_tile(u, j)[:, first:], op=ALU.add)
+            nc.vector.tensor_tensor(out=rows(u, j)[:, first:], in0=bank[:, first:], in1=relu_tile(u, j)[:, first:], op=ALU.max)
             if first:
                 nc.vector.tensor_scalar(out=rows(u, j)[:, :first], in0=bank[:, :first],
                                         scalar1=CLAMP, scalar2=-CLAMP, op0=ALU.min, op1=ALU.max)

@@ -300,8 +300,8 @@ def tile_modulatemlp_pa_kernel(tc, x, w_bytes, w_scale, weight, style_w, style_b
                                             op0=ALU.mult, op1=ALU.add)
 
         def take_negative(n, first=0):
-            nc.gpsimd.tensor_scalar(out=at(negative, n)[:].rearrange("p (t r) -> p t r", r=P)[:, first:],
-                                    in0=at(z, n)[:].rearrange("p (t c) -> p t c", c=O)[:, first:, :P], scalar1=0.0,
+            nc.gpsimd.tensor_scalar(out=at(negative, n)[:].rearrange("p (g r) -> p g r", g=2)[:, first:],
+                                    in0=at(z, n)[:].rearrange("p (g c) -> p g c", g=2)[:, first:, : 2 * P], scalar1=0.0,
                                     scalar2=-CLAMP / SLOPE, op0=ALU.min, op1=ALU.max)
 
         free_banks = [z_banks[2], z_banks[0], z_banks[1], z_banks[3]]
@@ -313,14 +313,15 @@ def tile_modulatemlp_pa_kernel(tc, x, w_bytes, w_scale, weight, style_w, style_b
             return taken[(u, j)]
 
         def turn_back(u, j):
-            for k in (1, 2, 3, 0):
+            opens = summed(u) and j == 0
+            for k in (2, 3, 0, 1):
                 nc.tensor.matmul(out=z_bank(u, j)[:, k * P : (k + 1) * P], lhsT=z_block(u, j, k), rhs=ident[:],
-                                 is_transpose=True, start=True, stop=k > 0 or not summed(u))
+                                 is_transpose=True, start=not (opens and k == 1), stop=not (opens and k < 2))
 
-        def add_steep(u, j):
-            first = ((u + 1) % 2 * J + j) * P
-            nc.tensor.matmul(out=z_bank(u, j)[:, :P], lhsT=at(negative, (u + 1) // 2)[:, first : first + P],
-                             rhs=steep_ident[:], start=False, stop=True)
+        def add_steep(u, k):
+            first = ((u + 1) % 2 * 2 + k) * P
+            nc.tensor.matmul(out=z_bank(u, 0)[:, k * P : (k + 1) * P], lhsT=at(negative, (u + 1) // 2)[:, first : first + P],
+                             rhs=steep_ident[:], start=False, stop=k == 1)
 
         def rows(u, j):
             place = u % 2 * J + j
@@ -330,11 +331,11 @@ def tile_modulatemlp_pa_kernel(tc, x, w_bytes, w_scale, weight, style_w, style_b
             return at(relu, J * u + j)
 
         def take_relu(u, j):
-            first = P if summed(u) else 0
+            first = 2 * P if summed(u) and j == 0 else 0
             nc.scalar.activation(out=relu_tile(u, j)[:, first:], in_=z_bank(u, j)[:, first:], func=ACT.Copy, scale=SLOPE)
 
         def finish(u, j):
-            first = P if summed(u) else 0
+            first = 2 * P if summed(u) and j == 0 else 0
             bank = z_bank(u, j)
             nc.vector.tensor_tensor(out=rows(u, j)[:, first:], in0=bank[:, first:], in1=relu_tile(u, j)[:, first:], op=ALU.max)
             if first:
@@ -356,7 +357,7 @@ def tile_modulatemlp_pa_kernel(tc, x, w_bytes, w_scale, weight, style_w, style_b
         def close_groups(u, count):
             first = u % 2 * J
             tiles = at(finished, u // 2)[:].rearrange("p (t o) -> p t o", o=O)[:, first : first + J * count]
-            plain = tiles[:, :, P if summed(u) else 0 :]
+            plain = tiles.rearrange("p (g j) o -> p g (j o)", j=J)[:, :, 2 * P if summed(u) else 0 :]
             nc.gpsimd.tensor_scalar(out=plain, in0=plain, scalar1=CLAMP, scalar2=-CLAMP, op0=ALU.min, op1=ALU.max)
             if u in WIDE:
                 nc.sync.dma_start(out=wide_view[:, u : u + count, :], in_=tiles.rearrange("p (g j) o -> p g (j o)", j=J))
@@ -459,7 +460,7 @@ def tile_modulatemlp_pa_kernel(tc, x, w_bytes, w_scale, weight, style_w, style_b
             even = i % 2 == 0
             if i <= LAST:
                 demodulate(nc.vector, 2 * i + 1, on_vector(i))
-            tiles = [(u, j) for u in turned_in(i - 1) for j in (range(J) if i in (3, PLAIN_FROM) else reversed(range(J)))]
+            tiles = [(u, j) for u in turned_in(i - 1) for j in (reversed(range(J)) if i == 3 else range(J))]
             held = tiles[-1:] if even and p < PAIRS - 1 else []
             for u, j in tiles[: len(tiles) - len(held)]:
                 finish(u, j)
@@ -482,7 +483,8 @@ def tile_modulatemlp_pa_kernel(tc, x, w_bytes, w_scale, weight, style_w, style_b
                     turn_back(u, j)
 
             parts = [] if i > LAST else on_scalar(i)[2 * PACK :] if i == 0 else on_scalar(i)
-            for q, part in parts[:PACK]:
+            split = 2 * PACK if even else PACK
+            for q, part in parts[:split]:
                 demodulate(nc.scalar, q, [part])
             if even and i and summed(i):
                 take_negative(i // 2)
@@ -508,11 +510,11 @@ def tile_modulatemlp_pa_kernel(tc, x, w_bytes, w_scale, weight, style_w, style_b
             if even and p + 1 in raw_pairs:
                 modulate_raw(p + 1)
             if i == 0 and summed(0):
-                take_negative(0, J)
+                take_negative(0, 1)
 
             if copies_in(i):
                 copy_raw(p + 1, x_banks[1], 1)
-            for q, part in parts[PACK:]:
+            for q, part in parts[split:]:
                 demodulate(nc.scalar, q, [part])
             if i == 1:
                 copy_early(2)
@@ -533,11 +535,15 @@ def tile_modulatemlp_pa_kernel(tc, x, w_bytes, w_scale, weight, style_w, style_b
             if i == 1:
                 d_product(1, z_banks[3], range(PACK))
             for u in turned_in(i):
-                for j in range(J):
+                for j in reversed(range(J)):
                     take_relu(u, j)
 
         def each_tile(step, g):
             for j in range(J):
+                step(g, j)
+
+        def plain_first(step, g):
+            for j in reversed(range(J)):
                 step(g, j)
 
         def open_bank(u, j):
@@ -570,15 +576,15 @@ def tile_modulatemlp_pa_kernel(tc, x, w_bytes, w_scale, weight, style_w, style_b
         spare = [free_banks.pop(0) for h in range(2)]
         for h in range(2):
             product(2 * LAST + h, bank=spare[h])
-        each_tile(take_relu, u - 2)
+        plain_first(take_relu, u - 2)
         negative_tile(u - 1, 0)
         close_groups(u - 4, 1)
-        each_tile(finish, u - 3)
+        plain_first(finish, u - 3)
         close_groups(u - 3, 1)
         turn_back(u - 1, 1)
         open_bank(u - 1, 0)
         add_term(u - 1, 0, False)
-        each_tile(finish, u - 2)
+        plain_first(finish, u - 2)
         close_groups(u - 2, 1)
         demodulate(nc.scalar, 2 * u, by_tile)
         demodulate(nc.vector, 2 * LAST + 1, by_tile[:TAIL_LAST], spare[1])

import math
from contextlib import ExitStack

import concourse.mybir as mybir
from concourse.masks import make_identity

SAMPLES, POINTS, LATENT, C, O = 128, 64, 512, 512, 512
EPS = 1e-8
CLAMP = 256.0
SLOPE = 0.2
GAIN = math.sqrt(2.0)
FLOPS = 2 * SAMPLES * POINTS * C * O + 2 * SAMPLES * LATENT * C + 2 * SAMPLES * C * O

F32 = mybir.dt.float32
BF16 = mybir.dt.bfloat16
U32 = mybir.dt.uint32
U8 = mybir.dt.uint8
FP8 = mybir.dt.float8_e4m3fn
X4 = mybir.dt.float8_e4m3fn_x4
ALU = mybir.AluOpType
ACT = mybir.ActivationFunctionType

P = 128
BANK = 512
PACK = 4
GROUP_SAMPLES = 4
TOKENS = GROUP_SAMPLES * POINTS
J = TOKENS // P
GROUPS = SAMPLES // GROUP_SAMPLES
PAIRS = GROUPS // 2
HALF = SAMPLES // 2
LAST = GROUPS - 1
RAW_PAIRS = range(1, PAIRS - 1)
EARLY_BANKS = 3
PLAIN_FROM = GROUPS - 3
ON_VECTOR = (1, 2)
RAMP = {0: 0, 1: 0, 2: 4, 29: 0}
SINGLY_FROM = 24
TAIL_LAST = 6
EARLY_FIRST = 4
SUMMED_FROM = 0
TAIL_MID = 6
FINISHED = 9
HOLD = 256
WIDE = range(20, GROUPS - 3)


def tile_modulatemlp_pa_kernel(tc, x, w_bytes, w_scale, weight, style_w, style_b, bias, out):
    nc = tc.nc
    x_view = x.rearrange("n l c -> (n l) c").rearrange("(t r) c -> r t c", r=P)
    out_view = out.rearrange("n l o -> (n l) o").rearrange("(t r) o -> r t o", r=P)
    wide_view = out.rearrange("n l o -> (n l) o").rearrange("(g r j) o -> r g (j o)", r=P, j=J)
    raw_pairs = list(RAW_PAIRS)
    early_pairs = raw_pairs[: 2 * EARLY_BANKS]

    with ExitStack() as ctx:
        ctx.enter_context(tc.manual_schedule())
        keep = ctx.enter_context(tc.tile_pool(name="keep", bufs=1))
        psum = ctx.enter_context(tc.psum_pool(name="psum", bufs=1))

        def ring(name, count, shape, dtype):
            return [keep.tile(shape, dtype, name="%s%d" % (name, r), align_bytes=64) for r in range(count)]

        def at(tiles, index):
            return tiles[index % len(tiles)]

        x_banks = [psum.tile([P, BANK], F32, name="x_bank%d" % r) for r in range(2)]
        y_banks = [psum.tile([P, BANK], F32, name="y_bank%d" % r) for r in range(2)]
        z_banks = [psum.tile([P, BANK], F32, name="z_bank%d" % r) for r in range(4)]

        style_w_sb = ring("style_w_sb", 2, [P, 2, LATENT], BF16)
        weight_sb = ring("weight_sb", 2, [P, 2, C], BF16)
        w_codes = keep.tile([P, LATENT], U8)
        w_scale_sb = keep.tile([P, PACK], F32)
        style_b_sb = keep.tile([P, PACK], BF16)
        bias_sb = keep.tile([PACK, P], BF16)
        style_w_view = style_w.rearrange("(m h e) l -> h m e l", h=2, e=2)
        weight_view = weight.rearrange("(h e m) c -> h m e c", h=2, e=2)
        nc.sync.dma_start(out=weight_sb[0][:, 0], in_=weight_view[0][:, 0])
        nc.sync.dma_start(out=w_codes[:], in_=w_bytes)
        nc.sync.dma_start(out=weight_sb[0][:, 1], in_=weight_view[0][:, 1])
        for h in range(2):
            nc.sync.dma_start(out=style_w_sb[h][:], in_=style_w_view[h])
        nc.scalar.dma_start(out=w_scale_sb[:], in_=w_scale.rearrange("o (p t) -> p (o t)", t=PACK))
        nc.scalar.dma_start(out=style_b_sb[:], in_=style_b.rearrange("(p t) -> p t", t=PACK))
        nc.scalar.dma_start(out=bias_sb[:], in_=bias.rearrange("(k m) -> k m", k=PACK))
        nc.sync.dma_start(out=weight_sb[1][:], in_=weight_view[1])

        x_first = ring("x_first", 2, [P, J, C], BF16)
        x_pairs = [None] + ring("x_pair", PAIRS - 1, [P, 2 * J, C], BF16)
        x_early = ring("x_early", len(early_pairs), [P, C], BF16)
        raw = ring("raw", max(2, len(early_pairs)), [P, P * PACK], BF16)

        def own_tiles(p):
            return 3 if p in raw_pairs else 4

        def x_rows(t):
            p, j = divmod(t, 2 * J)
            if p == 0:
                return x_first[j // J][:, j % J, :]
            if p in early_pairs and j == 3:
                return x_early[early_pairs.index(p)][:]
            return x_pairs[p][:, j, :]

        def load_pair(p):
            n = 3 if p in early_pairs else 4
            nc.sync.dma_start(out=x_pairs[p][:, :n, :], in_=x_view[:, 4 * p : 4 * p + n, :])

        def load_early(n):
            nc.sync.dma_start(out=x_early[n][:], in_=x_view[:, 4 * early_pairs[n] + 3, :])

        for u in range(2):
            nc.sync.dma_start(out=x_first[u][:], in_=x_view[:, u * J : (u + 1) * J, :])
        for n in range(EARLY_FIRST):
            load_early(n)
        load_pair(1)
        for n in range(EARLY_FIRST, 4):
            load_early(n)
        load_pair(2)
        for n in range(4, len(early_pairs)):
            load_early(n)
        for p in range(3, PAIRS):
            load_pair(p)

        warm = keep.tile([P, BANK], F32)
        nc.vector.memset(warm[:], 1.0)
        ident = keep.tile([P, P], F32)
        make_identity(nc, ident[:])
        ones = keep.tile([P, 1], F32)
        nc.vector.memset(ones[:], 1.0)
        half_eps = keep.tile([P, 1], F32)
        nc.scalar.activation(out=half_eps[:], in_=ones[:], func=ACT.Abs_reciprocal_sqrt, scale=(0.5 * EPS) ** -2)
        bias_rows = keep.tile([P, P], F32)
        nc.vector.memset(bias_rows[:], 0.0)
        steep_ident = keep.tile([P, P], F32)
        nc.vector.tensor_scalar(out=steep_ident[:], in0=ident[:], scalar1=-(1.0 - SLOPE), scalar2=None, op0=ALU.mult)


        def warm_up(bank, columns):
            nc.tensor.matmul(out=bank[:, :columns], lhsT=warm[:, :P], rhs=warm[:, :columns], start=True, stop=True)

        style_w_q = keep.tile([P, C], U32, align_bytes=64)
        style_w_s = keep.tile([P, C], U8, align_bytes=64)
        w_q = keep.tile([P, SAMPLES], U32, align_bytes=64)
        w_s = keep.tile([P, SAMPLES], U8, align_bytes=64)
        weight_q = keep.tile([P, O], U32, align_bytes=64)
        weight_s = keep.tile([P, O], U8, align_bytes=64)
        weight2_q = keep.tile([P, O], U32, align_bytes=64)
        weight2_s = keep.tile([P, O], U8, align_bytes=64)
        style2_q = keep.tile([P, SAMPLES], U32, align_bytes=64)
        style2_s = keep.tile([P, SAMPLES], U8, align_bytes=64)
        style_w_t = ring("style_w_t", 2, [P, 2 * P * PACK], BF16)
        weight_t = ring("weight_t", 2, [P, 2 * P * PACK], BF16)
        weight2_t = ring("weight2_t", 2, [P, 2 * P * PACK], BF16)
        w_t = keep.tile([P, SAMPLES, PACK], BF16, align_bytes=64)
        style2_t = ring("style2_t", 2, [P, HALF * PACK], BF16)
        w_bf = keep.tile([P, LATENT], BF16)
        style = ring("style", 2, [P, HALF, PACK], F32)
        decoef = ring("decoef", 2, [P, PACK, HALF], F32)
        bias_gain = keep.tile([P, PACK], F32)

        modulated = ring("modulated", 2, [P, 3 * P * PACK], BF16)
        modulated_raw = keep.tile([P, P * PACK], BF16, align_bytes=64)
        codes = ring("codes", 2, [P, 2 * TOKENS], U32)
        scales = ring("scales", 2, [P, 2 * TOKENS], U8)
        z = ring("z", 2, [P, 2 * J * O], F32)
        negative = ring("negative", 2, [P, 2 * J * P], F32)
        relu = ring("relu", 6, [P, O], F32)
        finished = ring("finished", FINISHED, [P, 2 * J * O], F32)

        def turn_tile(bank, j, rows):
            parts = bank[:].rearrange("p (u j r) -> p u j r", u=2, j=2)
            words = rows.bitcast(F32)
            for u in range(2):
                nc.tensor.transpose(parts[:, u, j, :], words[:, u::2], ident[:])

        def turn_rows(bank, rows):
            for j in range(2):
                turn_tile(bank, j, rows[:, j, :])

        def side_by_side(bank):
            return bank[:].bitcast(BF16).rearrange("p (u r e) -> p r u e", u=2, e=2)

        def copy_words(engine_copy, dst, bank, rows=slice(0, 2 * P)):
            engine_copy(out=dst.bitcast(F32).rearrange("p (r u) -> p r u", u=2),
                           in_=bank[:].rearrange("p (u r) -> p r u", u=2)[:, rows])

        def quantise_half(q, s, h, source):
            cols = slice(2 * P * h, 2 * P * (h + 1))
            nc.vector.quantize_mx(out=q[:, cols].bitcast(X4), scales=s[:, cols], in_=source[:])

        style_bank = z_banks[2]

        def make_style(h):
            sums = style_bank[:].rearrange("p (t n) -> p n t", t=PACK)[:, h * HALF : (h + 1) * HALF, :]
            nc.vector.scalar_tensor_tensor(
                out=style[h][:], in0=sums, scalar=1.0 / math.sqrt(LATENT),
                in1=style_b_sb[:].unsqueeze(1).to_broadcast([P, HALF, PACK]), op0=ALU.mult, op1=ALU.add)

        def square_style(h):
            flat = style[h][:].rearrange("p n t -> p (n t)")
            nc.vector.tensor_tensor(out=style2_t[h][:], in0=flat, in1=flat, op=ALU.mult)

        def quantise_style2(h):
            ns = slice(h * HALF, (h + 1) * HALF)
            nc.vector.quantize_mx(out=style2_q[:, ns].bitcast(X4), scales=style2_s[:, ns], in_=style2_t[h][:])

        def d_product(half, bank, blocks):
            ns = slice(half * HALF, (half + 1) * HALF)
            for k in blocks:
                cols = slice(k * P, (k + 1) * P)
                nc.tensor.matmul_mx(out=bank[:, k * HALF : (k + 1) * HALF], lhsT=weight2_q[:, cols].bitcast(X4),
                                    lhsT_scale=weight2_s[:, cols], rhs=style2_q[:, ns].bitcast(X4),
                                    rhs_scale=style2_s[:, ns], start=True, stop=True)

        def take_root(half, bank, blocks):
            cols = slice(blocks.start * HALF, blocks.stop * HALF)
            nc.scalar.activation(out=decoef[half][:].rearrange("p k n -> p (k n)")[:, cols], in_=bank[:, cols],
                                 func=ACT.Abs_reciprocal_sqrt, scale=0.5, bias=half_eps[:])

        def turn_x(t):
            turn_tile(at(x_banks, t // J), t % J, x_rows(t))

        early_banks = [z_banks[3], z_banks[0], z_banks[1]]

        def turn_early(b, tiles=range(2)):
            for j in tiles:
                turn_tile(early_banks[b], j, x_early[2 * b + j][:])

        def raw_tile(p):
            return at(raw, raw_pairs.index(p))

        def copy_raw(p, bank, j):
            copy_words(nc.scalar.copy, raw_tile(p)[:], bank, slice(j * P, (j + 1) * P))

        def copy_early(b):
            for n in range(2 * b, min(2 * b + 2, len(early_pairs))):
                copy_raw(early_pairs[n], early_banks[b], n % 2)

        def modulate(u, first=0, count=GROUP_SAMPLES):
            half, sample = divmod(u * GROUP_SAMPLES + first, HALF)
            factors = style[half][:, sample : sample + count, :].rearrange("p n (u e) -> p n u e", e=2)
            place = u % 2 * GROUP_SAMPLES + first
            target, place = (at(modulated, u // 2), place) if place < 6 else (modulated_raw, place - 6)
            nc.vector.tensor_tensor(
                out=target[:].rearrange("p (n l u e) -> p n l u e", l=POINTS, u=2, e=2)[:, place : place + count],
                in0=side_by_side(at(x_banks, u)).rearrange("p (n l) u e -> p n l u e", n=GROUP_SAMPLES)[:, first : first + count],
                in1=factors.unsqueeze(2).to_broadcast([P, count, POINTS, 2, 2]), op=ALU.mult)

        def modulate_raw(p):
            half, sample = divmod((2 * p + 1) * GROUP_SAMPLES + 2, HALF)
            nc.gpsimd.tensor_tensor(
                out=modulated_raw[:].rearrange("p (n l t) -> p n l t", n=2, t=PACK),
                in0=raw_tile(p)[:].rearrange("p (n l t) -> p n l t", n=2, t=PACK),
                in1=style[half][:, sample : sample + 2, :].unsqueeze(2).to_broadcast([P, 2, POINTS, PACK]), op=ALU.mult)

        def quantise(p, tokens=slice(0, 3 * P)):
            nc.vector.quantize_mx(out=at(codes, p)[:, tokens].bitcast(X4), scales=at(scales, p)[:, tokens],
                                  in_=at(modulated, p)[:, tokens.start * PACK : tokens.stop * PACK])

        def quantise_raw(p):
            nc.vector.quantize_mx(out=at(codes, p)[:, 3 * P :].bitcast(X4), scales=at(scales, p)[:, 3 * P :], in_=modulated_raw[:])

        def product(q, tokens=slice(0, TOKENS), bank=None):
            u, h = divmod(q, 2)
            bank = at(y_banks, q) if bank is None else bank
            moving = slice(u % 2 * TOKENS + tokens.start, u % 2 * TOKENS + tokens.stop)
            for e in range(2):
                cols = slice((2 * h + e) * P, (2 * h + e + 1) * P)
                nc.tensor.matmul_mx(out=bank[:, e * TOKENS : (e + 1) * TOKENS][:, tokens], lhsT=weight_q[:, cols].bitcast(X4),
                                    lhsT_scale=weight_s[:, cols], rhs=at(codes, u // 2)[:, moving].bitcast(X4),
                                    rhs_scale=at(scales, u // 2)[:, moving], start=True, stop=True)

        def z_block(u, j, k):
            first = (((u + 1) % 2 * J + j) * PACK + k) * P
            return at(z, (u + 1) // 2)[:, first : first + P]

        def summed(u):
            return SUMMED_FROM <= u < PLAIN_FROM

        def demodulate(engine, q, parts, bank=None):
            u, h = divmod(q, 2)
            bank = at(y_banks, q) if bank is None else bank
            for e, n in parts:
                k = 2 * h + e
                half, sample = divmod(u * GROUP_SAMPLES + n, HALF)
                j, r = divmod(n * POINTS, P)
                first = e * TOKENS + n * POINTS
                dst = z_block(u, j, k)[:, r : r + POINTS]
                src = bank[:, first : first + POINTS]
                if u in WIDE:
                    both = at(z, (u + 1) // 2)[:].rearrange("p (g j k r) -> p g k j r", g=2, j=J, k=PACK)
                    dst = both[:, (u + 1) % 2, k, :, n * POINTS // J : (n + 1) * POINTS // J]
                    src = src.rearrange("p (r j) -> p j r", j=J)
                factor = decoef[half][:, k, sample : sample + 1]
                if engine is nc.scalar:
                    nc.scalar.activation(out=dst, in_=src, func=ACT.Identity, scale=factor, bias=bias_gain[:, k : k + 1])
                else:
                    nc.vector.tensor_scalar(out=dst, in0=src, scalar1=factor, scalar2=bias_gain[:, k : k + 1],
                                            op0=ALU.mult, op1=ALU.add)

        def take_negative(n, first=0):
            nc.gpsimd.tensor_scalar(out=at(negative, n)[:].rearrange("p (g r) -> p g r", g=2)[:, first:],
                                    in0=at(z, n)[:].rearrange("p (g c) -> p g c", g=2)[:, first:, : 2 * P], scalar1=0.0,
                                    scalar2=-CLAMP / SLOPE, op0=ALU.min, op1=ALU.max)

        free_banks = [z_banks[2], z_banks[0], z_banks[1], z_banks[3]]
        taken = {}

        def z_bank(u, j):
            if (u, j) not in taken:
                taken[(u, j)] = free_banks.pop(0)
            return taken[(u, j)]

        def turn_back(u, j):
            opens = summed(u) and j == 0
            for k in (2, 3, 0, 1):
                nc.tensor.matmul(out=z_bank(u, j)[:, k * P : (k + 1) * P], lhsT=z_block(u, j, k), rhs=ident[:],
                                 is_transpose=True, start=not (opens and k == 1), stop=not (opens and k < 2))

        def add_steep(u, k):
            first = ((u + 1) % 2 * 2 + k) * P
            nc.tensor.matmul(out=z_bank(u, 0)[:, k * P : (k + 1) * P], lhsT=at(negative, (u + 1) // 2)[:, first : first + P],
                             rhs=steep_ident[:], start=False, stop=k == 1)

        def rows(u, j):
            place = u % 2 * J + j
            return at(finished, u // 2)[:, place * O : (place + 1) * O]

        def relu_tile(u, j):
            return at(relu, J * u + j)

        def take_relu(u, j):
            first = 2 * P if summed(u) and j == 0 else 0
            nc.scalar.activation(out=relu_tile(u, j)[:, first:], in_=z_bank(u, j)[:, first:], func=ACT.Copy, scale=SLOPE)

        def finish(u, j):
            first = 2 * P if summed(u) and j == 0 else 0
            bank = z_bank(u, j)
            nc.vector.tensor_tensor(out=rows(u, j)[:, first:], in0=bank[:, first:], in1=relu_tile(u, j)[:, first:], op=ALU.max)
            if first:
                nc.vector.tensor_scalar(out=rows(u, j)[:, :first], in0=bank[:, :first],
                                        scalar1=CLAMP, scalar2=-CLAMP, op0=ALU.min, op1=ALU.max)
            free_banks.append(bank)

        def store(u, j):
            nc.sync.dma_start(out=out_view[:, J * u + j, :], in_=rows(u, j))

        def clip_rows(engine, u, j):
            engine.tensor_scalar(out=rows(u, j), in0=rows(u, j), scalar1=CLAMP, scalar2=-CLAMP, op0=ALU.min, op1=ALU.max)

        def clip_before(u, j):
            first = ((u + 1) % 2 * J + j) * O
            tiles = at(z, (u + 1) // 2)[:, first : first + O]
            nc.gpsimd.tensor_scalar(out=tiles, in0=tiles, scalar1=CLAMP, scalar2=-CLAMP / SLOPE, op0=ALU.min, op1=ALU.max)

        def close_groups(u, count):
            first = u % 2 * J
            tiles = at(finished, u // 2)[:].rearrange("p (t o) -> p t o", o=O)[:, first : first + J * count]
            plain = tiles.rearrange("p (g j) o -> p g (j o)", j=J)[:, :, 2 * P if summed(u) else 0 :]
            nc.gpsimd.tensor_scalar(out=plain, in0=plain, scalar1=CLAMP, scalar2=-CLAMP, op0=ALU.min, op1=ALU.max)
            if u in WIDE:
                nc.sync.dma_start(out=wide_view[:, u : u + count, :], in_=tiles.rearrange("p (g j) o -> p g (j o)", j=J))
            else:
                nc.sync.dma_start(out=out_view[:, J * u : J * (u + count), :], in_=tiles)

        by_block = [(e, n) for e in range(2) for n in range(GROUP_SAMPLES)]
        by_tile = [(e, n) for n in range(GROUP_SAMPLES) for e in range(2)]

        def copies_in(i):
            ahead = (i + 3) // 2 + 1
            return i % 2 == 1 and ahead in raw_pairs and ahead not in early_pairs

        def on_vector(u):
            count = RAMP.get(u, ON_VECTOR[1] if copies_in(u) else 0 if u % 2 or copies_in(u + 1) else ON_VECTOR[0])
            return by_tile[:count]

        def on_scalar(u):
            return [(2 * u, part) for part in by_block] + [(2 * u + 1, part) for part in by_tile if part not in on_vector(u)]

        nc.vector.tensor_copy(out=w_bf[:], in_=w_codes[:].bitcast(FP8))
        w_bank = z_banks[3]
        w_words = w_bf[:].bitcast(F32)
        warm_up(x_banks[1], BANK)
        turn_rows(z_banks[0], weight_sb[0])
        for u in range(2):
            nc.tensor.transpose(w_bank[:, u * P : (u + 1) * P], w_words[:, u::2], ident[:])
        turn_rows(y_banks[0], style_w_sb[0])
        turn_rows(y_banks[1], style_w_sb[1])
        warm_up(x_banks[1], HOLD)
        nc.vector.tensor_tensor(
            out=w_t[:].rearrange("p n (u e) -> p n u e", e=2),
            in0=w_bank[:, : 2 * P].bitcast(BF16).rearrange("p (u n e) -> p n u e", u=2, e=2),
            in1=w_scale_sb[:].rearrange("p (u e) -> p u e", e=2).unsqueeze(1).to_broadcast([P, SAMPLES, 2, 2]),
            op=ALU.mult)
        copy_words(nc.scalar.copy, weight_t[0][:], z_banks[0])
        nc.vector.tensor_scalar(out=bias_rows[:PACK, :], in0=bias_sb[:], scalar1=GAIN, scalar2=None, op0=ALU.mult)
        nc.vector.quantize_mx(out=w_q[:].bitcast(X4), scales=w_s[:], in_=w_t[:].rearrange("p n k -> p (n k)"))
        for h in range(2):
            copy_words(nc.scalar.copy, style_w_t[h][:], y_banks[h])
        nc.tensor.transpose(w_bank[:, :P], bias_rows[:], ident[:])
        turn_rows(z_banks[1], weight_sb[1])
        nc.vector.tensor_tensor(out=weight2_t[0][:], in0=weight_t[0][:], in1=weight_t[0][:], op=ALU.mult)
        quantise_half(style_w_q, style_w_s, 0, style_w_t[0])
        quantise_half(weight_q, weight_s, 0, weight_t[0])
        quantise_half(style_w_q, style_w_s, 1, style_w_t[1])
        turn_x(0)
        for t in range(PACK):
            cols = slice(t * P, (t + 1) * P)
            nc.tensor.matmul_mx(out=style_bank[:, cols], lhsT=style_w_q[:, cols].bitcast(X4), lhsT_scale=style_w_s[:, cols],
                                rhs=w_q[:].bitcast(X4), rhs_scale=w_s[:], start=True, stop=True)
        turn_x(1)
        warm_up(y_banks[0], HOLD)
        for t in range(2, 2 * J):
            turn_x(t)
        copy_words(nc.scalar.copy, weight_t[1][:], z_banks[1])
        nc.scalar.activation(out=weight2_t[1][:], in_=weight_t[1][:], func=ACT.Square)
        nc.vector.tensor_copy(out=bias_gain[:], in_=w_bank[:, :PACK])
        turn_early(0)
        quantise_half(weight2_q, weight2_s, 0, weight2_t[0])
        quantise_half(weight_q, weight_s, 1, weight_t[1])
        make_style(0)
        square_style(0)
        modulate(0, 0, 2)
        quantise_style2(0)
        quantise(0, slice(0, P))
        turn_early(1, [0])
        warm_up(y_banks[0], HOLD)
        d_product(0, y_banks[0], range(0, 2))
        product(0, slice(0, P), y_banks[1])
        turn_early(1, [1])
        copy_early(0)
        take_root(0, y_banks[0], range(0, 2))
        demodulate(nc.scalar, 0, by_tile[:PACK], y_banks[1])
        copy_early(1)
        modulate(0, 2, 2)
        turn_x(4)
        turn_x(5)
        quantise_half(weight2_q, weight2_s, 1, weight2_t[1])
        quantise(0, slice(P, TOKENS))
        product(0, slice(P, TOKENS))
        d_product(0, z_banks[3], range(2, PACK))
        product(1)
        demodulate(nc.scalar, 0, by_tile[PACK:])
        take_root(0, z_banks[3], range(2, PACK))
        modulate(1, 0, 2)
        modulate(1, 2, 2)
        quantise(0, slice(TOKENS, 3 * P))
        make_style(1)
        quantise_raw(0)
        if 1 in raw_pairs:
            modulate_raw(1)
        modulate(2)

        def turned_in(i):
            return [i - 2] if i >= 2 else []

        for i in range(LAST - 1):
            p = (i + 3) // 2
            even = i % 2 == 0
            if i <= LAST:
                demodulate(nc.vector, 2 * i + 1, on_vector(i))
            tiles = [(u, j) for u in turned_in(i - 1) for j in (reversed(range(J)) if i == 3 else range(J))]
            held = tiles[-1:] if even and p < PAIRS - 1 else []
            for u, j in tiles[: len(tiles) - len(held)]:
                finish(u, j)
                if i == PLAIN_FROM and j == 0:
                    quantise_raw(PAIRS - 1)
                    quantise(PAIRS - 1)

            if i == SINGLY_FROM + 3:
                close_groups(i - 3, 1)

            if p < PAIRS:
                for t in range(4 * p + 2, 4 * p + own_tiles(p)) if even else range(4 * p, 4 * p + 2):
                    turn_x(t)
                if even and p + 2 in raw_pairs and p + 2 not in early_pairs:
                    turn_tile(x_banks[1], 1, x_rows(4 * (p + 2) + 3))
            if i == 1:
                turn_early(2)
            for u in turned_in(i):
                for j in range(J):
                    turn_back(u, j)

            parts = [] if i > LAST else on_scalar(i)[2 * PACK :] if i == 0 else on_scalar(i)
            split = 2 * PACK if even else PACK
            for q, part in parts[:split]:
                demodulate(nc.scalar, q, [part])
            if even and i and summed(i):
                take_negative(i // 2)
            if p < PAIRS and not even:
                modulate(2 * p)
            if p < PAIRS and even:
                modulate(2 * p + 1, 0, 2)
                if p not in raw_pairs:
                    modulate(2 * p + 1, 2, 2)
                for u, j in held:
                    finish(u, j)
                if i == 0:
                    square_style(1)
                if p < PAIRS - 1:
                    quantise_raw(p)
                    if i == 0:
                        quantise_style2(1)
                    quantise(p)
            if even and 0 <= i - 4 < SINGLY_FROM:
                close_groups(i - 4, 2)
            if i == SINGLY_FROM + 4:
                close_groups(i - 3, 1)
            if even and p + 1 in raw_pairs:
                modulate_raw(p + 1)
            if i == 0 and summed(0):
                take_negative(0, 1)

            if copies_in(i):
                copy_raw(p + 1, x_banks[1], 1)
            for q, part in parts[split:]:
                demodulate(nc.scalar, q, [part])
            if i == 1:
                copy_early(2)
            if i == 2:
                take_root(1, z_banks[3], range(PACK))

            for u in turned_in(i):
                for j in range(J if summed(u) else 0):
                    add_steep(u, j)
            if i == PLAIN_FROM:
                free_banks[:0] = x_banks
                for step in (turn_back, add_steep):
                    for j in range(J):
                        step(i - 1, j)
            if i < LAST:
                product(2 * i + 2)
                product(2 * i + 3)
            if i == 1:
                d_product(1, z_banks[3], range(PACK))
            for u in turned_in(i):
                for j in reversed(range(J)):
                    take_relu(u, j)

        def each_tile(step, g):
            for j in range(J):
                step(g, j)

        def plain_first(step, g):
            for j in reversed(range(J)):
                step(g, j)

        def open_bank(u, j):
            for k in range(PACK):
                nc.tensor.matmul(out=z_bank(u, j)[:, k * P : (k + 1) * P], lhsT=z_block(u, j, k), rhs=ident[:],
                                 is_transpose=True, start=k == 0, stop=False)

        def add_term(u, j, by_turns):
            for k in range(PACK):
                cols = slice(k * P, (k + 1) * P)
                nc.tensor.matmul(out=z_bank(u, j)[:, cols], lhsT=relu_tile(u, j)[:, cols], rhs=ident[:] if by_turns else steep_ident[:],
                                 is_transpose=by_turns, start=False, stop=k == PACK - 1)

        def z_tile(u, j):
            first = ((u + 1) % 2 * J + j) * O
            return at(z, (u + 1) // 2)[:, first : first + O]

        def negative_tile(u, j):
            nc.gpsimd.tensor_scalar(out=relu_tile(u, j)[:], in0=z_tile(u, j), scalar1=0.0, scalar2=-CLAMP / SLOPE, op0=ALU.min, op1=ALU.max)

        def steep_tile(u, j):
            nc.vector.tensor_scalar(out=relu_tile(u, j)[:], in0=z_tile(u, j), scalar1=-(1.0 - SLOPE), scalar2=0.0, op0=ALU.mult, op1=ALU.max)

        def empty(u, j):
            nc.vector.tensor_scalar(out=rows(u, j), in0=z_bank(u, j)[:], scalar1=CLAMP, scalar2=-CLAMP, op0=ALU.min, op1=ALU.max)
            free_banks.append(z_bank(u, j))
            store(u, j)

        u = LAST - 1
        spare = [free_banks.pop(0) for h in range(2)]
        for h in range(2):
            product(2 * LAST + h, bank=spare[h])
        plain_first(take_relu, u - 2)
        negative_tile(u - 1, 0)
        close_groups(u - 4, 1)
        plain_first(finish, u - 3)
        close_groups(u - 3, 1)
        turn_back(u - 1, 1)
        open_bank(u - 1, 0)
        add_term(u - 1, 0, False)
        plain_first(finish, u - 2)
        close_groups(u - 2, 1)
        demodulate(nc.scalar, 2 * u, by_tile)
        demodulate(nc.vector, 2 * LAST + 1, by_tile[:TAIL_LAST], spare[1])
        take_relu(u - 1, 1)
        demodulate(nc.scalar, 2 * u + 1, by_tile)
        each_tile(turn_back, u)
        finish(u - 1, 1)
        clip_rows(nc.gpsimd, u - 1, 1)
        empty(u - 1, 0)
        store(u - 1, 1)
        demodulate(nc.scalar, 2 * LAST, by_tile, spare[0])
        demodulate(nc.scalar, 2 * LAST + 1, by_tile[TAIL_LAST:], spare[1])
        steep_tile(LAST, 0)
        each_tile(take_relu, u)
        open_bank(LAST, 0)
        add_term(LAST, 0, True)
        steep_tile(LAST, 1)
        open_bank(LAST, 1)
        add_term(LAST, 1, True)
        finish(u, 0)
        clip_rows(nc.gpsimd, u, 0)
        empty(LAST, 0)
        store(u, 0)
        finish(u, 1)
        clip_rows(nc.gpsimd, u, 1)
        empty(LAST, 1)
        store(u, 1)
